import numpy as np
import ml_dtypes


def mxq(x, axis, fmt="e4m3"):
    dtype, down = {"e4m3": (ml_dtypes.float8_e4m3fn, 7), "e5m2": (ml_dtypes.float8_e5m2, 14)}[fmt]
    v = np.moveaxis(np.asarray(x, np.float32).astype(ml_dtypes.bfloat16).astype(np.float64), axis, -1)
    blocks = v.reshape(v.shape[:-1] + (-1, 32))
    amax = np.abs(blocks).max(-1, keepdims=True)
    byte = np.maximum(np.where(amax > 0, np.frexp(amax)[1] - 1 + 127, 0) - down, 1)
    scale = np.exp2(byte - 127.0)
    codes = (blocks / scale).astype(np.float32).astype(dtype).astype(np.float64)
    return np.moveaxis((codes * scale).reshape(v.shape), -1, axis)


WIDE = False


def mx_kscale(k):
    if not WIDE:
        return np.ones(k)
    levels = np.array([10, -10, 5, -5, 0])
    a = np.random.permutation(np.resize(levels, k // 512 * 4)).reshape(k // 512, 4)
    idx = np.arange(k)
    return np.exp2(a[idx // 512, idx % 128 // 32])


BF16 = ml_dtypes.bfloat16


def bf(x):
    return np.asarray(x, np.float32).astype(BF16)


def f64(x):
    return np.asarray(x).astype(np.float64)


B, IN, OUT, G, P = 512, 1024, 1024, 5, 3
NB = G + P
LO, HI = -1.0, 1.0


def silu(v):
    return v / (1.0 + np.exp(-v))


def b_splines(x, grid):
    xe = x[..., None]
    bases = np.logical_and(xe >= grid[:, :-1], xe < grid[:, 1:]).astype(np.float64)
    for k in range(1, P + 1):
        left = (xe - grid[:, :-(k + 1)]) / (grid[:, k:-1] - grid[:, :-(k + 1)])
        right = (grid[:, k + 1:] - xe) / (grid[:, k + 1:] - grid[:, 1:-k])
        bases = left * bases[..., :-1] + right * bases[..., 1:]
    return bases


def setup_inputs():
    s = mx_kscale(IN)
    s = s / s.max()
    h = (HI - LO) / G
    g = np.arange(-P, G + P + 1) * h + LO
    return {"x": bf(np.random.uniform(LO, HI, (B, IN)) * s),
            "base_weight": bf(np.random.standard_normal((OUT, IN)) * 2.5 / np.sqrt(IN) / s[None, :]),
            "spline_weight": bf(np.random.standard_normal((OUT, IN, NB))),
            "spline_scaler": bf(np.random.standard_normal((OUT, IN)) * 1.5 / np.sqrt(IN)),
            "grid": bf(np.tile(g[None, :], (IN, 1)))}


def reference(x, base_weight, spline_weight, spline_scaler, grid):
    x, grid = f64(x), f64(grid)
    base_out = mxq(silu(x), 1, "e4m3") @ mxq(f64(base_weight), 1, "e4m3").T
    ssw = f64(spline_weight) * f64(spline_scaler)[..., None]
    bs = b_splines(x, grid).reshape(x.shape[0], -1)
    spline_out = mxq(bs, 1, "e4m3") @ mxq(ssw.reshape(OUT, -1), 1, "e4m3").T
    return base_out + spline_out

@@ -1,0 +1,264 @@
+from contextlib import ExitStack
+
+import concourse.mybir as mybir
+from concourse.masks import make_identity
+
+F32 = mybir.dt.float32
+BF16 = mybir.dt.bfloat16
+U32 = mybir.dt.uint32
+U8 = mybir.dt.uint8
+FP8X4 = mybir.dt.float8_e4m3fn_x4
+ALU = mybir.AluOpType
+AF = mybir.ActivationFunctionType
+
+P = 128
+B = 512
+IN = 1024
+OUT = 1024
+NB = 8
+NK = 12
+NIT = IN // P
+NBT = B // P
+OH = 512
+FLOPS = 2 * B * OUT * (IN + IN * NB)
+
+
+def tile_bsplinekanlayer_kernel(tc, x, base_weight, spline_weight, spline_scaler, grid, out):
+    nc = tc.nc
+    with ExitStack() as ctx:
+        const = ctx.enter_context(tc.tile_pool(name="const", bufs=1))
+        keep = ctx.enter_context(tc.tile_pool(name="keep", bufs=1))
+        stage = ctx.enter_context(tc.tile_pool(name="stage", bufs=8))
+        rawp = ctx.enter_context(tc.tile_pool(name="rawp", bufs=2))
+        grp = ctx.enter_context(tc.tile_pool(name="grp", bufs=3))
+        wcp = ctx.enter_context(tc.tile_pool(name="wcp", bufs=3))
+        cubep = ctx.enter_context(tc.tile_pool(name="cubep", bufs=2))
+        planep = ctx.enter_context(tc.tile_pool(name="planep", bufs=1))
+        bgp = ctx.enter_context(tc.tile_pool(name="bgp", bufs=2))
+        outp = ctx.enter_context(tc.tile_pool(name="outp", bufs=2))
+        accp = ctx.enter_context(tc.psum_pool(name="accp", bufs=1))
+        trp = ctx.enter_context(tc.psum_pool(name="trp", bufs=4))
+
+        grid_sb = const.tile([P, NIT, NK], BF16)
+        nc.sync.dma_start(out=grid_sb[:], in_=grid.rearrange("(t p) r -> p t r", p=P))
+        x_sb = []
+        for bt in range(NBT):
+            xt = stage.tile([P, IN], BF16, name="x%d" % bt, tag="in2k")
+            nc.sync.dma_start(out=xt[:], in_=x[bt * P:(bt + 1) * P, :])
+            x_sb.append(xt)
+
+        ident_bf = const.tile([P, P], BF16)
+        make_identity(nc, ident_bf[:])
+        ident_f = const.tile([P, P], F32)
+        make_identity(nc, ident_f[:])
+        dup = const.tile([P, P, 2], BF16)
+        nc.vector.tensor_copy(out=dup[:], in_=ident_bf[:].unsqueeze(2).to_broadcast([P, P, 2]))
+
+        knot = const.tile([P, NIT, NK], F32)
+        nc.vector.tensor_copy(out=knot[:], in_=grid_sb[:])
+        neg_knot = const.tile([P, NIT, NK], F32)
+        nc.vector.tensor_scalar_mul(out=neg_knot[:], in0=knot[:], scalar1=-1.0)
+        dif = {}
+        for d in range(1, 5):
+            dd = const.tile([P, NIT, NK], F32, name="dif%d" % d)
+            nc.vector.tensor_tensor(out=dd[:, :, 0:NK - d], in0=knot[:, :, d:NK], in1=knot[:, :, 0:NK - d], op=ALU.subtract)
+            dif[d] = dd
+        mag = {}
+        for q in range(5):
+            factors = [dif[a][:, :, q - a:q - a + NB] for a in range(1, q + 1)]
+            factors.extend([dif[a][:, :, q:q + NB] for a in range(1, 5 - q)])
+            den = const.tile([P, NIT, NB], F32, name="mag%d" % q)
+            nc.vector.tensor_tensor(out=den[:], in0=factors[0], in1=factors[1], op=ALU.mult)
+            nc.vector.tensor_tensor(out=den[:], in0=den[:], in1=factors[2], op=ALU.mult)
+            nc.vector.tensor_tensor(out=den[:], in0=den[:], in1=factors[3], op=ALU.mult)
+            nc.vector.reciprocal(out=den[:], in_=den[:])
+            nc.vector.tensor_tensor(out=den[:], in0=den[:], in1=dif[4][:, :, 0:NB], op=ALU.mult)
+            mag[q] = den
+        neg_mag4 = const.tile([P, NIT, NB], F32)
+        nc.vector.tensor_scalar_mul(out=neg_mag4[:], in0=mag[4][:], scalar1=-1.0)
+        inv4 = const.tile([P, NIT, NB], F32)
+        nc.vector.reciprocal(out=inv4[:], in_=neg_mag4[:])
+        inv0 = const.tile([P, NIT, NB], F32)
+        nc.vector.reciprocal(out=inv0[:], in_=mag[0][:])
+        beta_q = const.tile([P, NIT, NB], F32)
+        nc.vector.tensor_tensor(out=beta_q[:, :, 1:8], in0=mag[3][:, :, 1:8], in1=inv4[:, :, 0:7], op=ALU.mult)
+        alpha_q = const.tile([P, NIT, NB], F32)
+        nc.vector.reciprocal(out=alpha_q[:, :, 2:8], in_=beta_q[:, :, 2:8])
+        nc.vector.tensor_tensor(out=alpha_q[:, :, 2:8], in0=alpha_q[:, :, 2:8], in1=mag[2][:, :, 2:8], op=ALU.mult)
+        nc.vector.tensor_tensor(out=alpha_q[:, :, 2:8], in0=alpha_q[:, :, 2:8], in1=inv4[:, :, 0:6], op=ALU.mult)
+        nc.vector.tensor_scalar_mul(out=alpha_q[:, :, 2:8], in0=alpha_q[:, :, 2:8], scalar1=-1.0)
+        beta_p = const.tile([P, NIT, NB], F32)
+        nc.vector.tensor_tensor(out=beta_p[:, :, 0:7], in0=mag[1][:, :, 0:7], in1=inv0[:, :, 1:8], op=ALU.mult)
+        nc.vector.tensor_scalar_mul(out=beta_p[:, :, 0:7], in0=beta_p[:, :, 0:7], scalar1=-1.0)
+        alpha_p = const.tile([P, NIT, NB], F32)
+        nc.vector.reciprocal(out=alpha_p[:, :, 0:6], in_=beta_p[:, :, 0:6])
+        nc.vector.tensor_tensor(out=alpha_p[:, :, 0:6], in0=alpha_p[:, :, 0:6], in1=mag[2][:, :, 0:6], op=ALU.mult)
+        nc.vector.tensor_tensor(out=alpha_p[:, :, 0:6], in0=alpha_p[:, :, 0:6], in1=inv0[:, :, 2:8], op=ALU.mult)
+
+        xT = keep.tile([P, NIT, B], BF16)
+        for pair in range(NIT // 2):
+            ps = trp.tile([P, 2, B], BF16, name="ps_x", tag="tr")
+            for s in range(2):
+                it = 2 * pair + s
+                for bt in range(NBT):
+                    nc.tensor.transpose(ps[:, s, bt * P:(bt + 1) * P], x_sb[bt][:, it * P:(it + 1) * P], ident_bf[:])
+            nc.scalar.copy(out=xT[:, 2 * pair:2 * pair + 2, :], in_=ps[:])
+
+        a_codes = keep.tile([P, 2, B], U32, align_bytes=64)
+        a_scales = keep.tile([P, 2, B], U8, align_bytes=64)
+        for g in range(2):
+            sg = grp.tile([P, B, 4], BF16, name="sg", tag="grp", align_bytes=64)
+            nc.scalar.activation(out=sg[:], in_=xT[:, 4 * g:4 * g + 4, :].rearrange("p t b -> p b t"), func=AF.Silu)
+            nc.vector.quantize_mx(out=a_codes[:, g, :].bitcast(FP8X4), scales=a_scales[:, g, :], in_=sg[:].rearrange("p b t -> p (b t)"))
+
+        scT2 = keep.tile([P, NIT, 2 * OUT], BF16)
+        bw_codes = keep.tile([P, 2, 2, OH], U32, align_bytes=64)
+        bw_scales = keep.tile([P, 2, 2, OH], U8, align_bytes=64)
+        bs_codes = keep.tile([P, NIT, 2, B], U32, align_bytes=64)
+        bs_scales = keep.tile([P, NIT, 2, B], U8, align_bytes=64)
+
+        def half_prologue(h):
+            sc_sb = []
+            for oo in range(4):
+                st = stage.tile([P, IN], BF16, name="sc%d" % oo, tag="in2k")
+                nc.sync.dma_start(out=st[:], in_=spline_scaler[(4 * h + oo) * P:(4 * h + oo + 1) * P, :])
+                sc_sb.append(st)
+            for it in range(NIT):
+                ps = trp.tile([P, 4, 2 * P], BF16, name="ps_sc", tag="tr")
+                for oo in range(4):
+                    nc.tensor.matmul(out=ps[:, oo, :], lhsT=sc_sb[oo][:, it * P:(it + 1) * P], rhs=dup[:].rearrange("p o e -> p (o e)"), start=True, stop=True)
+                nc.scalar.copy(out=scT2[:, it, h * 2 * OH:(h + 1) * 2 * OH], in_=ps[:].rearrange("p a b -> p (a b)"))
+            bw_sb = []
+            for oo in range(4):
+                bt_ = stage.tile([P, IN], BF16, name="bw%d" % oo, tag="in2k")
+                nc.sync.dma_start(out=bt_[:], in_=base_weight[(4 * h + oo) * P:(4 * h + oo + 1) * P, :])
+                bw_sb.append(bt_)
+            for g in range(2):
+                bwg = grp.tile([P, OH, 4], BF16, name="bwg", tag="grp", align_bytes=64)
+                for half in range(2):
+                    ps = trp.tile([P, 4, 2 * P], BF16, name="ps_bw", tag="tr")
+                    for t in range(4):
+                        for o2 in range(2):
+                            nc.tensor.transpose(ps[:, t, o2 * P:(o2 + 1) * P], bw_sb[2 * half + o2][:, (4 * g + t) * P:(4 * g + t + 1) * P], ident_bf[:])
+                    nc.scalar.copy(out=bwg[:, half * 256:(half + 1) * 256, :], in_=ps[:].rearrange("p t o -> p o t"))
+                nc.vector.quantize_mx(out=bw_codes[:, g, h, :].bitcast(FP8X4), scales=bw_scales[:, g, h, :], in_=bwg[:].rearrange("p o t -> p (o t)"))
+
+        def fma(o, a, s, b_):
+            nc.vector.scalar_tensor_tensor(out=o, in0=a, scalar=s, in1=b_, op0=ALU.mult, op1=ALU.add)
+
+        def basis(it):
+            v = xT[:, it, :]
+            cube = {}
+            for r in range(3, 9):
+                c = cubep.tile([P, B], F32, name="cube%d" % r)
+                nc.scalar.activation(out=c[:], in_=v, func=AF.Square, bias=neg_knot[:, it, r:r + 1], scale=1.0)
+                nc.vector.scalar_tensor_tensor(out=c[:], in0=v, scalar=knot[:, it, r:r + 1], in1=c[:], op0=ALU.subtract, op1=ALU.mult)
+                cube[r] = c
+            f = planep.tile([P, NB, B], F32, name="planes")
+            hi = {4: f[:, 0, :]}
+            for r in range(5, 8):
+                hq = cubep.tile([P, B], F32, name="hi%d" % r)
+                hi[r] = hq[:]
+            for r in range(4, 8):
+                nc.scalar.activation(out=hi[r], in_=cube[r][:], func=AF.Relu, scale=neg_mag4[:, it, r - 4:r - 3])
+            lo = {}
+            for r in range(3, 7):
+                nc.scalar.activation(out=cube[r][:], in_=cube[r][:], func=AF.Relu, scale=mag[0][:, it, r:r + 1])
+                lo[r] = cube[r][:]
+            nc.scalar.activation(out=f[:, 7, :], in_=cube[7][:], func=AF.Relu, scale=mag[0][:, it, 7:8])
+            lo[7] = f[:, 7, :]
+            nc.scalar.activation(out=cube[8][:], in_=cube[8][:], func=AF.Relu, scale=neg_mag4[:, it, 4:5])
+            hi[8] = cube[8][:]
+
+            fma(f[:, 1, :], hi[4], beta_q[:, it, 1:2], hi[5])
+            fma(f[:, 2, :], hi[4], alpha_q[:, it, 2:3], hi[5])
+            fma(f[:, 2, :], f[:, 2, :], beta_q[:, it, 2:3], hi[6])
+            fma(f[:, 3, :], hi[5], alpha_q[:, it, 3:4], hi[6])
+            fma(f[:, 3, :], f[:, 3, :], beta_q[:, it, 3:4], hi[7])
+            nc.vector.tensor_tensor(out=f[:, 3, :], in0=f[:, 3, :], in1=lo[3], op=ALU.min)
+            fma(f[:, 4, :], lo[6], alpha_p[:, it, 4:5], lo[5])
+            fma(f[:, 4, :], f[:, 4, :], beta_p[:, it, 4:5], lo[4])
+            nc.vector.tensor_tensor(out=f[:, 4, :], in0=f[:, 4, :], in1=hi[8], op=ALU.min)
+            fma(f[:, 5, :], lo[7], alpha_p[:, it, 5:6], lo[6])
+            fma(f[:, 5, :], f[:, 5, :], beta_p[:, it, 5:6], lo[5])
+            fma(f[:, 6, :], lo[7], beta_p[:, it, 6:7], lo[6])
+
+            for jh in range(2):
+                bg = bgp.tile([P, B, 4], BF16, name="bg", align_bytes=64)
+                src = f[:, 4 * jh:4 * jh + 4, :].rearrange("p t b -> p b t")
+                if jh == 0:
+                    nc.scalar.copy(out=bg[:], in_=src)
+                else:
+                    nc.vector.tensor_copy(out=bg[:], in_=src)
+                nc.vector.quantize_mx(out=bs_codes[:, it, jh, :].bitcast(FP8X4), scales=bs_scales[:, it, jh, :], in_=bg[:].rearrange("p b t -> p (b t)"))
+
+        sw_view = spline_weight.rearrange("(t p) i j -> p t (i j)", p=P)
+
+        def weights(it, h, acc):
+            raw = rawp.tile([P, 4, P * NB], BF16, name="raw")
+            nc.sync.dma_start(out=raw[:], in_=sw_view[:, 4 * h:4 * h + 4, it * P * NB:(it + 1) * P * NB])
+            words = raw[:].bitcast(F32).rearrange("p t (i m) -> p t m i", m=4)
+            for jh in range(2):
+                wg = grp.tile([P, OH, 4], BF16, name="wg", tag="grp", align_bytes=64)
+                for half in range(2):
+                    ps = trp.tile([P, 2, 2 * P], F32, name="ps_w", tag="tr")
+                    for m0 in range(2):
+                        for o2 in range(2):
+                            nc.tensor.transpose(ps[:, m0, o2 * P:(o2 + 1) * P], words[:, 2 * half + o2, 2 * jh + m0, :], ident_f[:])
+                    lo_col = h * 2 * OH + half * OH
+                    nc.vector.tensor_tensor(
+                        out=wg[:, half * 256:(half + 1) * 256, :].rearrange("p o (m e) -> p o m e", e=2),
+                        in0=ps[:].bitcast(BF16).rearrange("p m (o e) -> p o m e", e=2),
+                        in1=scT2[:, it, lo_col:lo_col + OH].rearrange("p (o e) -> p o e", e=2).unsqueeze(2).to_broadcast([P, 256, 2, 2]),
+                        op=ALU.mult,
+                    )
+                wc = wcp.tile([P, OH], U32, name="wc", align_bytes=64)
+                ws = wcp.tile([P, OH], U8, name="ws", align_bytes=64)
+                nc.vector.quantize_mx(out=wc[:].bitcast(FP8X4), scales=ws[:], in_=wg[:].rearrange("p o t -> p (o t)"))
+                for bt in range(NBT):
+                    nc.tensor.matmul_mx(
+                        out=acc[bt][:],
+                        lhsT=bs_codes[:, it, jh, bt * P:(bt + 1) * P].bitcast(FP8X4),
+                        lhsT_scale=bs_scales[:, it, jh, bt * P:(bt + 1) * P],
+                        rhs=wc[:].bitcast(FP8X4),
+                        rhs_scale=ws[:],
+                        start=False,
+                        stop=(it == NIT - 1 and jh == 1),
+                    )
+
+        def open_round(h):
+            acc = []
+            for bt in range(NBT):
+                a = accp.tile([P, OH], F32, name="acc%d" % bt)
+                acc.append(a)
+            for g in range(2):
+                for bt in range(NBT):
+                    nc.tensor.matmul_mx(
+                        out=acc[bt][:],
+                        lhsT=a_codes[:, g, bt * P:(bt + 1) * P].bitcast(FP8X4),
+                        lhsT_scale=a_scales[:, g, bt * P:(bt + 1) * P],
+                        rhs=bw_codes[:, g, h, :].bitcast(FP8X4),
+                        rhs_scale=bw_scales[:, g, h, :],
+                        start=(g == 0),
+                        stop=False,
+                    )
+            return acc
+
+        def close_round(h, acc):
+            for bt in range(NBT):
+                o_sb = outp.tile([P, OH], F32, name="o_sb")
+                nc.scalar.copy(out=o_sb[:], in_=acc[bt][:])
+                nc.sync.dma_start(out=out[bt * P:(bt + 1) * P, h * OH:(h + 1) * OH], in_=o_sb[:])
+
+        half_prologue(0)
+        acc0 = open_round(0)
+        for it in range(NIT):
+            basis(it)
+            weights(it, 0, acc0)
+            if it == 3:
+                half_prologue(1)
+        close_round(0, acc0)
+        acc1 = open_round(1)
+        for it in range(NIT):
+            weights(it, 1, acc1)
+        close_round(1, acc1)

@@ -21,23 +21,31 @@ NIT = IN // P
 NBT = B // P
 OH = 512
 FLOPS = 2 * B * OUT * (IN + IN * NB)
+CUBE_ORDER = (4, 5, 6, 7, 3, 8)
+CLIP_HI = {4: "act", 5: "act", 6: "act", 7: "act"}
+CLIP_LO = {4: "act", 5: "act", 6: "act", 7: "act"}
+REGROUP_ON_VECTOR = ()
 
 
 def tile_bsplinekanlayer_kernel(tc, x, base_weight, spline_weight, spline_scaler, grid, out):
     nc = tc.nc
     with ExitStack() as ctx:
+        ctx.enter_context(tc.manual_schedule())
         const = ctx.enter_context(tc.tile_pool(name="const", bufs=1))
         keep = ctx.enter_context(tc.tile_pool(name="keep", bufs=1))
         stage = ctx.enter_context(tc.tile_pool(name="stage", bufs=8))
         rawp = ctx.enter_context(tc.tile_pool(name="rawp", bufs=2))
+        sctp = ctx.enter_context(tc.tile_pool(name="sctp", bufs=1))
+        scbp = ctx.enter_context(tc.tile_pool(name="scbp", bufs=3))
         grp = ctx.enter_context(tc.tile_pool(name="grp", bufs=3))
         wcp = ctx.enter_context(tc.tile_pool(name="wcp", bufs=3))
         cubep = ctx.enter_context(tc.tile_pool(name="cubep", bufs=2))
-        planep = ctx.enter_context(tc.tile_pool(name="planep", bufs=1))
+        planep = ctx.enter_context(tc.tile_pool(name="planep", bufs=2))
         bgp = ctx.enter_context(tc.tile_pool(name="bgp", bufs=2))
         outp = ctx.enter_context(tc.tile_pool(name="outp", bufs=2))
         accp = ctx.enter_context(tc.psum_pool(name="accp", bufs=1))
-        trp = ctx.enter_context(tc.psum_pool(name="trp", bufs=4))
+        trw = ctx.enter_context(tc.psum_pool(name="trw", bufs=3))
+        trp = ctx.enter_context(tc.psum_pool(name="trp", bufs=1))
 
         grid_sb = const.tile([P, NIT, NK], BF16)
         nc.sync.dma_start(out=grid_sb[:], in_=grid.rearrange("(t p) r -> p t r", p=P))
@@ -47,6 +55,9 @@ def tile_bsplinekanlayer_kernel(tc, x, base_weight, spline_weight, spline_scaler
             nc.sync.dma_start(out=xt[:], in_=x[bt * P:(bt + 1) * P, :])
             x_sb.append(xt)
 
+        warm = const.tile([P, 2], F32)
+        nc.vector.memset(warm[:, 0:1], 0.0)
+        nc.scalar.activation(out=warm[:, 1:2], in_=warm[:, 0:1], func=AF.Silu)
         ident_bf = const.tile([P, P], BF16)
         make_identity(nc, ident_bf[:])
         ident_f = const.tile([P, P], F32)
@@ -64,39 +75,51 @@ def tile_bsplinekanlayer_kernel(tc, x, base_weight, spline_weight, spline_scaler
             nc.vector.tensor_tensor(out=dd[:, :, 0:NK - d], in0=knot[:, :, d:NK], in1=knot[:, :, 0:NK - d], op=ALU.subtract)
             dif[d] = dd
         mag = {}
+        need = {0: (3, 8), 1: (4, 7), 2: (2, 6), 3: (1, 4), 4: (0, 5)}
         for q in range(5):
-            factors = [dif[a][:, :, q - a:q - a + NB] for a in range(1, q + 1)]
-            factors.extend([dif[a][:, :, q:q + NB] for a in range(1, 5 - q)])
+            j0, j1 = need[q]
+            factors = [dif[a][:, :, q - a + j0:q - a + j1] for a in range(1, q + 1)]
+            factors.extend([dif[a][:, :, q + j0:q + j1] for a in range(1, 5 - q)])
             den = const.tile([P, NIT, NB], F32, name="mag%d" % q)
-            nc.vector.tensor_tensor(out=den[:], in0=factors[0], in1=factors[1], op=ALU.mult)
-            nc.vector.tensor_tensor(out=den[:], in0=den[:], in1=factors[2], op=ALU.mult)
-            nc.vector.tensor_tensor(out=den[:], in0=den[:], in1=factors[3], op=ALU.mult)
-            nc.vector.reciprocal(out=den[:], in_=den[:])
-            nc.vector.tensor_tensor(out=den[:], in0=den[:], in1=dif[4][:, :, 0:NB], op=ALU.mult)
+            dv = den[:, :, j0:j1]
+            nc.vector.tensor_tensor(out=dv, in0=factors[0], in1=factors[1], op=ALU.mult)
+            nc.vector.tensor_tensor(out=dv, in0=dv, in1=factors[2], op=ALU.mult)
+            nc.vector.tensor_tensor(out=dv, in0=dv, in1=factors[3], op=ALU.mult)
+            nc.vector.reciprocal(out=dv, in_=dv)
+            nc.vector.tensor_tensor(out=dv, in0=dv, in1=dif[4][:, :, j0:j1], op=ALU.mult)
             mag[q] = den
         neg_mag4 = const.tile([P, NIT, NB], F32)
-        nc.vector.tensor_scalar_mul(out=neg_mag4[:], in0=mag[4][:], scalar1=-1.0)
+        nc.vector.tensor_scalar_mul(out=neg_mag4[:, :, 0:5], in0=mag[4][:, :, 0:5], scalar1=-1.0)
         inv4 = const.tile([P, NIT, NB], F32)
-        nc.vector.reciprocal(out=inv4[:], in_=neg_mag4[:])
+        nc.vector.reciprocal(out=inv4[:, :, 0:3], in_=neg_mag4[:, :, 0:3])
         inv0 = const.tile([P, NIT, NB], F32)
-        nc.vector.reciprocal(out=inv0[:], in_=mag[0][:])
+        nc.vector.reciprocal(out=inv0[:, :, 5:8], in_=mag[0][:, :, 5:8])
         beta_q = const.tile([P, NIT, NB], F32)
-        nc.vector.tensor_tensor(out=beta_q[:, :, 1:8], in0=mag[3][:, :, 1:8], in1=inv4[:, :, 0:7], op=ALU.mult)
+        nc.vector.tensor_tensor(out=beta_q[:, :, 1:4], in0=mag[3][:, :, 1:4], in1=inv4[:, :, 0:3], op=ALU.mult)
         alpha_q = const.tile([P, NIT, NB], F32)
-        nc.vector.reciprocal(out=alpha_q[:, :, 2:8], in_=beta_q[:, :, 2:8])
-        nc.vector.tensor_tensor(out=alpha_q[:, :, 2:8], in0=alpha_q[:, :, 2:8], in1=mag[2][:, :, 2:8], op=ALU.mult)
-        nc.vector.tensor_tensor(out=alpha_q[:, :, 2:8], in0=alpha_q[:, :, 2:8], in1=inv4[:, :, 0:6], op=ALU.mult)
-        nc.vector.tensor_scalar_mul(out=alpha_q[:, :, 2:8], in0=alpha_q[:, :, 2:8], scalar1=-1.0)
+        nc.vector.reciprocal(out=alpha_q[:, :, 2:4], in_=beta_q[:, :, 2:4])
+        nc.vector.tensor_tensor(out=alpha_q[:, :, 2:4], in0=alpha_q[:, :, 2:4], in1=mag[2][:, :, 2:4], op=ALU.mult)
+        nc.vector.tensor_tensor(out=alpha_q[:, :, 2:4], in0=alpha_q[:, :, 2:4], in1=inv4[:, :, 0:2], op=ALU.mult)
+        nc.vector.tensor_scalar_mul(out=alpha_q[:, :, 2:4], in0=alpha_q[:, :, 2:4], scalar1=-1.0)
         beta_p = const.tile([P, NIT, NB], F32)
-        nc.vector.tensor_tensor(out=beta_p[:, :, 0:7], in0=mag[1][:, :, 0:7], in1=inv0[:, :, 1:8], op=ALU.mult)
-        nc.vector.tensor_scalar_mul(out=beta_p[:, :, 0:7], in0=beta_p[:, :, 0:7], scalar1=-1.0)
+        nc.vector.tensor_tensor(out=beta_p[:, :, 4:7], in0=mag[1][:, :, 4:7], in1=inv0[:, :, 5:8], op=ALU.mult)
+        nc.vector.tensor_scalar_mul(out=beta_p[:, :, 4:7], in0=beta_p[:, :, 4:7], scalar1=-1.0)
         alpha_p = const.tile([P, NIT, NB], F32)
-        nc.vector.reciprocal(out=alpha_p[:, :, 0:6], in_=beta_p[:, :, 0:6])
-        nc.vector.tensor_tensor(out=alpha_p[:, :, 0:6], in0=alpha_p[:, :, 0:6], in1=mag[2][:, :, 0:6], op=ALU.mult)
-        nc.vector.tensor_tensor(out=alpha_p[:, :, 0:6], in0=alpha_p[:, :, 0:6], in1=inv0[:, :, 2:8], op=ALU.mult)
+        nc.vector.reciprocal(out=alpha_p[:, :, 4:6], in_=beta_p[:, :, 4:6])
+        nc.vector.tensor_tensor(out=alpha_p[:, :, 4:6], in0=alpha_p[:, :, 4:6], in1=mag[2][:, :, 4:6], op=ALU.mult)
+        nc.vector.tensor_tensor(out=alpha_p[:, :, 4:6], in0=alpha_p[:, :, 4:6], in1=inv0[:, :, 6:8], op=ALU.mult)
 
         xT = keep.tile([P, NIT, B], BF16)
-        for pair in range(NIT // 2):
+        a_codes = keep.tile([P, 2, B], U32, align_bytes=64)
+        a_scales = keep.tile([P, 2, B], U8, align_bytes=64)
+        bw_codes = keep.tile([P, 2, 2, OH], U32, align_bytes=64)
+        bw_scales = keep.tile([P, 2, 2, OH], U8, align_bytes=64)
+        bs_codes = keep.tile([P, NIT, 2, B], U32, align_bytes=64)
+        bs_scales = keep.tile([P, NIT, 2, B], U8, align_bytes=64)
+        sw_view = spline_weight.rearrange("(t p) i j -> p t (i j)", p=P)
+        sc_view = spline_scaler.rearrange("(t p) i -> p t i", p=P)
+
+        def x_pair(pair):
             ps = trp.tile([P, 2, B], BF16, name="ps_x", tag="tr")
             for s in range(2):
                 it = 2 * pair + s
@@ -104,161 +127,277 @@ def tile_bsplinekanlayer_kernel(tc, x, base_weight, spline_weight, spline_scaler
                     nc.tensor.transpose(ps[:, s, bt * P:(bt + 1) * P], x_sb[bt][:, it * P:(it + 1) * P], ident_bf[:])
             nc.scalar.copy(out=xT[:, 2 * pair:2 * pair + 2, :], in_=ps[:])
 
-        a_codes = keep.tile([P, 2, B], U32, align_bytes=64)
-        a_scales = keep.tile([P, 2, B], U8, align_bytes=64)
-        for g in range(2):
+        def silu_group(g):
             sg = grp.tile([P, B, 4], BF16, name="sg", tag="grp", align_bytes=64)
             nc.scalar.activation(out=sg[:], in_=xT[:, 4 * g:4 * g + 4, :].rearrange("p t b -> p b t"), func=AF.Silu)
+            return sg
+
+        def silu_quant(g, sg):
             nc.vector.quantize_mx(out=a_codes[:, g, :].bitcast(FP8X4), scales=a_scales[:, g, :], in_=sg[:].rearrange("p b t -> p (b t)"))
 
-        scT2 = keep.tile([P, NIT, 2 * OUT], BF16)
-        bw_codes = keep.tile([P, 2, 2, OH], U32, align_bytes=64)
-        bw_scales = keep.tile([P, 2, 2, OH], U8, align_bytes=64)
-        bs_codes = keep.tile([P, NIT, 2, B], U32, align_bytes=64)
-        bs_scales = keep.tile([P, NIT, 2, B], U8, align_bytes=64)
+        def load_rows(src, h, label):
+            tiles = []
+            for oo in range(4):
+                st = stage.tile([P, IN], BF16, name="%s%d" % (label, oo), tag="in2k")
+                nc.sync.dma_start(out=st[:], in_=src[(4 * h + oo) * P:(4 * h + oo + 1) * P, :])
+                tiles.append(st)
+            return tiles
 
-        def half_prologue(h):
-            sc_sb = []
+        def load_scaler(it, h):
+            blk = scbp.tile([P, 4, P], BF16, name="scblk")
+            nc.sync.dma_start(out=blk[:], in_=sc_view[:, 4 * h:4 * h + 4, it * P:(it + 1) * P])
+            return blk
+
+        def scaler_tile(blk, it):
+            ps = trp.tile([P, 4, 2 * P], BF16, name="ps_sc", tag="tr")
             for oo in range(4):
-                st = stage.tile([P, IN], BF16, name="sc%d" % oo, tag="in2k")
-                nc.sync.dma_start(out=st[:], in_=spline_scaler[(4 * h + oo) * P:(4 * h + oo + 1) * P, :])
-                sc_sb.append(st)
-            for it in range(NIT):
-                ps = trp.tile([P, 4, 2 * P], BF16, name="ps_sc", tag="tr")
-                for oo in range(4):
-                    nc.tensor.matmul(out=ps[:, oo, :], lhsT=sc_sb[oo][:, it * P:(it + 1) * P], rhs=dup[:].rearrange("p o e -> p (o e)"), start=True, stop=True)
-                nc.scalar.copy(out=scT2[:, it, h * 2 * OH:(h + 1) * 2 * OH], in_=ps[:].rearrange("p a b -> p (a b)"))
-            bw_sb = []
-            for oo in range(4):
-                bt_ = stage.tile([P, IN], BF16, name="bw%d" % oo, tag="in2k")
-                nc.sync.dma_start(out=bt_[:], in_=base_weight[(4 * h + oo) * P:(4 * h + oo + 1) * P, :])
-                bw_sb.append(bt_)
-            for g in range(2):
-                bwg = grp.tile([P, OH, 4], BF16, name="bwg", tag="grp", align_bytes=64)
-                for half in range(2):
-                    ps = trp.tile([P, 4, 2 * P], BF16, name="ps_bw", tag="tr")
-                    for t in range(4):
-                        for o2 in range(2):
-                            nc.tensor.transpose(ps[:, t, o2 * P:(o2 + 1) * P], bw_sb[2 * half + o2][:, (4 * g + t) * P:(4 * g + t + 1) * P], ident_bf[:])
-                    nc.scalar.copy(out=bwg[:, half * 256:(half + 1) * 256, :], in_=ps[:].rearrange("p t o -> p o t"))
-                nc.vector.quantize_mx(out=bw_codes[:, g, h, :].bitcast(FP8X4), scales=bw_scales[:, g, h, :], in_=bwg[:].rearrange("p o t -> p (o t)"))
+                nc.tensor.matmul(out=ps[:, oo, :], lhsT=blk[:, oo, :], rhs=dup[:].rearrange("p o e -> p (o e)"), start=True, stop=True)
+            sct = sctp.tile([P, 2 * OH], BF16, name="sct%d" % it)
+            nc.scalar.copy(out=sct[:], in_=ps[:].rearrange("p a b -> p (a b)"))
+            return sct
+
+        def base_bank(bw_sb, bwg, g, half):
+            ps = trp.tile([P, 4, 2 * P], BF16, name="ps_bw", tag="tr")
+            for t in range(4):
+                for o2 in range(2):
+                    nc.tensor.transpose(ps[:, t, o2 * P:(o2 + 1) * P], bw_sb[2 * half + o2][:, (4 * g + t) * P:(4 * g + t + 1) * P], ident_bf[:])
+            nc.scalar.copy(out=bwg[:, half * 256:(half + 1) * 256, :], in_=ps[:].rearrange("p t o -> p o t"))
+
+        def base_quant(bwg, g, h):
+            nc.vector.quantize_mx(out=bw_codes[:, g, h, :].bitcast(FP8X4), scales=bw_scales[:, g, h, :], in_=bwg[:].rearrange("p o t -> p (o t)"))
 
         def fma(o, a, s, b_):
             nc.vector.scalar_tensor_tensor(out=o, in0=a, scalar=s, in1=b_, op0=ALU.mult, op1=ALU.add)
 
-        def basis(it):
-            v = xT[:, it, :]
+        def clip(where, o, c, s):
+            if where == "act":
+                nc.scalar.activation(out=o, in_=c, func=AF.Relu, scale=s)
+            elif where == "dve":
+                nc.vector.tensor_scalar(out=o, in0=c, scalar1=s, scalar2=0.0, op0=ALU.mult, op1=ALU.max)
+            else:
+                nc.gpsimd.tensor_scalar(out=o, in0=c, scalar1=s, scalar2=0.0, op0=ALU.mult, op1=ALU.max)
+
+        def squares(it):
             cube = {}
-            for r in range(3, 9):
+            for r in CUBE_ORDER:
                 c = cubep.tile([P, B], F32, name="cube%d" % r)
-                nc.scalar.activation(out=c[:], in_=v, func=AF.Square, bias=neg_knot[:, it, r:r + 1], scale=1.0)
-                nc.vector.scalar_tensor_tensor(out=c[:], in0=v, scalar=knot[:, it, r:r + 1], in1=c[:], op0=ALU.subtract, op1=ALU.mult)
+                nc.scalar.activation(out=c[:], in_=xT[:, it, :], func=AF.Square, bias=neg_knot[:, it, r:r + 1], scale=1.0)
                 cube[r] = c
-            f = planep.tile([P, NB, B], F32, name="planes")
-            hi = {4: f[:, 0, :]}
+            return cube
+
+        def products(it, cube):
+            for r in CUBE_ORDER:
+                nc.vector.scalar_tensor_tensor(out=cube[r][:], in0=xT[:, it, :], scalar=knot[:, it, r:r + 1], in1=cube[r][:], op0=ALU.subtract, op1=ALU.mult)
+
+        def clips(it, cube):
+            flo = planep.tile([P, 4, B], F32, name="flo")
+            fhi = planep.tile([P, 4, B], F32, name="fhi")
+            hi = {4: flo[:, 0, :]}
             for r in range(5, 8):
                 hq = cubep.tile([P, B], F32, name="hi%d" % r)
                 hi[r] = hq[:]
             for r in range(4, 8):
-                nc.scalar.activation(out=hi[r], in_=cube[r][:], func=AF.Relu, scale=neg_mag4[:, it, r - 4:r - 3])
-            lo = {}
-            for r in range(3, 7):
-                nc.scalar.activation(out=cube[r][:], in_=cube[r][:], func=AF.Relu, scale=mag[0][:, it, r:r + 1])
+                clip(CLIP_HI[r], hi[r], cube[r][:], neg_mag4[:, it, r - 4:r - 3])
+            lo = {7: fhi[:, 3, :]}
+            clip(CLIP_LO[7], lo[7], cube[7][:], mag[0][:, it, 7:8])
+            for r in range(6, 3, -1):
+                clip(CLIP_LO[r], cube[r][:], cube[r][:], mag[0][:, it, r:r + 1])
                 lo[r] = cube[r][:]
-            nc.scalar.activation(out=f[:, 7, :], in_=cube[7][:], func=AF.Relu, scale=mag[0][:, it, 7:8])
-            lo[7] = f[:, 7, :]
-            nc.scalar.activation(out=cube[8][:], in_=cube[8][:], func=AF.Relu, scale=neg_mag4[:, it, 4:5])
-            hi[8] = cube[8][:]
+            return {"flo": flo, "fhi": fhi, "hi": hi, "lo": lo, "cube": cube}
 
-            fma(f[:, 1, :], hi[4], beta_q[:, it, 1:2], hi[5])
-            fma(f[:, 2, :], hi[4], alpha_q[:, it, 2:3], hi[5])
-            fma(f[:, 2, :], f[:, 2, :], beta_q[:, it, 2:3], hi[6])
-            fma(f[:, 3, :], hi[5], alpha_q[:, it, 3:4], hi[6])
-            fma(f[:, 3, :], f[:, 3, :], beta_q[:, it, 3:4], hi[7])
-            nc.vector.tensor_tensor(out=f[:, 3, :], in0=f[:, 3, :], in1=lo[3], op=ALU.min)
-            fma(f[:, 4, :], lo[6], alpha_p[:, it, 4:5], lo[5])
-            fma(f[:, 4, :], f[:, 4, :], beta_p[:, it, 4:5], lo[4])
-            nc.vector.tensor_tensor(out=f[:, 4, :], in0=f[:, 4, :], in1=hi[8], op=ALU.min)
-            fma(f[:, 5, :], lo[7], alpha_p[:, it, 5:6], lo[6])
-            fma(f[:, 5, :], f[:, 5, :], beta_p[:, it, 5:6], lo[5])
-            fma(f[:, 6, :], lo[7], beta_p[:, it, 6:7], lo[6])
+        def sums_lo(it, st):
+            flo, hi = st["flo"], st["hi"]
+            fma(flo[:, 1, :], hi[4], beta_q[:, it, 1:2], hi[5])
+            fma(flo[:, 2, :], hi[4], alpha_q[:, it, 2:3], hi[5])
+            fma(flo[:, 3, :], hi[5], alpha_q[:, it, 3:4], hi[6])
+            fma(flo[:, 2, :], flo[:, 2, :], beta_q[:, it, 2:3], hi[6])
+            fma(flo[:, 3, :], flo[:, 3, :], beta_q[:, it, 3:4], hi[7])
+            nc.vector.scalar_tensor_tensor(out=flo[:, 3, :], in0=st["cube"][3][:], scalar=mag[0][:, it, 3:4], in1=flo[:, 3, :], op0=ALU.mult, op1=ALU.min)
 
-            for jh in range(2):
-                bg = bgp.tile([P, B, 4], BF16, name="bg", align_bytes=64)
-                src = f[:, 4 * jh:4 * jh + 4, :].rearrange("p t b -> p b t")
-                if jh == 0:
-                    nc.scalar.copy(out=bg[:], in_=src)
-                else:
-                    nc.vector.tensor_copy(out=bg[:], in_=src)
-                nc.vector.quantize_mx(out=bs_codes[:, it, jh, :].bitcast(FP8X4), scales=bs_scales[:, it, jh, :], in_=bg[:].rearrange("p b t -> p (b t)"))
+        def sums_hi(it, st):
+            fhi, lo = st["fhi"], st["lo"]
+            fma(fhi[:, 2, :], lo[7], beta_p[:, it, 6:7], lo[6])
+            fma(fhi[:, 1, :], lo[7], alpha_p[:, it, 5:6], lo[6])
+            fma(fhi[:, 0, :], lo[6], alpha_p[:, it, 4:5], lo[5])
+            fma(fhi[:, 1, :], fhi[:, 1, :], beta_p[:, it, 5:6], lo[5])
+            fma(fhi[:, 0, :], fhi[:, 0, :], beta_p[:, it, 4:5], lo[4])
+            nc.vector.scalar_tensor_tensor(out=fhi[:, 0, :], in0=st["cube"][8][:], scalar=neg_mag4[:, it, 4:5], in1=fhi[:, 0, :], op0=ALU.mult, op1=ALU.min)
 
-        sw_view = spline_weight.rearrange("(t p) i j -> p t (i j)", p=P)
+        def regroup(it, jh, planes):
+            bg = bgp.tile([P, B, 4], BF16, name="bg", align_bytes=64)
+            if (it, jh) in REGROUP_ON_VECTOR:
+                nc.vector.tensor_copy(out=bg[:], in_=planes[:].rearrange("p t b -> p b t"))
+            else:
+                nc.scalar.copy(out=bg[:], in_=planes[:].rearrange("p t b -> p b t"))
+            return bg
 
-        def weights(it, h, acc):
+        def basis_quant(it, jh, bg):
+            nc.vector.quantize_mx(out=bs_codes[:, it, jh, :].bitcast(FP8X4), scales=bs_scales[:, it, jh, :], in_=bg[:].rearrange("p b t -> p (b t)"))
+
+        def load_raw(q):
+            it, h = q % NIT, q // NIT
             raw = rawp.tile([P, 4, P * NB], BF16, name="raw")
             nc.sync.dma_start(out=raw[:], in_=sw_view[:, 4 * h:4 * h + 4, it * P * NB:(it + 1) * P * NB])
-            words = raw[:].bitcast(F32).rearrange("p t (i m) -> p t m i", m=4)
-            for jh in range(2):
-                wg = grp.tile([P, OH, 4], BF16, name="wg", tag="grp", align_bytes=64)
-                for half in range(2):
-                    ps = trp.tile([P, 2, 2 * P], F32, name="ps_w", tag="tr")
-                    for m0 in range(2):
-                        for o2 in range(2):
-                            nc.tensor.transpose(ps[:, m0, o2 * P:(o2 + 1) * P], words[:, 2 * half + o2, 2 * jh + m0, :], ident_f[:])
-                    lo_col = h * 2 * OH + half * OH
-                    nc.vector.tensor_tensor(
-                        out=wg[:, half * 256:(half + 1) * 256, :].rearrange("p o (m e) -> p o m e", e=2),
-                        in0=ps[:].bitcast(BF16).rearrange("p m (o e) -> p o m e", e=2),
-                        in1=scT2[:, it, lo_col:lo_col + OH].rearrange("p (o e) -> p o e", e=2).unsqueeze(2).to_broadcast([P, 256, 2, 2]),
-                        op=ALU.mult,
-                    )
-                wc = wcp.tile([P, OH], U32, name="wc", align_bytes=64)
-                ws = wcp.tile([P, OH], U8, name="ws", align_bytes=64)
-                nc.vector.quantize_mx(out=wc[:].bitcast(FP8X4), scales=ws[:], in_=wg[:].rearrange("p o t -> p (o t)"))
-                for bt in range(NBT):
-                    nc.tensor.matmul_mx(
-                        out=acc[bt][:],
-                        lhsT=bs_codes[:, it, jh, bt * P:(bt + 1) * P].bitcast(FP8X4),
-                        lhsT_scale=bs_scales[:, it, jh, bt * P:(bt + 1) * P],
-                        rhs=wc[:].bitcast(FP8X4),
-                        rhs_scale=ws[:],
-                        start=False,
-                        stop=(it == NIT - 1 and jh == 1),
-                    )
+            return raw
 
-        def open_round(h):
+        def w_bank(raw, jh, half):
+            words = raw[:].bitcast(F32).rearrange("p t (i m) -> p t m i", m=4)
+            ps = trw.tile([P, 2, 2 * P], F32, name="ps_w", tag="w")
+            for m0 in range(2):
+                for o2 in range(2):
+                    nc.tensor.transpose(ps[:, m0, o2 * P:(o2 + 1) * P], words[:, 2 * half + o2, 2 * jh + m0, :], ident_f[:])
+            return ps
+
+        def w_scale(wg, ps, sct, half):
+            nc.vector.tensor_tensor(
+                out=wg[:, half * 256:(half + 1) * 256, :].rearrange("p o (m e) -> p o m e", e=2),
+                in0=ps[:].bitcast(BF16).rearrange("p m (o e) -> p o m e", e=2),
+                in1=sct[:, half * OH:(half + 1) * OH].rearrange("p (o e) -> p o e", e=2).unsqueeze(2).to_broadcast([P, 256, 2, 2]),
+                op=ALU.mult,
+            )
+
+        def w_quant(wg):
+            wc = wcp.tile([P, OH], U32, name="wc", align_bytes=64)
+            ws = wcp.tile([P, OH], U8, name="ws", align_bytes=64)
+            nc.vector.quantize_mx(out=wc[:].bitcast(FP8X4), scales=ws[:], in_=wg[:].rearrange("p o t -> p (o t)"))
+            return wc, ws
+
+        def passes(acc, lhs_c, lhs_s, rhs_c, rhs_s, first, last):
+            for bt in range(NBT):
+                nc.tensor.matmul_mx(
+                    out=acc[bt][:],
+                    lhsT=lhs_c[:, bt * P:(bt + 1) * P].bitcast(FP8X4),
+                    lhsT_scale=lhs_s[:, bt * P:(bt + 1) * P],
+                    rhs=rhs_c.bitcast(FP8X4),
+                    rhs_scale=rhs_s,
+                    start=first,
+                    stop=last,
+                )
+
+        def new_acc():
             acc = []
             for bt in range(NBT):
                 a = accp.tile([P, OH], F32, name="acc%d" % bt)
                 acc.append(a)
-            for g in range(2):
-                for bt in range(NBT):
-                    nc.tensor.matmul_mx(
-                        out=acc[bt][:],
-                        lhsT=a_codes[:, g, bt * P:(bt + 1) * P].bitcast(FP8X4),
-                        lhsT_scale=a_scales[:, g, bt * P:(bt + 1) * P],
-                        rhs=bw_codes[:, g, h, :].bitcast(FP8X4),
-                        rhs_scale=bw_scales[:, g, h, :],
-                        start=(g == 0),
-                        stop=False,
-                    )
             return acc
+
+        def base_passes(acc, h):
+            for g in range(2):
+                passes(acc, a_codes[:, g, :], a_scales[:, g, :], bw_codes[:, g, h, :], bw_scales[:, g, h, :], False, g == 1)
 
         def close_round(h, acc):
             for bt in range(NBT):
                 o_sb = outp.tile([P, OH], F32, name="o_sb")
-                nc.scalar.copy(out=o_sb[:], in_=acc[bt][:])
+                if bt % 2 == 0:
+                    nc.scalar.copy(out=o_sb[:], in_=acc[bt][:])
+                else:
+                    nc.vector.tensor_copy(out=o_sb[:], in_=acc[bt][:])
                 nc.sync.dma_start(out=out[bt * P:(bt + 1) * P, h * OH:(h + 1) * OH], in_=o_sb[:])
 
-        half_prologue(0)
-        acc0 = open_round(0)
-        for it in range(NIT):
-            basis(it)
-            weights(it, 0, acc0)
-            if it == 3:
-                half_prologue(1)
-        close_round(0, acc0)
-        acc1 = open_round(1)
-        for it in range(NIT):
-            weights(it, 1, acc1)
-        close_round(1, acc1)
+        blk = {(0, 0): load_scaler(0, 0)}
+        raws = {0: load_raw(0), 1: load_raw(1)}
+        blk[(1, 0)] = load_scaler(1, 0)
+        bw_rows = {0: load_rows(base_weight, 0, "bwa")}
+        x_pair(0)
+        cube = squares(0)
+        products(0, cube)
+        sct = {0: scaler_tile(blk[(0, 0)], 0)}
+        state = clips(0, cube)
+        acc = new_acc()
+        bwg = {}
+        done = {}
+        extra = {0: ("x", 1), 2: ("x", 2), 4: ("x", 3), 1: ("b", 0, 0), 3: ("b", 0, 1), 5: ("b", 1, 0), 6: ("b", 1, 1)}
+        for n in range(NIT):
+            if n >= 1:
+                for jh in range(2):
+                    wc, ws = done[(n - 1, jh)]
+                    passes(acc, bs_codes[:, n - 1, jh, :], bs_scales[:, n - 1, jh, :], wc[:], ws[:], n == 1 and jh == 0, False)
+            b00 = w_bank(raws[n], 0, 0)
+            b01 = w_bank(raws[n], 0, 1)
+            b10 = w_bank(raws[n], 1, 0)
+            if n >= 1:
+                blk[(n - 1, 1)] = load_scaler(n - 1, 1)
+            if n + 2 < NIT:
+                blk[(n + 2, 0)] = load_scaler(n + 2, 0)
+            if n == 5:
+                bw_rows[1] = load_rows(base_weight, 1, "bwb")
+            sums_lo(n, state)
+            if n + 1 < NIT:
+                cube = squares(n + 1)
+                sct[n + 1] = scaler_tile(blk[(n + 1, 0)], n + 1)
+            sums_hi(n, state)
+            bg0 = regroup(n, 0, state["flo"])
+            if n >= 1:
+                sct[n - 1] = scaler_tile(blk[(n - 1, 1)], n - 1)
+            if n + 1 < NIT:
+                products(n + 1, cube)
+            bg1 = regroup(n, 1, state["fhi"])
+            if n in extra:
+                e = extra[n]
+                if e[0] == "x":
+                    x_pair(e[1])
+                else:
+                    if e[2] == 0:
+                        bwg[e[1]] = grp.tile([P, OH, 4], BF16, name="bwg", tag="grp", align_bytes=64)
+                    base_bank(bw_rows[0], bwg[e[1]], e[1], e[2])
+            if n in (1, 5):
+                sg = silu_group(n // 4)
+            basis_quant(n, 0, bg0)
+            wg0 = grp.tile([P, OH, 4], BF16, name="wg", tag="grp", align_bytes=64)
+            w_scale(wg0, b00, sct[n], 0)
+            w_scale(wg0, b01, sct[n], 1)
+            b11 = w_bank(raws[n], 1, 1)
+            raws[n + 2] = load_raw(n + 2)
+            done[(n, 0)] = w_quant(wg0)
+            basis_quant(n, 1, bg1)
+            wg1 = grp.tile([P, OH, 4], BF16, name="wg", tag="grp", align_bytes=64)
+            w_scale(wg1, b10, sct[n], 0)
+            w_scale(wg1, b11, sct[n], 1)
+            done[(n, 1)] = w_quant(wg1)
+            if n in (1, 5):
+                silu_quant(n // 4, sg)
+            if n in (3, 6):
+                base_quant(bwg[n // 6], n // 6, 0)
+            if n + 1 < NIT:
+                state = clips(n + 1, cube)
+        for jh in range(2):
+            wc, ws = done[(NIT - 1, jh)]
+            passes(acc, bs_codes[:, NIT - 1, jh, :], bs_scales[:, NIT - 1, jh, :], wc[:], ws[:], False, False)
+        base_passes(acc, 0)
+        blk[(NIT - 1, 1)] = load_scaler(NIT - 1, 1)
+        sct[NIT - 1] = scaler_tile(blk[(NIT - 1, 1)], NIT - 1)
+        close_round(0, acc)
+
+        acc = new_acc()
+        units = [(n, jh) for n in range(NIT) for jh in range(2)]
+        bank = {}
+
+        def lift(k, half):
+            if k < len(units):
+                n, jh = units[k]
+                bank[(k, half)] = w_bank(raws[NIT + n], jh, half)
+                if jh == 1 and half == 1 and n + 2 < NIT:
+                    raws[NIT + n + 2] = load_raw(NIT + n + 2)
+
+        lift(0, 0)
+        lift(0, 1)
+        lift(1, 0)
+        late = {2: (0, 0), 4: (0, 1), 6: (1, 0), 8: (1, 1)}
+        for k in range(len(units)):
+            n, jh = units[k]
+            wg = grp.tile([P, OH, 4], BF16, name="wg", tag="grp", align_bytes=64)
+            w_scale(wg, bank[(k, 0)], sct[n], 0)
+            lift(k + 1, 1)
+            w_scale(wg, bank[(k, 1)], sct[n], 1)
+            wc, ws = w_quant(wg)
+            passes(acc, bs_codes[:, n, jh, :], bs_scales[:, n, jh, :], wc[:], ws[:], k == 0, False)
+            lift(k + 2, 0)
+            if k in late:
+                g, half = late[k]
+                if half == 0:
+                    bwg[g] = grp.tile([P, OH, 4], BF16, name="bwg", tag="grp", align_bytes=64)
+                base_bank(bw_rows[1], bwg[g], g, half)
+                if half == 1:
+                    base_quant(bwg[g], g, 1)
+        base_passes(acc, 1)
+        close_round(1, acc)

@@ -21,22 +21,20 @@ NIT = IN // P
 NBT = B // P
 OH = 512
 FLOPS = 2 * B * OUT * (IN + IN * NB)
-CUBE_ORDER = (4, 5, 6, 7, 3, 8)
-CLIP_HI = {4: "act", 5: "act", 6: "act", 7: "act"}
-CLIP_LO = {4: "act", 5: "act", 6: "act", 7: "act"}
+CLIP_HI = {4: "dve", 5: "act", 6: "act", 7: "act"}
+CLIP_LO = {4: "act", 5: "act", 6: "act", 7: "dve"}
 REGROUP_ON_VECTOR = ()
 
 
 def tile_bsplinekanlayer_kernel(tc, x, base_weight, spline_weight, spline_scaler, grid, out):
     nc = tc.nc
     with ExitStack() as ctx:
-        ctx.enter_context(tc.manual_schedule())
         const = ctx.enter_context(tc.tile_pool(name="const", bufs=1))
         keep = ctx.enter_context(tc.tile_pool(name="keep", bufs=1))
         stage = ctx.enter_context(tc.tile_pool(name="stage", bufs=8))
         rawp = ctx.enter_context(tc.tile_pool(name="rawp", bufs=2))
         sctp = ctx.enter_context(tc.tile_pool(name="sctp", bufs=1))
-        scbp = ctx.enter_context(tc.tile_pool(name="scbp", bufs=3))
+        diagp = ctx.enter_context(tc.tile_pool(name="diagp", bufs=2))
         grp = ctx.enter_context(tc.tile_pool(name="grp", bufs=3))
         wcp = ctx.enter_context(tc.tile_pool(name="wcp", bufs=3))
         cubep = ctx.enter_context(tc.tile_pool(name="cubep", bufs=2))
@@ -44,8 +42,7 @@ def tile_bsplinekanlayer_kernel(tc, x, base_weight, spline_weight, spline_scaler
         bgp = ctx.enter_context(tc.tile_pool(name="bgp", bufs=2))
         outp = ctx.enter_context(tc.tile_pool(name="outp", bufs=2))
         accp = ctx.enter_context(tc.psum_pool(name="accp", bufs=1))
-        trw = ctx.enter_context(tc.psum_pool(name="trw", bufs=3))
-        trp = ctx.enter_context(tc.psum_pool(name="trp", bufs=1))
+        trp = ctx.enter_context(tc.psum_pool(name="trp", bufs=4))
 
         grid_sb = const.tile([P, NIT, NK], BF16)
         nc.sync.dma_start(out=grid_sb[:], in_=grid.rearrange("(t p) r -> p t r", p=P))
@@ -62,8 +59,6 @@ def tile_bsplinekanlayer_kernel(tc, x, base_weight, spline_weight, spline_scaler
         make_identity(nc, ident_bf[:])
         ident_f = const.tile([P, P], F32)
         make_identity(nc, ident_f[:])
-        dup = const.tile([P, P, 2], BF16)
-        nc.vector.tensor_copy(out=dup[:], in_=ident_bf[:].unsqueeze(2).to_broadcast([P, P, 2]))
 
         knot = const.tile([P, NIT, NK], F32)
         nc.vector.tensor_copy(out=knot[:], in_=grid_sb[:])
@@ -96,30 +91,23 @@ def tile_bsplinekanlayer_kernel(tc, x, base_weight, spline_weight, spline_scaler
         nc.vector.reciprocal(out=inv0[:, :, 5:8], in_=mag[0][:, :, 5:8])
         beta_q = const.tile([P, NIT, NB], F32)
         nc.vector.tensor_tensor(out=beta_q[:, :, 1:4], in0=mag[3][:, :, 1:4], in1=inv4[:, :, 0:3], op=ALU.mult)
+        gam_q = const.tile([P, NIT, NB], F32)
+        nc.vector.tensor_tensor(out=gam_q[:, :, 2:4], in0=mag[2][:, :, 2:4], in1=inv4[:, :, 0:2], op=ALU.mult)
+        nc.vector.tensor_scalar_mul(out=gam_q[:, :, 2:4], in0=gam_q[:, :, 2:4], scalar1=-1.0)
         alpha_q = const.tile([P, NIT, NB], F32)
-        nc.vector.reciprocal(out=alpha_q[:, :, 2:4], in_=beta_q[:, :, 2:4])
-        nc.vector.tensor_tensor(out=alpha_q[:, :, 2:4], in0=alpha_q[:, :, 2:4], in1=mag[2][:, :, 2:4], op=ALU.mult)
-        nc.vector.tensor_tensor(out=alpha_q[:, :, 2:4], in0=alpha_q[:, :, 2:4], in1=inv4[:, :, 0:2], op=ALU.mult)
-        nc.vector.tensor_scalar_mul(out=alpha_q[:, :, 2:4], in0=alpha_q[:, :, 2:4], scalar1=-1.0)
+        nc.vector.reciprocal(out=alpha_q[:, :, 2:3], in_=beta_q[:, :, 2:3])
+        nc.vector.tensor_tensor(out=alpha_q[:, :, 2:3], in0=alpha_q[:, :, 2:3], in1=gam_q[:, :, 2:3], op=ALU.mult)
         beta_p = const.tile([P, NIT, NB], F32)
         nc.vector.tensor_tensor(out=beta_p[:, :, 4:7], in0=mag[1][:, :, 4:7], in1=inv0[:, :, 5:8], op=ALU.mult)
         nc.vector.tensor_scalar_mul(out=beta_p[:, :, 4:7], in0=beta_p[:, :, 4:7], scalar1=-1.0)
+        gam_p = const.tile([P, NIT, NB], F32)
+        nc.vector.tensor_tensor(out=gam_p[:, :, 4:6], in0=mag[2][:, :, 4:6], in1=inv0[:, :, 6:8], op=ALU.mult)
         alpha_p = const.tile([P, NIT, NB], F32)
-        nc.vector.reciprocal(out=alpha_p[:, :, 4:6], in_=beta_p[:, :, 4:6])
-        nc.vector.tensor_tensor(out=alpha_p[:, :, 4:6], in0=alpha_p[:, :, 4:6], in1=mag[2][:, :, 4:6], op=ALU.mult)
-        nc.vector.tensor_tensor(out=alpha_p[:, :, 4:6], in0=alpha_p[:, :, 4:6], in1=inv0[:, :, 6:8], op=ALU.mult)
+        nc.vector.reciprocal(out=alpha_p[:, :, 5:6], in_=beta_p[:, :, 5:6])
+        nc.vector.tensor_tensor(out=alpha_p[:, :, 5:6], in0=alpha_p[:, :, 5:6], in1=gam_p[:, :, 5:6], op=ALU.mult)
 
         xT = keep.tile([P, NIT, B], BF16)
-        a_codes = keep.tile([P, 2, B], U32, align_bytes=64)
-        a_scales = keep.tile([P, 2, B], U8, align_bytes=64)
-        bw_codes = keep.tile([P, 2, 2, OH], U32, align_bytes=64)
-        bw_scales = keep.tile([P, 2, 2, OH], U8, align_bytes=64)
-        bs_codes = keep.tile([P, NIT, 2, B], U32, align_bytes=64)
-        bs_scales = keep.tile([P, NIT, 2, B], U8, align_bytes=64)
-        sw_view = spline_weight.rearrange("(t p) i j -> p t (i j)", p=P)
-        sc_view = spline_scaler.rearrange("(t p) i -> p t i", p=P)
-
-        def x_pair(pair):
+        for pair in range(NIT // 2):
             ps = trp.tile([P, 2, B], BF16, name="ps_x", tag="tr")
             for s in range(2):
                 it = 2 * pair + s
@@ -127,13 +115,17 @@ def tile_bsplinekanlayer_kernel(tc, x, base_weight, spline_weight, spline_scaler
                     nc.tensor.transpose(ps[:, s, bt * P:(bt + 1) * P], x_sb[bt][:, it * P:(it + 1) * P], ident_bf[:])
             nc.scalar.copy(out=xT[:, 2 * pair:2 * pair + 2, :], in_=ps[:])
 
-        def silu_group(g):
+        a_codes = keep.tile([P, 2, B], U32, align_bytes=64)
+        a_scales = keep.tile([P, 2, B], U8, align_bytes=64)
+        for g in range(2):
             sg = grp.tile([P, B, 4], BF16, name="sg", tag="grp", align_bytes=64)
             nc.scalar.activation(out=sg[:], in_=xT[:, 4 * g:4 * g + 4, :].rearrange("p t b -> p b t"), func=AF.Silu)
-            return sg
-
-        def silu_quant(g, sg):
             nc.vector.quantize_mx(out=a_codes[:, g, :].bitcast(FP8X4), scales=a_scales[:, g, :], in_=sg[:].rearrange("p b t -> p (b t)"))
+
+        bw_codes = keep.tile([P, 2, 2, OH], U32, align_bytes=64)
+        bw_scales = keep.tile([P, 2, 2, OH], U8, align_bytes=64)
+        bs_codes = keep.tile([P, NIT, 2, B], U32, align_bytes=64)
+        bs_scales = keep.tile([P, NIT, 2, B], U8, align_bytes=64)
 
         def load_rows(src, h, label):
             tiles = []
@@ -143,31 +135,38 @@ def tile_bsplinekanlayer_kernel(tc, x, base_weight, spline_weight, spline_scaler
                 tiles.append(st)
             return tiles
 
-        def load_scaler(it, h):
-            blk = scbp.tile([P, 4, P], BF16, name="scblk")
-            nc.sync.dma_start(out=blk[:], in_=sc_view[:, 4 * h:4 * h + 4, it * P:(it + 1) * P])
-            return blk
-
-        def scaler_tile(blk, it):
-            ps = trp.tile([P, 4, 2 * P], BF16, name="ps_sc", tag="tr")
+        def scaler_tile(sc_sb, it):
+            ps = trp.tile([P, 4, P], BF16, name="ps_sc", tag="tr")
             for oo in range(4):
-                nc.tensor.matmul(out=ps[:, oo, :], lhsT=blk[:, oo, :], rhs=dup[:].rearrange("p o e -> p (o e)"), start=True, stop=True)
+                nc.tensor.transpose(ps[:, oo, :], sc_sb[oo][:, it * P:(it + 1) * P], ident_bf[:])
             sct = sctp.tile([P, 2 * OH], BF16, name="sct%d" % it)
-            nc.scalar.copy(out=sct[:], in_=ps[:].rearrange("p a b -> p (a b)"))
+            nc.scalar.copy(out=sct[:].rearrange("p (o e) -> p o e", e=2), in_=ps[:].rearrange("p a b -> p (a b)").unsqueeze(2).to_broadcast([P, OH, 2]))
             return sct
 
-        def base_bank(bw_sb, bwg, g, half):
-            ps = trp.tile([P, 4, 2 * P], BF16, name="ps_bw", tag="tr")
-            for t in range(4):
-                for o2 in range(2):
-                    nc.tensor.transpose(ps[:, t, o2 * P:(o2 + 1) * P], bw_sb[2 * half + o2][:, (4 * g + t) * P:(4 * g + t + 1) * P], ident_bf[:])
-            nc.scalar.copy(out=bwg[:, half * 256:(half + 1) * 256, :], in_=ps[:].rearrange("p t o -> p o t"))
-
-        def base_quant(bwg, g, h):
-            nc.vector.quantize_mx(out=bw_codes[:, g, h, :].bitcast(FP8X4), scales=bw_scales[:, g, h, :], in_=bwg[:].rearrange("p o t -> p (o t)"))
+        def base_codes(bw_sb, h):
+            for g in range(2):
+                bwg = grp.tile([P, OH, 4], BF16, name="bwg", tag="grp", align_bytes=64)
+                for half in range(2):
+                    ps = trp.tile([P, 4, 2 * P], BF16, name="ps_bw", tag="tr")
+                    for t in range(4):
+                        for o2 in range(2):
+                            nc.tensor.transpose(ps[:, t, o2 * P:(o2 + 1) * P], bw_sb[2 * half + o2][:, (4 * g + t) * P:(4 * g + t + 1) * P], ident_bf[:])
+                    nc.scalar.copy(out=bwg[:, half * 256:(half + 1) * 256, :], in_=ps[:].rearrange("p t o -> p o t"))
+                nc.vector.quantize_mx(out=bw_codes[:, g, h, :].bitcast(FP8X4), scales=bw_scales[:, g, h, :], in_=bwg[:].rearrange("p o t -> p (o t)"))
 
         def fma(o, a, s, b_):
             nc.vector.scalar_tensor_tensor(out=o, in0=a, scalar=s, in1=b_, op0=ALU.mult, op1=ALU.add)
+
+        def cubes(it):
+            v = xT[:, it, :]
+            cube = {}
+            for r in range(3, 9):
+                c = cubep.tile([P, B], F32, name="cube%d" % r)
+                nc.scalar.activation(out=c[:], in_=v, func=AF.Square, bias=neg_knot[:, it, r:r + 1], scale=1.0)
+                cube[r] = c
+            for r in range(3, 9):
+                nc.vector.scalar_tensor_tensor(out=cube[r][:], in0=v, scalar=knot[:, it, r:r + 1], in1=cube[r][:], op0=ALU.subtract, op1=ALU.mult)
+            return cube
 
         def clip(where, o, c, s):
             if where == "act":
@@ -177,19 +176,18 @@ def tile_bsplinekanlayer_kernel(tc, x, base_weight, spline_weight, spline_scaler
             else:
                 nc.gpsimd.tensor_scalar(out=o, in0=c, scalar1=s, scalar2=0.0, op0=ALU.mult, op1=ALU.max)
 
-        def squares(it):
-            cube = {}
-            for r in CUBE_ORDER:
-                c = cubep.tile([P, B], F32, name="cube%d" % r)
-                nc.scalar.activation(out=c[:], in_=xT[:, it, :], func=AF.Square, bias=neg_knot[:, it, r:r + 1], scale=1.0)
-                cube[r] = c
-            return cube
+        def three_terms(a, b_, cb, c, cc):
+            db = diagp.tile([P, P], F32, name="db")
+            nc.gpsimd.tensor_scalar(out=db[:], in0=ident_f[:], scalar1=cb, scalar2=0.0, op0=ALU.mult, op1=ALU.add)
+            dc = diagp.tile([P, P], F32, name="dc")
+            nc.gpsimd.tensor_scalar(out=dc[:], in0=ident_f[:], scalar1=cc, scalar2=0.0, op0=ALU.mult, op1=ALU.add)
+            ps = trp.tile([P, B], F32, name="ps_sum", tag="tr")
+            nc.tensor.matmul(out=ps[:], lhsT=ident_f[:], rhs=a, start=True, stop=False)
+            nc.tensor.matmul(out=ps[:], lhsT=db[:], rhs=b_, start=False, stop=False)
+            nc.tensor.matmul(out=ps[:], lhsT=dc[:], rhs=c, start=False, stop=True)
+            return ps
 
-        def products(it, cube):
-            for r in CUBE_ORDER:
-                nc.vector.scalar_tensor_tensor(out=cube[r][:], in0=xT[:, it, :], scalar=knot[:, it, r:r + 1], in1=cube[r][:], op0=ALU.subtract, op1=ALU.mult)
-
-        def clips(it, cube):
+        def combine(it, cube):
             flo = planep.tile([P, 4, B], F32, name="flo")
             fhi = planep.tile([P, 4, B], F32, name="fhi")
             hi = {4: flo[:, 0, :]}
@@ -198,206 +196,122 @@ def tile_bsplinekanlayer_kernel(tc, x, base_weight, spline_weight, spline_scaler
                 hi[r] = hq[:]
             for r in range(4, 8):
                 clip(CLIP_HI[r], hi[r], cube[r][:], neg_mag4[:, it, r - 4:r - 3])
+            fma(flo[:, 1, :], hi[4], beta_q[:, it, 1:2], hi[5])
+            fma(flo[:, 2, :], hi[4], alpha_q[:, it, 2:3], hi[5])
+            fma(flo[:, 2, :], flo[:, 2, :], beta_q[:, it, 2:3], hi[6])
+            s3 = three_terms(hi[7], hi[6], beta_q[:, it, 3:4], hi[5], gam_q[:, it, 3:4])
+            nc.vector.scalar_tensor_tensor(out=flo[:, 3, :], in0=cube[3][:], scalar=mag[0][:, it, 3:4], in1=s3[:], op0=ALU.mult, op1=ALU.min)
             lo = {7: fhi[:, 3, :]}
             clip(CLIP_LO[7], lo[7], cube[7][:], mag[0][:, it, 7:8])
             for r in range(6, 3, -1):
                 clip(CLIP_LO[r], cube[r][:], cube[r][:], mag[0][:, it, r:r + 1])
                 lo[r] = cube[r][:]
-            return {"flo": flo, "fhi": fhi, "hi": hi, "lo": lo, "cube": cube}
-
-        def sums_lo(it, st):
-            flo, hi = st["flo"], st["hi"]
-            fma(flo[:, 1, :], hi[4], beta_q[:, it, 1:2], hi[5])
-            fma(flo[:, 2, :], hi[4], alpha_q[:, it, 2:3], hi[5])
-            fma(flo[:, 3, :], hi[5], alpha_q[:, it, 3:4], hi[6])
-            fma(flo[:, 2, :], flo[:, 2, :], beta_q[:, it, 2:3], hi[6])
-            fma(flo[:, 3, :], flo[:, 3, :], beta_q[:, it, 3:4], hi[7])
-            nc.vector.scalar_tensor_tensor(out=flo[:, 3, :], in0=st["cube"][3][:], scalar=mag[0][:, it, 3:4], in1=flo[:, 3, :], op0=ALU.mult, op1=ALU.min)
-
-        def sums_hi(it, st):
-            fhi, lo = st["fhi"], st["lo"]
             fma(fhi[:, 2, :], lo[7], beta_p[:, it, 6:7], lo[6])
             fma(fhi[:, 1, :], lo[7], alpha_p[:, it, 5:6], lo[6])
-            fma(fhi[:, 0, :], lo[6], alpha_p[:, it, 4:5], lo[5])
             fma(fhi[:, 1, :], fhi[:, 1, :], beta_p[:, it, 5:6], lo[5])
-            fma(fhi[:, 0, :], fhi[:, 0, :], beta_p[:, it, 4:5], lo[4])
-            nc.vector.scalar_tensor_tensor(out=fhi[:, 0, :], in0=st["cube"][8][:], scalar=neg_mag4[:, it, 4:5], in1=fhi[:, 0, :], op0=ALU.mult, op1=ALU.min)
+            s4 = three_terms(lo[4], lo[5], beta_p[:, it, 4:5], lo[6], gam_p[:, it, 4:5])
+            nc.vector.scalar_tensor_tensor(out=fhi[:, 0, :], in0=cube[8][:], scalar=neg_mag4[:, it, 4:5], in1=s4[:], op0=ALU.mult, op1=ALU.min)
+            return [flo, fhi]
 
-        def regroup(it, jh, planes):
-            bg = bgp.tile([P, B, 4], BF16, name="bg", align_bytes=64)
-            if (it, jh) in REGROUP_ON_VECTOR:
-                nc.vector.tensor_copy(out=bg[:], in_=planes[:].rearrange("p t b -> p b t"))
-            else:
-                nc.scalar.copy(out=bg[:], in_=planes[:].rearrange("p t b -> p b t"))
-            return bg
+        def regroup(it, planes):
+            for jh in range(2):
+                bg = bgp.tile([P, B, 4], BF16, name="bg", align_bytes=64)
+                if (it, jh) in REGROUP_ON_VECTOR:
+                    nc.vector.tensor_copy(out=bg[:], in_=planes[jh][:].rearrange("p t b -> p b t"))
+                else:
+                    nc.scalar.copy(out=bg[:], in_=planes[jh][:].rearrange("p t b -> p b t"))
+                nc.vector.quantize_mx(out=bs_codes[:, it, jh, :].bitcast(FP8X4), scales=bs_scales[:, it, jh, :], in_=bg[:].rearrange("p b t -> p (b t)"))
 
-        def basis_quant(it, jh, bg):
-            nc.vector.quantize_mx(out=bs_codes[:, it, jh, :].bitcast(FP8X4), scales=bs_scales[:, it, jh, :], in_=bg[:].rearrange("p b t -> p (b t)"))
+        sw_view = spline_weight.rearrange("(t p) i j -> p t (i j)", p=P)
 
-        def load_raw(q):
-            it, h = q % NIT, q // NIT
+        def load_raw(it, h):
             raw = rawp.tile([P, 4, P * NB], BF16, name="raw")
             nc.sync.dma_start(out=raw[:], in_=sw_view[:, 4 * h:4 * h + 4, it * P * NB:(it + 1) * P * NB])
             return raw
 
-        def w_bank(raw, jh, half):
+        def weights(it, raw, sct, acc):
             words = raw[:].bitcast(F32).rearrange("p t (i m) -> p t m i", m=4)
-            ps = trw.tile([P, 2, 2 * P], F32, name="ps_w", tag="w")
-            for m0 in range(2):
-                for o2 in range(2):
-                    nc.tensor.transpose(ps[:, m0, o2 * P:(o2 + 1) * P], words[:, 2 * half + o2, 2 * jh + m0, :], ident_f[:])
-            return ps
+            for jh in range(2):
+                wg = grp.tile([P, OH, 4], BF16, name="wg", tag="grp", align_bytes=64)
+                for half in range(2):
+                    ps = trp.tile([P, 2, 2 * P], F32, name="ps_w", tag="tr")
+                    for m0 in range(2):
+                        for o2 in range(2):
+                            nc.tensor.transpose(ps[:, m0, o2 * P:(o2 + 1) * P], words[:, 2 * half + o2, 2 * jh + m0, :], ident_f[:])
+                    nc.vector.tensor_tensor(
+                        out=wg[:, half * 256:(half + 1) * 256, :].rearrange("p o (m e) -> p o m e", e=2),
+                        in0=ps[:].bitcast(BF16).rearrange("p m (o e) -> p o m e", e=2),
+                        in1=sct[:, half * OH:(half + 1) * OH].rearrange("p (o e) -> p o e", e=2).unsqueeze(2).to_broadcast([P, 256, 2, 2]),
+                        op=ALU.mult,
+                    )
+                wc = wcp.tile([P, OH], U32, name="wc", align_bytes=64)
+                ws = wcp.tile([P, OH], U8, name="ws", align_bytes=64)
+                nc.vector.quantize_mx(out=wc[:].bitcast(FP8X4), scales=ws[:], in_=wg[:].rearrange("p o t -> p (o t)"))
+                for bt in range(NBT):
+                    nc.tensor.matmul_mx(
+                        out=acc[bt][:],
+                        lhsT=bs_codes[:, it, jh, bt * P:(bt + 1) * P].bitcast(FP8X4),
+                        lhsT_scale=bs_scales[:, it, jh, bt * P:(bt + 1) * P],
+                        rhs=wc[:].bitcast(FP8X4),
+                        rhs_scale=ws[:],
+                        start=False,
+                        stop=(it == NIT - 1 and jh == 1),
+                    )
 
-        def w_scale(wg, ps, sct, half):
-            nc.vector.tensor_tensor(
-                out=wg[:, half * 256:(half + 1) * 256, :].rearrange("p o (m e) -> p o m e", e=2),
-                in0=ps[:].bitcast(BF16).rearrange("p m (o e) -> p o m e", e=2),
-                in1=sct[:, half * OH:(half + 1) * OH].rearrange("p (o e) -> p o e", e=2).unsqueeze(2).to_broadcast([P, 256, 2, 2]),
-                op=ALU.mult,
-            )
-
-        def w_quant(wg):
-            wc = wcp.tile([P, OH], U32, name="wc", align_bytes=64)
-            ws = wcp.tile([P, OH], U8, name="ws", align_bytes=64)
-            nc.vector.quantize_mx(out=wc[:].bitcast(FP8X4), scales=ws[:], in_=wg[:].rearrange("p o t -> p (o t)"))
-            return wc, ws
-
-        def passes(acc, lhs_c, lhs_s, rhs_c, rhs_s, first, last):
-            for bt in range(NBT):
-                nc.tensor.matmul_mx(
-                    out=acc[bt][:],
-                    lhsT=lhs_c[:, bt * P:(bt + 1) * P].bitcast(FP8X4),
-                    lhsT_scale=lhs_s[:, bt * P:(bt + 1) * P],
-                    rhs=rhs_c.bitcast(FP8X4),
-                    rhs_scale=rhs_s,
-                    start=first,
-                    stop=last,
-                )
-
-        def new_acc():
+        def open_round(h):
             acc = []
             for bt in range(NBT):
                 a = accp.tile([P, OH], F32, name="acc%d" % bt)
                 acc.append(a)
-            return acc
-
-        def base_passes(acc, h):
             for g in range(2):
-                passes(acc, a_codes[:, g, :], a_scales[:, g, :], bw_codes[:, g, h, :], bw_scales[:, g, h, :], False, g == 1)
+                for bt in range(NBT):
+                    nc.tensor.matmul_mx(
+                        out=acc[bt][:],
+                        lhsT=a_codes[:, g, bt * P:(bt + 1) * P].bitcast(FP8X4),
+                        lhsT_scale=a_scales[:, g, bt * P:(bt + 1) * P],
+                        rhs=bw_codes[:, g, h, :].bitcast(FP8X4),
+                        rhs_scale=bw_scales[:, g, h, :],
+                        start=(g == 0),
+                        stop=False,
+                    )
+            return acc
 
         def close_round(h, acc):
             for bt in range(NBT):
                 o_sb = outp.tile([P, OH], F32, name="o_sb")
-                if bt % 2 == 0:
+                if bt % 2 == 0 or h == 0:
                     nc.scalar.copy(out=o_sb[:], in_=acc[bt][:])
                 else:
                     nc.vector.tensor_copy(out=o_sb[:], in_=acc[bt][:])
                 nc.sync.dma_start(out=out[bt * P:(bt + 1) * P, h * OH:(h + 1) * OH], in_=o_sb[:])
 
-        blk = {(0, 0): load_scaler(0, 0)}
-        raws = {0: load_raw(0), 1: load_raw(1)}
-        blk[(1, 0)] = load_scaler(1, 0)
-        bw_rows = {0: load_rows(base_weight, 0, "bwa")}
-        x_pair(0)
-        cube = squares(0)
-        products(0, cube)
-        sct = {0: scaler_tile(blk[(0, 0)], 0)}
-        state = clips(0, cube)
-        acc = new_acc()
-        bwg = {}
-        done = {}
-        extra = {0: ("x", 1), 2: ("x", 2), 4: ("x", 3), 1: ("b", 0, 0), 3: ("b", 0, 1), 5: ("b", 1, 0), 6: ("b", 1, 1)}
-        for n in range(NIT):
-            if n >= 1:
-                for jh in range(2):
-                    wc, ws = done[(n - 1, jh)]
-                    passes(acc, bs_codes[:, n - 1, jh, :], bs_scales[:, n - 1, jh, :], wc[:], ws[:], n == 1 and jh == 0, False)
-            b00 = w_bank(raws[n], 0, 0)
-            b01 = w_bank(raws[n], 0, 1)
-            b10 = w_bank(raws[n], 1, 0)
-            if n >= 1:
-                blk[(n - 1, 1)] = load_scaler(n - 1, 1)
-            if n + 2 < NIT:
-                blk[(n + 2, 0)] = load_scaler(n + 2, 0)
-            if n == 5:
-                bw_rows[1] = load_rows(base_weight, 1, "bwb")
-            sums_lo(n, state)
-            if n + 1 < NIT:
-                cube = squares(n + 1)
-                sct[n + 1] = scaler_tile(blk[(n + 1, 0)], n + 1)
-            sums_hi(n, state)
-            bg0 = regroup(n, 0, state["flo"])
-            if n >= 1:
-                sct[n - 1] = scaler_tile(blk[(n - 1, 1)], n - 1)
-            if n + 1 < NIT:
-                products(n + 1, cube)
-            bg1 = regroup(n, 1, state["fhi"])
-            if n in extra:
-                e = extra[n]
-                if e[0] == "x":
-                    x_pair(e[1])
-                else:
-                    if e[2] == 0:
-                        bwg[e[1]] = grp.tile([P, OH, 4], BF16, name="bwg", tag="grp", align_bytes=64)
-                    base_bank(bw_rows[0], bwg[e[1]], e[1], e[2])
-            if n in (1, 5):
-                sg = silu_group(n // 4)
-            basis_quant(n, 0, bg0)
-            wg0 = grp.tile([P, OH, 4], BF16, name="wg", tag="grp", align_bytes=64)
-            w_scale(wg0, b00, sct[n], 0)
-            w_scale(wg0, b01, sct[n], 1)
-            b11 = w_bank(raws[n], 1, 1)
-            raws[n + 2] = load_raw(n + 2)
-            done[(n, 0)] = w_quant(wg0)
-            basis_quant(n, 1, bg1)
-            wg1 = grp.tile([P, OH, 4], BF16, name="wg", tag="grp", align_bytes=64)
-            w_scale(wg1, b10, sct[n], 0)
-            w_scale(wg1, b11, sct[n], 1)
-            done[(n, 1)] = w_quant(wg1)
-            if n in (1, 5):
-                silu_quant(n // 4, sg)
-            if n in (3, 6):
-                base_quant(bwg[n // 6], n // 6, 0)
-            if n + 1 < NIT:
-                state = clips(n + 1, cube)
-        for jh in range(2):
-            wc, ws = done[(NIT - 1, jh)]
-            passes(acc, bs_codes[:, NIT - 1, jh, :], bs_scales[:, NIT - 1, jh, :], wc[:], ws[:], False, False)
-        base_passes(acc, 0)
-        blk[(NIT - 1, 1)] = load_scaler(NIT - 1, 1)
-        sct[NIT - 1] = scaler_tile(blk[(NIT - 1, 1)], NIT - 1)
-        close_round(0, acc)
-
-        acc = new_acc()
-        units = [(n, jh) for n in range(NIT) for jh in range(2)]
-        bank = {}
-
-        def lift(k, half):
-            if k < len(units):
-                n, jh = units[k]
-                bank[(k, half)] = w_bank(raws[NIT + n], jh, half)
-                if jh == 1 and half == 1 and n + 2 < NIT:
-                    raws[NIT + n + 2] = load_raw(NIT + n + 2)
-
-        lift(0, 0)
-        lift(0, 1)
-        lift(1, 0)
-        late = {2: (0, 0), 4: (0, 1), 6: (1, 0), 8: (1, 1)}
-        for k in range(len(units)):
-            n, jh = units[k]
-            wg = grp.tile([P, OH, 4], BF16, name="wg", tag="grp", align_bytes=64)
-            w_scale(wg, bank[(k, 0)], sct[n], 0)
-            lift(k + 1, 1)
-            w_scale(wg, bank[(k, 1)], sct[n], 1)
-            wc, ws = w_quant(wg)
-            passes(acc, bs_codes[:, n, jh, :], bs_scales[:, n, jh, :], wc[:], ws[:], k == 0, False)
-            lift(k + 2, 0)
-            if k in late:
-                g, half = late[k]
-                if half == 0:
-                    bwg[g] = grp.tile([P, OH, 4], BF16, name="bwg", tag="grp", align_bytes=64)
-                base_bank(bw_rows[1], bwg[g], g, half)
-                if half == 1:
-                    base_quant(bwg[g], g, 1)
-        base_passes(acc, 1)
-        close_round(1, acc)
+        cube_next = cubes(0)
+        sc0 = load_rows(spline_scaler, 0, "sca")
+        raws = {0: load_raw(0, 0)}
+        bw0 = load_rows(base_weight, 0, "bwa")
+        sct = {}
+        for it in range(NIT):
+            sct[it] = scaler_tile(sc0, it)
+        base_codes(bw0, 0)
+        acc0 = open_round(0)
+        sc1 = load_rows(spline_scaler, 1, "scb")
+        bw1 = load_rows(base_weight, 1, "bwb")
+        for it in range(NIT):
+            if it + 1 < NIT:
+                raws[it + 1] = load_raw(it + 1, 0)
+            planes = combine(it, cube_next)
+            if it + 1 < NIT:
+                cube_next = cubes(it + 1)
+            regroup(it, planes)
+            weights(it, raws[it], sct[it], acc0)
+            sct[it] = scaler_tile(sc1, it)
+            if it == 3:
+                base_codes(bw1, 1)
+        raws = {0: load_raw(0, 1)}
+        close_round(0, acc0)
+        acc1 = open_round(1)
+        for it in range(NIT):
+            if it + 1 < NIT:
+                raws[it + 1] = load_raw(it + 1, 1)
+            weights(it, raws[it], sct[it], acc1)
+        close_round(1, acc1)

@@ -21,9 +21,9 @@ NIT = IN // P
 NBT = B // P
 OH = 512
 FLOPS = 2 * B * OUT * (IN + IN * NB)
-CLIP_HI = {4: "dve", 5: "act", 6: "act", 7: "act"}
-CLIP_LO = {4: "act", 5: "act", 6: "act", 7: "dve"}
-REGROUP_ON_VECTOR = ()
+CLIP_HI = {4: "dve", 5: "dve", 6: "act", 7: "act"}
+CLIP_LO = {4: "act", 5: "act", 6: "dve", 7: "dve"}
+REGROUP_ON_VECTOR = ((1, 1), (3, 1), (5, 1), (7, 1))
 
 
 def tile_bsplinekanlayer_kernel(tc, x, base_weight, spline_weight, spline_scaler, grid, out):

@@ -21,9 +21,9 @@ NIT = IN // P
 NBT = B // P
 OH = 512
 FLOPS = 2 * B * OUT * (IN + IN * NB)
-CLIP_HI = {4: "dve", 5: "dve", 6: "act", 7: "act"}
-CLIP_LO = {4: "act", 5: "act", 6: "dve", 7: "dve"}
-REGROUP_ON_VECTOR = ((1, 1), (3, 1), (5, 1), (7, 1))
+CLIP_HI = {4: "act", 5: "act", 6: "act", 7: "act"}
+CLIP_LO = {4: "act", 5: "act", 6: "act", 7: "act"}
+REGROUP_ON_VECTOR = ()
 
 
 def tile_bsplinekanlayer_kernel(tc, x, base_weight, spline_weight, spline_scaler, grid, out):
@@ -34,7 +34,6 @@ def tile_bsplinekanlayer_kernel(tc, x, base_weight, spline_weight, spline_scaler
         stage = ctx.enter_context(tc.tile_pool(name="stage", bufs=8))
         rawp = ctx.enter_context(tc.tile_pool(name="rawp", bufs=2))
         sctp = ctx.enter_context(tc.tile_pool(name="sctp", bufs=1))
-        diagp = ctx.enter_context(tc.tile_pool(name="diagp", bufs=2))
         grp = ctx.enter_context(tc.tile_pool(name="grp", bufs=3))
         wcp = ctx.enter_context(tc.tile_pool(name="wcp", bufs=3))
         cubep = ctx.enter_context(tc.tile_pool(name="cubep", bufs=2))
@@ -59,6 +58,8 @@ def tile_bsplinekanlayer_kernel(tc, x, base_weight, spline_weight, spline_scaler
         make_identity(nc, ident_bf[:])
         ident_f = const.tile([P, P], F32)
         make_identity(nc, ident_f[:])
+        dup = const.tile([P, P, 2], BF16)
+        nc.vector.tensor_copy(out=dup[:], in_=ident_bf[:].unsqueeze(2).to_broadcast([P, P, 2]))
 
         knot = const.tile([P, NIT, NK], F32)
         nc.vector.tensor_copy(out=knot[:], in_=grid_sb[:])
@@ -91,20 +92,18 @@ def tile_bsplinekanlayer_kernel(tc, x, base_weight, spline_weight, spline_scaler
         nc.vector.reciprocal(out=inv0[:, :, 5:8], in_=mag[0][:, :, 5:8])
         beta_q = const.tile([P, NIT, NB], F32)
         nc.vector.tensor_tensor(out=beta_q[:, :, 1:4], in0=mag[3][:, :, 1:4], in1=inv4[:, :, 0:3], op=ALU.mult)
-        gam_q = const.tile([P, NIT, NB], F32)
-        nc.vector.tensor_tensor(out=gam_q[:, :, 2:4], in0=mag[2][:, :, 2:4], in1=inv4[:, :, 0:2], op=ALU.mult)
-        nc.vector.tensor_scalar_mul(out=gam_q[:, :, 2:4], in0=gam_q[:, :, 2:4], scalar1=-1.0)
         alpha_q = const.tile([P, NIT, NB], F32)
-        nc.vector.reciprocal(out=alpha_q[:, :, 2:3], in_=beta_q[:, :, 2:3])
-        nc.vector.tensor_tensor(out=alpha_q[:, :, 2:3], in0=alpha_q[:, :, 2:3], in1=gam_q[:, :, 2:3], op=ALU.mult)
+        nc.vector.reciprocal(out=alpha_q[:, :, 2:4], in_=beta_q[:, :, 2:4])
+        nc.vector.tensor_tensor(out=alpha_q[:, :, 2:4], in0=alpha_q[:, :, 2:4], in1=mag[2][:, :, 2:4], op=ALU.mult)
+        nc.vector.tensor_tensor(out=alpha_q[:, :, 2:4], in0=alpha_q[:, :, 2:4], in1=inv4[:, :, 0:2], op=ALU.mult)
+        nc.vector.tensor_scalar_mul(out=alpha_q[:, :, 2:4], in0=alpha_q[:, :, 2:4], scalar1=-1.0)
         beta_p = const.tile([P, NIT, NB], F32)
         nc.vector.tensor_tensor(out=beta_p[:, :, 4:7], in0=mag[1][:, :, 4:7], in1=inv0[:, :, 5:8], op=ALU.mult)
         nc.vector.tensor_scalar_mul(out=beta_p[:, :, 4:7], in0=beta_p[:, :, 4:7], scalar1=-1.0)
-        gam_p = const.tile([P, NIT, NB], F32)
-        nc.vector.tensor_tensor(out=gam_p[:, :, 4:6], in0=mag[2][:, :, 4:6], in1=inv0[:, :, 6:8], op=ALU.mult)
         alpha_p = const.tile([P, NIT, NB], F32)
-        nc.vector.reciprocal(out=alpha_p[:, :, 5:6], in_=beta_p[:, :, 5:6])
-        nc.vector.tensor_tensor(out=alpha_p[:, :, 5:6], in0=alpha_p[:, :, 5:6], in1=gam_p[:, :, 5:6], op=ALU.mult)
+        nc.vector.reciprocal(out=alpha_p[:, :, 4:6], in_=beta_p[:, :, 4:6])
+        nc.vector.tensor_tensor(out=alpha_p[:, :, 4:6], in0=alpha_p[:, :, 4:6], in1=mag[2][:, :, 4:6], op=ALU.mult)
+        nc.vector.tensor_tensor(out=alpha_p[:, :, 4:6], in0=alpha_p[:, :, 4:6], in1=inv0[:, :, 6:8], op=ALU.mult)
 
         xT = keep.tile([P, NIT, B], BF16)
         for pair in range(NIT // 2):
@@ -136,11 +135,11 @@ def tile_bsplinekanlayer_kernel(tc, x, base_weight, spline_weight, spline_scaler
             return tiles
 
         def scaler_tile(sc_sb, it):
-            ps = trp.tile([P, 4, P], BF16, name="ps_sc", tag="tr")
+            ps = trp.tile([P, 4, 2 * P], BF16, name="ps_sc", tag="tr")
             for oo in range(4):
-                nc.tensor.transpose(ps[:, oo, :], sc_sb[oo][:, it * P:(it + 1) * P], ident_bf[:])
+                nc.tensor.matmul(out=ps[:, oo, :], lhsT=sc_sb[oo][:, it * P:(it + 1) * P], rhs=dup[:].rearrange("p o e -> p (o e)"), start=True, stop=True)
             sct = sctp.tile([P, 2 * OH], BF16, name="sct%d" % it)
-            nc.scalar.copy(out=sct[:].rearrange("p (o e) -> p o e", e=2), in_=ps[:].rearrange("p a b -> p (a b)").unsqueeze(2).to_broadcast([P, OH, 2]))
+            nc.scalar.copy(out=sct[:], in_=ps[:].rearrange("p a b -> p (a b)"))
             return sct
 
         def base_codes(bw_sb, h):
@@ -176,17 +175,6 @@ def tile_bsplinekanlayer_kernel(tc, x, base_weight, spline_weight, spline_scaler
             else:
                 nc.gpsimd.tensor_scalar(out=o, in0=c, scalar1=s, scalar2=0.0, op0=ALU.mult, op1=ALU.max)
 
-        def three_terms(a, b_, cb, c, cc):
-            db = diagp.tile([P, P], F32, name="db")
-            nc.gpsimd.tensor_scalar(out=db[:], in0=ident_f[:], scalar1=cb, scalar2=0.0, op0=ALU.mult, op1=ALU.add)
-            dc = diagp.tile([P, P], F32, name="dc")
-            nc.gpsimd.tensor_scalar(out=dc[:], in0=ident_f[:], scalar1=cc, scalar2=0.0, op0=ALU.mult, op1=ALU.add)
-            ps = trp.tile([P, B], F32, name="ps_sum", tag="tr")
-            nc.tensor.matmul(out=ps[:], lhsT=ident_f[:], rhs=a, start=True, stop=False)
-            nc.tensor.matmul(out=ps[:], lhsT=db[:], rhs=b_, start=False, stop=False)
-            nc.tensor.matmul(out=ps[:], lhsT=dc[:], rhs=c, start=False, stop=True)
-            return ps
-
         def combine(it, cube):
             flo = planep.tile([P, 4, B], F32, name="flo")
             fhi = planep.tile([P, 4, B], F32, name="fhi")
@@ -199,8 +187,9 @@ def tile_bsplinekanlayer_kernel(tc, x, base_weight, spline_weight, spline_scaler
             fma(flo[:, 1, :], hi[4], beta_q[:, it, 1:2], hi[5])
             fma(flo[:, 2, :], hi[4], alpha_q[:, it, 2:3], hi[5])
             fma(flo[:, 2, :], flo[:, 2, :], beta_q[:, it, 2:3], hi[6])
-            s3 = three_terms(hi[7], hi[6], beta_q[:, it, 3:4], hi[5], gam_q[:, it, 3:4])
-            nc.vector.scalar_tensor_tensor(out=flo[:, 3, :], in0=cube[3][:], scalar=mag[0][:, it, 3:4], in1=s3[:], op0=ALU.mult, op1=ALU.min)
+            fma(flo[:, 3, :], hi[5], alpha_q[:, it, 3:4], hi[6])
+            fma(flo[:, 3, :], flo[:, 3, :], beta_q[:, it, 3:4], hi[7])
+            nc.vector.scalar_tensor_tensor(out=flo[:, 3, :], in0=cube[3][:], scalar=mag[0][:, it, 3:4], in1=flo[:, 3, :], op0=ALU.mult, op1=ALU.min)
             lo = {7: fhi[:, 3, :]}
             clip(CLIP_LO[7], lo[7], cube[7][:], mag[0][:, it, 7:8])
             for r in range(6, 3, -1):
@@ -209,8 +198,9 @@ def tile_bsplinekanlayer_kernel(tc, x, base_weight, spline_weight, spline_scaler
             fma(fhi[:, 2, :], lo[7], beta_p[:, it, 6:7], lo[6])
             fma(fhi[:, 1, :], lo[7], alpha_p[:, it, 5:6], lo[6])
             fma(fhi[:, 1, :], fhi[:, 1, :], beta_p[:, it, 5:6], lo[5])
-            s4 = three_terms(lo[4], lo[5], beta_p[:, it, 4:5], lo[6], gam_p[:, it, 4:5])
-            nc.vector.scalar_tensor_tensor(out=fhi[:, 0, :], in0=cube[8][:], scalar=neg_mag4[:, it, 4:5], in1=s4[:], op0=ALU.mult, op1=ALU.min)
+            fma(fhi[:, 0, :], lo[6], alpha_p[:, it, 4:5], lo[5])
+            fma(fhi[:, 0, :], fhi[:, 0, :], beta_p[:, it, 4:5], lo[4])
+            nc.vector.scalar_tensor_tensor(out=fhi[:, 0, :], in0=cube[8][:], scalar=neg_mag4[:, it, 4:5], in1=fhi[:, 0, :], op0=ALU.mult, op1=ALU.min)
             return [flo, fhi]
 
         def regroup(it, planes):

@@ -20,10 +20,8 @@ NK = 12
 NIT = IN // P
 NBT = B // P
 OH = 512
+HB = 256
 FLOPS = 2 * B * OUT * (IN + IN * NB)
-CLIP_HI = {4: "act", 5: "act", 6: "act", 7: "act"}
-CLIP_LO = {4: "act", 5: "act", 6: "act", 7: "act"}
-REGROUP_ON_VECTOR = ()
 
 
 def tile_bsplinekanlayer_kernel(tc, x, base_weight, spline_weight, spline_scaler, grid, out):
@@ -31,14 +29,15 @@ def tile_bsplinekanlayer_kernel(tc, x, base_weight, spline_weight, spline_scaler
     with ExitStack() as ctx:
         const = ctx.enter_context(tc.tile_pool(name="const", bufs=1))
         keep = ctx.enter_context(tc.tile_pool(name="keep", bufs=1))
-        stage = ctx.enter_context(tc.tile_pool(name="stage", bufs=8))
-        rawp = ctx.enter_context(tc.tile_pool(name="rawp", bufs=2))
-        sctp = ctx.enter_context(tc.tile_pool(name="sctp", bufs=1))
+        stage = ctx.enter_context(tc.tile_pool(name="stage", bufs=4))
+        scp = ctx.enter_context(tc.tile_pool(name="scp", bufs=2))
+        rawp = ctx.enter_context(tc.tile_pool(name="rawp", bufs=5))
+        sctp = ctx.enter_context(tc.tile_pool(name="sctp", bufs=2))
         grp = ctx.enter_context(tc.tile_pool(name="grp", bufs=3))
-        wcp = ctx.enter_context(tc.tile_pool(name="wcp", bufs=3))
+        bs0p = ctx.enter_context(tc.tile_pool(name="bs0p", bufs=3))
         cubep = ctx.enter_context(tc.tile_pool(name="cubep", bufs=2))
         planep = ctx.enter_context(tc.tile_pool(name="planep", bufs=2))
-        bgp = ctx.enter_context(tc.tile_pool(name="bgp", bufs=2))
+        bgp = ctx.enter_context(tc.tile_pool(name="bgp", bufs=4))
         outp = ctx.enter_context(tc.tile_pool(name="outp", bufs=2))
         accp = ctx.enter_context(tc.psum_pool(name="accp", bufs=1))
         trp = ctx.enter_context(tc.psum_pool(name="trp", bufs=4))
@@ -71,7 +70,7 @@ def tile_bsplinekanlayer_kernel(tc, x, base_weight, spline_weight, spline_scaler
             nc.vector.tensor_tensor(out=dd[:, :, 0:NK - d], in0=knot[:, :, d:NK], in1=knot[:, :, 0:NK - d], op=ALU.subtract)
             dif[d] = dd
         mag = {}
-        need = {0: (3, 8), 1: (4, 7), 2: (2, 6), 3: (1, 4), 4: (0, 5)}
+        need = {0: (4, 8), 1: (3, 7), 2: (2, 6), 3: (1, 5), 4: (0, 4)}
         for q in range(5):
             j0, j1 = need[q]
             factors = [dif[a][:, :, q - a + j0:q - a + j1] for a in range(1, q + 1)]
@@ -85,25 +84,41 @@ def tile_bsplinekanlayer_kernel(tc, x, base_weight, spline_weight, spline_scaler
             nc.vector.tensor_tensor(out=dv, in0=dv, in1=dif[4][:, :, j0:j1], op=ALU.mult)
             mag[q] = den
         neg_mag4 = const.tile([P, NIT, NB], F32)
-        nc.vector.tensor_scalar_mul(out=neg_mag4[:, :, 0:5], in0=mag[4][:, :, 0:5], scalar1=-1.0)
+        nc.vector.tensor_scalar_mul(out=neg_mag4[:, :, 0:4], in0=mag[4][:, :, 0:4], scalar1=-1.0)
         inv4 = const.tile([P, NIT, NB], F32)
         nc.vector.reciprocal(out=inv4[:, :, 0:3], in_=neg_mag4[:, :, 0:3])
         inv0 = const.tile([P, NIT, NB], F32)
         nc.vector.reciprocal(out=inv0[:, :, 5:8], in_=mag[0][:, :, 5:8])
-        beta_q = const.tile([P, NIT, NB], F32)
-        nc.vector.tensor_tensor(out=beta_q[:, :, 1:4], in0=mag[3][:, :, 1:4], in1=inv4[:, :, 0:3], op=ALU.mult)
+        c_hi = {}
+        for q, j0 in ((3, 1), (2, 2), (1, 3)):
+            n = 4 - j0
+            t = const.tile([P, NIT, NB], F32, name="chi%d" % q)
+            nc.vector.tensor_tensor(out=t[:, :, j0:4], in0=mag[q][:, :, j0:4], in1=inv4[:, :, 0:n], op=ALU.mult)
+            c_hi[q] = t
+        c_lo = {}
+        for q, j1 in ((1, 7), (2, 6), (3, 5)):
+            n = j1 - 4
+            t = const.tile([P, NIT, NB], F32, name="clo%d" % q)
+            nc.vector.tensor_tensor(out=t[:, :, 4:j1], in0=mag[q][:, :, 4:j1], in1=inv0[:, :, 4 + q:8], op=ALU.mult)
+            c_lo[q] = t
+        beta_q = c_hi[3]
         alpha_q = const.tile([P, NIT, NB], F32)
         nc.vector.reciprocal(out=alpha_q[:, :, 2:4], in_=beta_q[:, :, 2:4])
-        nc.vector.tensor_tensor(out=alpha_q[:, :, 2:4], in0=alpha_q[:, :, 2:4], in1=mag[2][:, :, 2:4], op=ALU.mult)
-        nc.vector.tensor_tensor(out=alpha_q[:, :, 2:4], in0=alpha_q[:, :, 2:4], in1=inv4[:, :, 0:2], op=ALU.mult)
+        nc.vector.tensor_tensor(out=alpha_q[:, :, 2:4], in0=alpha_q[:, :, 2:4], in1=c_hi[2][:, :, 2:4], op=ALU.mult)
         nc.vector.tensor_scalar_mul(out=alpha_q[:, :, 2:4], in0=alpha_q[:, :, 2:4], scalar1=-1.0)
+        gamma_q = const.tile([P, NIT, NB], F32)
+        nc.vector.reciprocal(out=gamma_q[:, :, 3:4], in_=c_hi[2][:, :, 3:4])
+        nc.vector.tensor_tensor(out=gamma_q[:, :, 3:4], in0=gamma_q[:, :, 3:4], in1=c_hi[1][:, :, 3:4], op=ALU.mult)
+        nc.vector.tensor_scalar_mul(out=gamma_q[:, :, 3:4], in0=gamma_q[:, :, 3:4], scalar1=-1.0)
         beta_p = const.tile([P, NIT, NB], F32)
-        nc.vector.tensor_tensor(out=beta_p[:, :, 4:7], in0=mag[1][:, :, 4:7], in1=inv0[:, :, 5:8], op=ALU.mult)
-        nc.vector.tensor_scalar_mul(out=beta_p[:, :, 4:7], in0=beta_p[:, :, 4:7], scalar1=-1.0)
+        nc.vector.tensor_scalar_mul(out=beta_p[:, :, 4:7], in0=c_lo[1][:, :, 4:7], scalar1=-1.0)
         alpha_p = const.tile([P, NIT, NB], F32)
         nc.vector.reciprocal(out=alpha_p[:, :, 4:6], in_=beta_p[:, :, 4:6])
-        nc.vector.tensor_tensor(out=alpha_p[:, :, 4:6], in0=alpha_p[:, :, 4:6], in1=mag[2][:, :, 4:6], op=ALU.mult)
-        nc.vector.tensor_tensor(out=alpha_p[:, :, 4:6], in0=alpha_p[:, :, 4:6], in1=inv0[:, :, 6:8], op=ALU.mult)
+        nc.vector.tensor_tensor(out=alpha_p[:, :, 4:6], in0=alpha_p[:, :, 4:6], in1=c_lo[2][:, :, 4:6], op=ALU.mult)
+        gamma_p = const.tile([P, NIT, NB], F32)
+        nc.vector.reciprocal(out=gamma_p[:, :, 4:5], in_=c_lo[2][:, :, 4:5])
+        nc.vector.tensor_tensor(out=gamma_p[:, :, 4:5], in0=gamma_p[:, :, 4:5], in1=c_lo[3][:, :, 4:5], op=ALU.mult)
+        nc.vector.tensor_scalar_mul(out=gamma_p[:, :, 4:5], in0=gamma_p[:, :, 4:5], scalar1=-1.0)
 
         xT = keep.tile([P, NIT, B], BF16)
         for pair in range(NIT // 2):
@@ -116,31 +131,34 @@ def tile_bsplinekanlayer_kernel(tc, x, base_weight, spline_weight, spline_scaler
 
         a_codes = keep.tile([P, 2, B], U32, align_bytes=64)
         a_scales = keep.tile([P, 2, B], U8, align_bytes=64)
-        for g in range(2):
+        bw_codes = keep.tile([P, 2, 2, OH], U32, align_bytes=64)
+        bw_scales = keep.tile([P, 2, 2, OH], U8, align_bytes=64)
+        w_codes = []
+        w_scales = []
+        b1_codes = []
+        b1_scales = []
+        for it in range(NIT):
+            wc = keep.tile([P, 2, 2, OH], U32, name="wc%d" % it, align_bytes=64)
+            ws = keep.tile([P, 2, 2, OH], U8, name="ws%d" % it, align_bytes=64)
+            bc = keep.tile([P, 2, HB], U32, name="bc%d" % it, align_bytes=64)
+            bsc = keep.tile([P, 2, HB], U8, name="bsc%d" % it, align_bytes=64)
+            w_codes.append(wc)
+            w_scales.append(ws)
+            b1_codes.append(bc)
+            b1_scales.append(bsc)
+
+        def silu_codes(g):
             sg = grp.tile([P, B, 4], BF16, name="sg", tag="grp", align_bytes=64)
             nc.scalar.activation(out=sg[:], in_=xT[:, 4 * g:4 * g + 4, :].rearrange("p t b -> p b t"), func=AF.Silu)
             nc.vector.quantize_mx(out=a_codes[:, g, :].bitcast(FP8X4), scales=a_scales[:, g, :], in_=sg[:].rearrange("p b t -> p (b t)"))
 
-        bw_codes = keep.tile([P, 2, 2, OH], U32, align_bytes=64)
-        bw_scales = keep.tile([P, 2, 2, OH], U8, align_bytes=64)
-        bs_codes = keep.tile([P, NIT, 2, B], U32, align_bytes=64)
-        bs_scales = keep.tile([P, NIT, 2, B], U8, align_bytes=64)
-
-        def load_rows(src, h, label):
+        def load_base(h):
             tiles = []
             for oo in range(4):
-                st = stage.tile([P, IN], BF16, name="%s%d" % (label, oo), tag="in2k")
-                nc.sync.dma_start(out=st[:], in_=src[(4 * h + oo) * P:(4 * h + oo + 1) * P, :])
+                st = stage.tile([P, IN], BF16, name="bw%d" % oo, tag="in2k")
+                nc.sync.dma_start(out=st[:], in_=base_weight[(4 * h + oo) * P:(4 * h + oo + 1) * P, :])
                 tiles.append(st)
             return tiles
-
-        def scaler_tile(sc_sb, it):
-            ps = trp.tile([P, 4, 2 * P], BF16, name="ps_sc", tag="tr")
-            for oo in range(4):
-                nc.tensor.matmul(out=ps[:, oo, :], lhsT=sc_sb[oo][:, it * P:(it + 1) * P], rhs=dup[:].rearrange("p o e -> p (o e)"), start=True, stop=True)
-            sct = sctp.tile([P, 2 * OH], BF16, name="sct%d" % it)
-            nc.scalar.copy(out=sct[:], in_=ps[:].rearrange("p a b -> p (a b)"))
-            return sct
 
         def base_codes(bw_sb, h):
             for g in range(2):
@@ -153,155 +171,209 @@ def tile_bsplinekanlayer_kernel(tc, x, base_weight, spline_weight, spline_scaler
                     nc.scalar.copy(out=bwg[:, half * 256:(half + 1) * 256, :], in_=ps[:].rearrange("p t o -> p o t"))
                 nc.vector.quantize_mx(out=bw_codes[:, g, h, :].bitcast(FP8X4), scales=bw_scales[:, g, h, :], in_=bwg[:].rearrange("p o t -> p (o t)"))
 
+        sc_view = spline_scaler.rearrange("(t p) i -> p t i", p=P)
+
+        def load_scaler(quarter):
+            st = scp.tile([P, 8, 256], BF16, name="sc")
+            nc.sync.dma_start(out=st[:], in_=sc_view[:, :, quarter * 256:(quarter + 1) * 256])
+            return st
+
+        def scaler_tile(sc_sb, it, h):
+            ps = trp.tile([P, 4, 2 * P], BF16, name="ps_sc", tag="tr")
+            for oo in range(4):
+                nc.tensor.matmul(out=ps[:, oo, :], lhsT=sc_sb[:, 4 * h + oo, (it % 2) * P:(it % 2 + 1) * P], rhs=dup[:].rearrange("p o e -> p (o e)"), start=True, stop=True)
+            sct = sctp.tile([P, 2 * OH], BF16, name="sct%d" % h)
+            nc.scalar.copy(out=sct[:], in_=ps[:].rearrange("p a b -> p (a b)"))
+            return sct
+
         def fma(o, a, s, b_):
             nc.vector.scalar_tensor_tensor(out=o, in0=a, scalar=s, in1=b_, op0=ALU.mult, op1=ALU.add)
 
-        def cubes(it):
-            v = xT[:, it, :]
+        def cubes(u):
+            it, hb = u
+            v = xT[:, it, hb * HB:(hb + 1) * HB]
             cube = {}
-            for r in range(3, 9):
-                c = cubep.tile([P, B], F32, name="cube%d" % r)
+            for r in range(4, 8):
+                c = cubep.tile([P, HB], F32, name="cube%d" % r)
                 nc.scalar.activation(out=c[:], in_=v, func=AF.Square, bias=neg_knot[:, it, r:r + 1], scale=1.0)
                 cube[r] = c
-            for r in range(3, 9):
+            for r in range(4, 8):
                 nc.vector.scalar_tensor_tensor(out=cube[r][:], in0=v, scalar=knot[:, it, r:r + 1], in1=cube[r][:], op0=ALU.subtract, op1=ALU.mult)
             return cube
 
-        def clip(where, o, c, s):
-            if where == "act":
-                nc.scalar.activation(out=o, in_=c, func=AF.Relu, scale=s)
-            elif where == "dve":
-                nc.vector.tensor_scalar(out=o, in0=c, scalar1=s, scalar2=0.0, op0=ALU.mult, op1=ALU.max)
-            else:
-                nc.gpsimd.tensor_scalar(out=o, in0=c, scalar1=s, scalar2=0.0, op0=ALU.mult, op1=ALU.max)
+        def clip(o, c, s):
+            nc.scalar.activation(out=o, in_=c, func=AF.Relu, scale=s)
 
-        def combine(it, cube):
-            flo = planep.tile([P, 4, B], F32, name="flo")
-            fhi = planep.tile([P, 4, B], F32, name="fhi")
+        def combine(u, cube):
+            it = u[0]
+            flo = planep.tile([P, 4, HB], F32, name="flo")
+            fhi = planep.tile([P, 4, HB], F32, name="fhi")
             hi = {4: flo[:, 0, :]}
             for r in range(5, 8):
-                hq = cubep.tile([P, B], F32, name="hi%d" % r)
+                hq = cubep.tile([P, HB], F32, name="hi%d" % r)
                 hi[r] = hq[:]
             for r in range(4, 8):
-                clip(CLIP_HI[r], hi[r], cube[r][:], neg_mag4[:, it, r - 4:r - 3])
-            fma(flo[:, 1, :], hi[4], beta_q[:, it, 1:2], hi[5])
-            fma(flo[:, 2, :], hi[4], alpha_q[:, it, 2:3], hi[5])
-            fma(flo[:, 2, :], flo[:, 2, :], beta_q[:, it, 2:3], hi[6])
-            fma(flo[:, 3, :], hi[5], alpha_q[:, it, 3:4], hi[6])
-            fma(flo[:, 3, :], flo[:, 3, :], beta_q[:, it, 3:4], hi[7])
-            nc.vector.scalar_tensor_tensor(out=flo[:, 3, :], in0=cube[3][:], scalar=mag[0][:, it, 3:4], in1=flo[:, 3, :], op0=ALU.mult, op1=ALU.min)
+                clip(hi[r], cube[r][:], neg_mag4[:, it, r - 4:r - 3])
             lo = {7: fhi[:, 3, :]}
-            clip(CLIP_LO[7], lo[7], cube[7][:], mag[0][:, it, 7:8])
+            clip(lo[7], cube[7][:], mag[0][:, it, 7:8])
             for r in range(6, 3, -1):
-                clip(CLIP_LO[r], cube[r][:], cube[r][:], mag[0][:, it, r:r + 1])
+                clip(cube[r][:], cube[r][:], mag[0][:, it, r:r + 1])
                 lo[r] = cube[r][:]
-            fma(fhi[:, 2, :], lo[7], beta_p[:, it, 6:7], lo[6])
-            fma(fhi[:, 1, :], lo[7], alpha_p[:, it, 5:6], lo[6])
-            fma(fhi[:, 1, :], fhi[:, 1, :], beta_p[:, it, 5:6], lo[5])
-            fma(fhi[:, 0, :], lo[6], alpha_p[:, it, 4:5], lo[5])
-            fma(fhi[:, 0, :], fhi[:, 0, :], beta_p[:, it, 4:5], lo[4])
-            nc.vector.scalar_tensor_tensor(out=fhi[:, 0, :], in0=cube[8][:], scalar=neg_mag4[:, it, 4:5], in1=fhi[:, 0, :], op0=ALU.mult, op1=ALU.min)
+            n1, n2, n3 = flo[:, 1, :], flo[:, 2, :], flo[:, 3, :]
+            n6, n5, n4 = fhi[:, 2, :], fhi[:, 1, :], fhi[:, 0, :]
+            fma(n3, hi[4], gamma_q[:, it, 3:4], hi[5])
+            fma(n2, hi[4], alpha_q[:, it, 2:3], hi[5])
+            fma(n1, hi[4], beta_q[:, it, 1:2], hi[5])
+            fma(n3, n3, alpha_q[:, it, 3:4], hi[6])
+            fma(n2, n2, beta_q[:, it, 2:3], hi[6])
+            fma(n4, lo[7], gamma_p[:, it, 4:5], lo[6])
+            fma(n3, n3, beta_q[:, it, 3:4], hi[7])
+            fma(n5, lo[7], alpha_p[:, it, 5:6], lo[6])
+            fma(n6, lo[7], beta_p[:, it, 6:7], lo[6])
+            fma(n4, n4, alpha_p[:, it, 4:5], lo[5])
+            fma(n5, n5, beta_p[:, it, 5:6], lo[5])
+            fma(n4, n4, beta_p[:, it, 4:5], lo[4])
             return [flo, fhi]
 
-        def regroup(it, planes):
+        b0 = {}
+
+        def regroup(u, planes):
+            it, hb = u
+            if hb == 0:
+                bc = bs0p.tile([P, 2, HB], U32, name="bc_now", align_bytes=64)
+                bsc = bs0p.tile([P, 2, HB], U8, name="bsc_now", align_bytes=64)
+                b0[it] = (bc, bsc)
+            else:
+                bc, bsc = b1_codes[it], b1_scales[it]
             for jh in range(2):
-                bg = bgp.tile([P, B, 4], BF16, name="bg", align_bytes=64)
-                if (it, jh) in REGROUP_ON_VECTOR:
-                    nc.vector.tensor_copy(out=bg[:], in_=planes[jh][:].rearrange("p t b -> p b t"))
-                else:
-                    nc.scalar.copy(out=bg[:], in_=planes[jh][:].rearrange("p t b -> p b t"))
-                nc.vector.quantize_mx(out=bs_codes[:, it, jh, :].bitcast(FP8X4), scales=bs_scales[:, it, jh, :], in_=bg[:].rearrange("p b t -> p (b t)"))
+                bg = bgp.tile([P, HB, 4], BF16, name="bg", align_bytes=64)
+                nc.scalar.copy(out=bg[:], in_=planes[jh][:].rearrange("p t b -> p b t"))
+                nc.vector.quantize_mx(out=bc[:, jh, :].bitcast(FP8X4), scales=bsc[:, jh, :], in_=bg[:].rearrange("p b t -> p (b t)"))
 
         sw_view = spline_weight.rearrange("(t p) i j -> p t (i j)", p=P)
 
         def load_raw(it, h):
-            raw = rawp.tile([P, 4, P * NB], BF16, name="raw")
-            nc.sync.dma_start(out=raw[:], in_=sw_view[:, 4 * h:4 * h + 4, it * P * NB:(it + 1) * P * NB])
-            return raw
+            tiles = []
+            for half in range(2):
+                raw = rawp.tile([P, 2, P * NB], BF16, name="raw")
+                nc.sync.dma_start(out=raw[:], in_=sw_view[:, 4 * h + 2 * half:4 * h + 2 * half + 2, it * P * NB:(it + 1) * P * NB])
+                tiles.append(raw)
+            return tiles
 
-        def weights(it, raw, sct, acc):
-            words = raw[:].bitcast(F32).rearrange("p t (i m) -> p t m i", m=4)
+        def weights(it, h, raw, sct):
+            words = [r[:].bitcast(F32).rearrange("p t (i m) -> p t m i", m=4) for r in raw]
             for jh in range(2):
                 wg = grp.tile([P, OH, 4], BF16, name="wg", tag="grp", align_bytes=64)
                 for half in range(2):
                     ps = trp.tile([P, 2, 2 * P], F32, name="ps_w", tag="tr")
                     for m0 in range(2):
                         for o2 in range(2):
-                            nc.tensor.transpose(ps[:, m0, o2 * P:(o2 + 1) * P], words[:, 2 * half + o2, 2 * jh + m0, :], ident_f[:])
+                            nc.tensor.transpose(ps[:, m0, o2 * P:(o2 + 1) * P], words[half][:, o2, 2 * jh + m0, :], ident_f[:])
                     nc.vector.tensor_tensor(
                         out=wg[:, half * 256:(half + 1) * 256, :].rearrange("p o (m e) -> p o m e", e=2),
                         in0=ps[:].bitcast(BF16).rearrange("p m (o e) -> p o m e", e=2),
                         in1=sct[:, half * OH:(half + 1) * OH].rearrange("p (o e) -> p o e", e=2).unsqueeze(2).to_broadcast([P, 256, 2, 2]),
                         op=ALU.mult,
                     )
-                wc = wcp.tile([P, OH], U32, name="wc", align_bytes=64)
-                ws = wcp.tile([P, OH], U8, name="ws", align_bytes=64)
-                nc.vector.quantize_mx(out=wc[:].bitcast(FP8X4), scales=ws[:], in_=wg[:].rearrange("p o t -> p (o t)"))
-                for bt in range(NBT):
-                    nc.tensor.matmul_mx(
-                        out=acc[bt][:],
-                        lhsT=bs_codes[:, it, jh, bt * P:(bt + 1) * P].bitcast(FP8X4),
-                        lhsT_scale=bs_scales[:, it, jh, bt * P:(bt + 1) * P],
-                        rhs=wc[:].bitcast(FP8X4),
-                        rhs_scale=ws[:],
-                        start=False,
-                        stop=(it == NIT - 1 and jh == 1),
-                    )
+                nc.vector.quantize_mx(out=w_codes[it][:, jh, h, :].bitcast(FP8X4), scales=w_scales[it][:, jh, h, :], in_=wg[:].rearrange("p o t -> p (o t)"))
 
-        def open_round(h):
-            acc = []
-            for bt in range(NBT):
-                a = accp.tile([P, OH], F32, name="acc%d" % bt)
-                acc.append(a)
+        acc = {}
+
+        def open_round(hb):
+            for b2 in range(2):
+                for h in range(2):
+                    acc[b2, h] = accp.tile([P, OH], F32, name="acc%d%d" % (b2, h))
+
+        def base_pass(hb, start):
             for g in range(2):
-                for bt in range(NBT):
-                    nc.tensor.matmul_mx(
-                        out=acc[bt][:],
-                        lhsT=a_codes[:, g, bt * P:(bt + 1) * P].bitcast(FP8X4),
-                        lhsT_scale=a_scales[:, g, bt * P:(bt + 1) * P],
-                        rhs=bw_codes[:, g, h, :].bitcast(FP8X4),
-                        rhs_scale=bw_scales[:, g, h, :],
-                        start=(g == 0),
-                        stop=False,
-                    )
-            return acc
+                for b2 in range(2):
+                    c0 = (2 * hb + b2) * P
+                    for h in range(2):
+                        nc.tensor.matmul_mx(
+                            out=acc[b2, h][:],
+                            lhsT=a_codes[:, g, c0:c0 + P].bitcast(FP8X4),
+                            lhsT_scale=a_scales[:, g, c0:c0 + P],
+                            rhs=bw_codes[:, g, h, :].bitcast(FP8X4),
+                            rhs_scale=bw_scales[:, g, h, :],
+                            start=(start and g == 0),
+                            stop=False,
+                        )
 
-        def close_round(h, acc):
-            for bt in range(NBT):
-                o_sb = outp.tile([P, OH], F32, name="o_sb")
-                if bt % 2 == 0 or h == 0:
-                    nc.scalar.copy(out=o_sb[:], in_=acc[bt][:])
-                else:
-                    nc.vector.tensor_copy(out=o_sb[:], in_=acc[bt][:])
-                nc.sync.dma_start(out=out[bt * P:(bt + 1) * P, h * OH:(h + 1) * OH], in_=o_sb[:])
+        def spline_pass(hb, it, start, stop):
+            bc, bsc = b0[it] if hb == 0 else (b1_codes[it], b1_scales[it])
+            for h in range(2):
+                for jh in range(2):
+                    for b2 in range(2):
+                        nc.tensor.matmul_mx(
+                            out=acc[b2, h][:],
+                            lhsT=bc[:, jh, b2 * P:(b2 + 1) * P].bitcast(FP8X4),
+                            lhsT_scale=bsc[:, jh, b2 * P:(b2 + 1) * P],
+                            rhs=w_codes[it][:, jh, h, :].bitcast(FP8X4),
+                            rhs_scale=w_scales[it][:, jh, h, :],
+                            start=(start and jh == 0),
+                            stop=(stop and jh == 1),
+                        )
 
-        cube_next = cubes(0)
-        sc0 = load_rows(spline_scaler, 0, "sca")
-        raws = {0: load_raw(0, 0)}
-        bw0 = load_rows(base_weight, 0, "bwa")
-        sct = {}
+        def close_round(hb):
+            for h in range(2):
+                for b2 in range(2):
+                    bt = 2 * hb + b2
+                    o_sb = outp.tile([P, OH], F32, name="o_sb")
+                    nc.scalar.copy(out=o_sb[:], in_=acc[b2, h][:])
+                    nc.sync.dma_start(out=out[bt * P:(bt + 1) * P, h * OH:(h + 1) * OH], in_=o_sb[:])
+
+        order = []
         for it in range(NIT):
-            sct[it] = scaler_tile(sc0, it)
-        base_codes(bw0, 0)
-        acc0 = open_round(0)
-        sc1 = load_rows(spline_scaler, 1, "scb")
-        bw1 = load_rows(base_weight, 1, "bwb")
+            order.append((it, 0))
+            if it % 2 == 1:
+                order.append((it // 2, 1))
+        second = [(it, 1) for it in range(4, NIT)]
+        order.extend(second)
+        follower = {order[n]: order[n + 1] for n in range(len(order) - 1)}
+
+        cube_next = cubes(order[0])
+        sc_sb = {0: load_scaler(0)}
+        raws = {(0, 0): load_raw(0, 0), (0, 1): load_raw(0, 1)}
+        sct = {(0, h): scaler_tile(sc_sb[0], 0, h) for h in range(2)}
+        open_round(0)
         for it in range(NIT):
+            units = [u for u in order if u == (it, 0) or (it % 2 == 1 and u == (it // 2, 1))]
+            for u in units:
+                planes = combine(u, cube_next)
+                if u in follower:
+                    cube_next = cubes(follower[u])
+                regroup(u, planes)
+            for h in range(2):
+                if it + 1 < NIT:
+                    raws[it + 1, h] = load_raw(it + 1, h)
+                weights(it, h, raws[it, h], sct[it, h])
             if it + 1 < NIT:
-                raws[it + 1] = load_raw(it + 1, 0)
-            planes = combine(it, cube_next)
-            if it + 1 < NIT:
-                cube_next = cubes(it + 1)
-            regroup(it, planes)
-            weights(it, raws[it], sct[it], acc0)
-            sct[it] = scaler_tile(sc1, it)
+                q = (it + 1) // 2
+                if q not in sc_sb:
+                    sc_sb[q] = load_scaler(q)
+                for h in range(2):
+                    sct[it + 1, h] = scaler_tile(sc_sb[q], it + 1, h)
+            spline_pass(0, it, it == 0, it == NIT - 1)
+            if it == 2:
+                bw0 = load_base(0)
             if it == 3:
+                silu_codes(0)
+                silu_codes(1)
+                base_codes(bw0, 0)
+                bw1 = load_base(1)
+            if it == 4:
                 base_codes(bw1, 1)
-        raws = {0: load_raw(0, 1)}
-        close_round(0, acc0)
-        acc1 = open_round(1)
+                base_pass(0, False)
+        close_round(0)
+
+        open_round(1)
+        base_pass(1, True)
         for it in range(NIT):
-            if it + 1 < NIT:
-                raws[it + 1] = load_raw(it + 1, 1)
-            weights(it, raws[it], sct[it], acc1)
-        close_round(1, acc1)
+            u = (it, 1)
+            if u in second:
+                planes = combine(u, cube_next)
+                if u in follower:
+                    cube_next = cubes(follower[u])
+                regroup(u, planes)
+            spline_pass(1, it, False, it == NIT - 1)
+        close_round(1)

@@ -18,37 +18,85 @@ OUT = 1024
 NB = 8
 NK = 12
 NIT = IN // P
-NBT = B // P
 OH = 512
 HB = 256
+AHEAD = 2
 FLOPS = 2 * B * OUT * (IN + IN * NB)
+
+
+def weave(*streams):
+    total = [len(s) for s in streams]
+    done = [0] * len(streams)
+    merged = []
+    for step in range(sum(total)):
+        best = None
+        for n in range(len(streams)):
+            if done[n] < total[n]:
+                due = (done[n] + 0.5) / total[n]
+                if best is None or due < best[0]:
+                    best = (due, n)
+        n = best[1]
+        merged.append(streams[n][done[n]])
+        done[n] += 1
+    return merged
 
 
 def tile_bsplinekanlayer_kernel(tc, x, base_weight, spline_weight, spline_scaler, grid, out):
     nc = tc.nc
     with ExitStack() as ctx:
         const = ctx.enter_context(tc.tile_pool(name="const", bufs=1))
-        keep = ctx.enter_context(tc.tile_pool(name="keep", bufs=1))
         stage = ctx.enter_context(tc.tile_pool(name="stage", bufs=4))
+        accp = ctx.enter_context(tc.psum_pool(name="accp", bufs=1))
+        trp = ctx.enter_context(tc.psum_pool(name="trp", bufs=3))
+        miscp = ctx.enter_context(tc.psum_pool(name="miscp", bufs=1))
+        keep = ctx.enter_context(tc.tile_pool(name="keep", bufs=1))
         scp = ctx.enter_context(tc.tile_pool(name="scp", bufs=2))
         rawp = ctx.enter_context(tc.tile_pool(name="rawp", bufs=5))
         sctp = ctx.enter_context(tc.tile_pool(name="sctp", bufs=2))
         grp = ctx.enter_context(tc.tile_pool(name="grp", bufs=3))
         bs0p = ctx.enter_context(tc.tile_pool(name="bs0p", bufs=3))
-        cubep = ctx.enter_context(tc.tile_pool(name="cubep", bufs=2))
-        planep = ctx.enter_context(tc.tile_pool(name="planep", bufs=2))
+        cubep = ctx.enter_context(tc.tile_pool(name="cubep", bufs=4))
+        hip = ctx.enter_context(tc.tile_pool(name="hip", bufs=2))
+        planep = ctx.enter_context(tc.tile_pool(name="planep", bufs=3))
         bgp = ctx.enter_context(tc.tile_pool(name="bgp", bufs=4))
-        outp = ctx.enter_context(tc.tile_pool(name="outp", bufs=2))
-        accp = ctx.enter_context(tc.psum_pool(name="accp", bufs=1))
-        trp = ctx.enter_context(tc.psum_pool(name="trp", bufs=4))
+        ctx.enter_context(tc.manual_schedule())
+
+        x_view = x.rearrange("(t p) i -> p t i", p=P)
+        sc_view = spline_scaler.rearrange("(t p) i -> p t i", p=P)
+        sw_view = spline_weight.rearrange("(t p) i j -> p t (i j)", p=P)
+
+        x_sb = {}
+        sc_sb = {}
+        raws = {}
+        base_sb = {}
+
+        def load_x(quarter):
+            x_sb[quarter] = stage.tile([P, 4, 256], BF16, name="x%d" % quarter, tag="in2k")
+            nc.sync.dma_start(out=x_sb[quarter][:], in_=x_view[:, :, quarter * 256:(quarter + 1) * 256])
+
+        def load_scaler(quarter):
+            sc_sb[quarter] = scp.tile([P, 8, 256], BF16, name="sc%d" % quarter, tag="sc")
+            nc.sync.dma_start(out=sc_sb[quarter][:], in_=sc_view[:, :, quarter * 256:(quarter + 1) * 256])
+
+        def load_raw(n):
+            it, t0 = n // 4, 2 * (n % 4)
+            raws[n] = rawp.tile([P, 2, P * NB], BF16, name="raw%d" % n, tag="raw")
+            nc.sync.dma_start(out=raws[n][:], in_=sw_view[:, t0:t0 + 2, it * P * NB:(it + 1) * P * NB])
+
+        def load_base(n):
+            base_sb[n] = stage.tile([P, IN], BF16, name="bw%d" % n, tag="in2k")
+            nc.sync.dma_start(out=base_sb[n][:], in_=base_weight[n * P:(n + 1) * P, :])
 
         grid_sb = const.tile([P, NIT, NK], BF16)
         nc.sync.dma_start(out=grid_sb[:], in_=grid.rearrange("(t p) r -> p t r", p=P))
-        x_sb = []
-        for bt in range(NBT):
-            xt = stage.tile([P, IN], BF16, name="x%d" % bt, tag="in2k")
-            nc.sync.dma_start(out=xt[:], in_=x[bt * P:(bt + 1) * P, :])
-            x_sb.append(xt)
+        load_x(0)
+        load_scaler(0)
+        load_raw(0)
+        load_x(1)
+        for n in range(1, 4):
+            load_raw(n)
+        for quarter in range(2, 4):
+            load_x(quarter)
 
         warm = const.tile([P, 2], F32)
         nc.vector.memset(warm[:, 0:1], 0.0)
@@ -60,235 +108,244 @@ def tile_bsplinekanlayer_kernel(tc, x, base_weight, spline_weight, spline_scaler
         dup = const.tile([P, P, 2], BF16)
         nc.vector.tensor_copy(out=dup[:], in_=ident_bf[:].unsqueeze(2).to_broadcast([P, P, 2]))
 
+        def tt(o, a, b_, op):
+            nc.vector.tensor_tensor(out=o, in0=a, in1=b_, op=op)
+
         knot = const.tile([P, NIT, NK], F32)
         nc.vector.tensor_copy(out=knot[:], in_=grid_sb[:])
         neg_knot = const.tile([P, NIT, NK], F32)
         nc.vector.tensor_scalar_mul(out=neg_knot[:], in0=knot[:], scalar1=-1.0)
         dif = {}
         for d in range(1, 5):
-            dd = const.tile([P, NIT, NK], F32, name="dif%d" % d)
-            nc.vector.tensor_tensor(out=dd[:, :, 0:NK - d], in0=knot[:, :, d:NK], in1=knot[:, :, 0:NK - d], op=ALU.subtract)
-            dif[d] = dd
-        mag = {}
-        need = {0: (4, 8), 1: (3, 7), 2: (2, 6), 3: (1, 5), 4: (0, 4)}
-        for q in range(5):
-            j0, j1 = need[q]
-            factors = [dif[a][:, :, q - a + j0:q - a + j1] for a in range(1, q + 1)]
-            factors.extend([dif[a][:, :, q + j0:q + j1] for a in range(1, 5 - q)])
-            den = const.tile([P, NIT, NB], F32, name="mag%d" % q)
-            dv = den[:, :, j0:j1]
-            nc.vector.tensor_tensor(out=dv, in0=factors[0], in1=factors[1], op=ALU.mult)
-            nc.vector.tensor_tensor(out=dv, in0=dv, in1=factors[2], op=ALU.mult)
-            nc.vector.tensor_tensor(out=dv, in0=dv, in1=factors[3], op=ALU.mult)
-            nc.vector.reciprocal(out=dv, in_=dv)
-            nc.vector.tensor_tensor(out=dv, in0=dv, in1=dif[4][:, :, j0:j1], op=ALU.mult)
-            mag[q] = den
-        neg_mag4 = const.tile([P, NIT, NB], F32)
-        nc.vector.tensor_scalar_mul(out=neg_mag4[:, :, 0:4], in0=mag[4][:, :, 0:4], scalar1=-1.0)
-        inv4 = const.tile([P, NIT, NB], F32)
-        nc.vector.reciprocal(out=inv4[:, :, 0:3], in_=neg_mag4[:, :, 0:3])
-        inv0 = const.tile([P, NIT, NB], F32)
-        nc.vector.reciprocal(out=inv0[:, :, 5:8], in_=mag[0][:, :, 5:8])
-        c_hi = {}
-        for q, j0 in ((3, 1), (2, 2), (1, 3)):
-            n = 4 - j0
-            t = const.tile([P, NIT, NB], F32, name="chi%d" % q)
-            nc.vector.tensor_tensor(out=t[:, :, j0:4], in0=mag[q][:, :, j0:4], in1=inv4[:, :, 0:n], op=ALU.mult)
-            c_hi[q] = t
-        c_lo = {}
-        for q, j1 in ((1, 7), (2, 6), (3, 5)):
-            n = j1 - 4
-            t = const.tile([P, NIT, NB], F32, name="clo%d" % q)
-            nc.vector.tensor_tensor(out=t[:, :, 4:j1], in0=mag[q][:, :, 4:j1], in1=inv0[:, :, 4 + q:8], op=ALU.mult)
-            c_lo[q] = t
-        beta_q = c_hi[3]
-        alpha_q = const.tile([P, NIT, NB], F32)
-        nc.vector.reciprocal(out=alpha_q[:, :, 2:4], in_=beta_q[:, :, 2:4])
-        nc.vector.tensor_tensor(out=alpha_q[:, :, 2:4], in0=alpha_q[:, :, 2:4], in1=c_hi[2][:, :, 2:4], op=ALU.mult)
-        nc.vector.tensor_scalar_mul(out=alpha_q[:, :, 2:4], in0=alpha_q[:, :, 2:4], scalar1=-1.0)
-        gamma_q = const.tile([P, NIT, NB], F32)
-        nc.vector.reciprocal(out=gamma_q[:, :, 3:4], in_=c_hi[2][:, :, 3:4])
-        nc.vector.tensor_tensor(out=gamma_q[:, :, 3:4], in0=gamma_q[:, :, 3:4], in1=c_hi[1][:, :, 3:4], op=ALU.mult)
-        nc.vector.tensor_scalar_mul(out=gamma_q[:, :, 3:4], in0=gamma_q[:, :, 3:4], scalar1=-1.0)
-        beta_p = const.tile([P, NIT, NB], F32)
-        nc.vector.tensor_scalar_mul(out=beta_p[:, :, 4:7], in0=c_lo[1][:, :, 4:7], scalar1=-1.0)
-        alpha_p = const.tile([P, NIT, NB], F32)
-        nc.vector.reciprocal(out=alpha_p[:, :, 4:6], in_=beta_p[:, :, 4:6])
-        nc.vector.tensor_tensor(out=alpha_p[:, :, 4:6], in0=alpha_p[:, :, 4:6], in1=c_lo[2][:, :, 4:6], op=ALU.mult)
-        gamma_p = const.tile([P, NIT, NB], F32)
-        nc.vector.reciprocal(out=gamma_p[:, :, 4:5], in_=c_lo[2][:, :, 4:5])
-        nc.vector.tensor_tensor(out=gamma_p[:, :, 4:5], in0=gamma_p[:, :, 4:5], in1=c_lo[3][:, :, 4:5], op=ALU.mult)
-        nc.vector.tensor_scalar_mul(out=gamma_p[:, :, 4:5], in0=gamma_p[:, :, 4:5], scalar1=-1.0)
+            dif[d] = const.tile([P, NIT, NK], F32, name="dif%d" % d)
+            tt(dif[d][:, :, 0:NK - d], knot[:, :, d:NK], knot[:, :, 0:NK - d], ALU.subtract)
+        left = {d: dif[d][:, :, 4 - d:8 - d] for d in range(1, 5)}
+        right = {d: dif[d][:, :, 4:8] for d in range(1, 5)}
+        mag = const.tile([P, NIT, 5, 4], F32)
+        part = const.tile([P, NIT, 4, 4], F32)
+        tt(part[:, :, 0, :], left[1], left[2], ALU.mult)
+        tt(part[:, :, 1, :], right[1], right[2], ALU.mult)
+        tt(part[:, :, 2, :], part[:, :, 0, :], left[3], ALU.mult)
+        tt(part[:, :, 3, :], part[:, :, 1, :], right[3], ALU.mult)
+        tt(mag[:, :, 2, :], part[:, :, 0, :], part[:, :, 1, :], ALU.mult)
+        tt(mag[:, :, 4, :], part[:, :, 2, :], left[4], ALU.mult)
+        tt(mag[:, :, 0, :], part[:, :, 3, :], right[4], ALU.mult)
+        tt(mag[:, :, 1, :], left[1], part[:, :, 3, :], ALU.mult)
+        tt(mag[:, :, 3, :], part[:, :, 2, :], right[1], ALU.mult)
+        neg_mag4 = const.tile([P, NIT, 4], F32)
+        inv = const.tile([P, NIT, 2, 4], F32)
+        of_hi = {}
+        of_lo = {}
+        for q in (3, 1, 2):
+            of_hi[q] = const.tile([P, NIT, 4], F32, name="ofhi%d" % q)
+            of_lo[q] = const.tile([P, NIT, 4], F32, name="oflo%d" % q)
+
+        def finish_coefficients():
+            nc.vector.reciprocal(out=mag[:], in_=mag[:])
+            for q in (4, 0, 3, 1, 2):
+                tt(mag[:, :, q, :], mag[:, :, q, :], dif[4][:, :, 4 - q:8 - q], ALU.mult)
+            nc.vector.tensor_scalar_mul(out=neg_mag4[:], in0=mag[:, :, 4, :], scalar1=-1.0)
+            nc.vector.reciprocal(out=inv[:, :, 0, :], in_=mag[:, :, 4, :])
+            nc.vector.reciprocal(out=inv[:, :, 1, :], in_=mag[:, :, 0, :])
+            for q in (3, 1, 2):
+                for side, factor in ((0, of_hi[q]), (1, of_lo[q])):
+                    nc.vector.scalar_tensor_tensor(out=factor[:], in0=mag[:, :, q, :], scalar=(1.0 if q == 2 else -1.0), in1=inv[:, :, side, :], op0=ALU.mult, op1=ALU.mult)
 
         xT = keep.tile([P, NIT, B], BF16)
-        for pair in range(NIT // 2):
-            ps = trp.tile([P, 2, B], BF16, name="ps_x", tag="tr")
-            for s in range(2):
-                it = 2 * pair + s
-                for bt in range(NBT):
-                    nc.tensor.transpose(ps[:, s, bt * P:(bt + 1) * P], x_sb[bt][:, it * P:(it + 1) * P], ident_bf[:])
-            nc.scalar.copy(out=xT[:, 2 * pair:2 * pair + 2, :], in_=ps[:])
-
         a_codes = keep.tile([P, 2, B], U32, align_bytes=64)
         a_scales = keep.tile([P, 2, B], U8, align_bytes=64)
         bw_codes = keep.tile([P, 2, 2, OH], U32, align_bytes=64)
         bw_scales = keep.tile([P, 2, 2, OH], U8, align_bytes=64)
         w_codes = []
         w_scales = []
-        b1_codes = []
-        b1_scales = []
+        b_codes = {}
+        b_scales = {}
         for it in range(NIT):
-            wc = keep.tile([P, 2, 2, OH], U32, name="wc%d" % it, align_bytes=64)
-            ws = keep.tile([P, 2, 2, OH], U8, name="ws%d" % it, align_bytes=64)
-            bc = keep.tile([P, 2, HB], U32, name="bc%d" % it, align_bytes=64)
-            bsc = keep.tile([P, 2, HB], U8, name="bsc%d" % it, align_bytes=64)
-            w_codes.append(wc)
-            w_scales.append(ws)
-            b1_codes.append(bc)
-            b1_scales.append(bsc)
+            w_codes.append(keep.tile([P, 2, 2, OH], U32, name="wc%d" % it, align_bytes=64))
+            w_scales.append(keep.tile([P, OH], U8, name="ws%d" % it, align_bytes=64))
+            b_codes[it, 1] = keep.tile([P, 2, HB], U32, name="bc%d" % it, align_bytes=64)
+            b_scales[it, 1] = keep.tile([P, 2, HB], U8, name="bsc%d" % it, align_bytes=64)
 
-        def silu_codes(g):
-            sg = grp.tile([P, B, 4], BF16, name="sg", tag="grp", align_bytes=64)
-            nc.scalar.activation(out=sg[:], in_=xT[:, 4 * g:4 * g + 4, :].rearrange("p t b -> p b t"), func=AF.Silu)
-            nc.vector.quantize_mx(out=a_codes[:, g, :].bitcast(FP8X4), scales=a_scales[:, g, :], in_=sg[:].rearrange("p b t -> p (b t)"))
+        def turn_x(quarter, pool, tag):
+            ps = pool.tile([P, 2, B], BF16, name="ps_x%d" % quarter, tag=tag)
+            for s in range(2):
+                for bt in range(4):
+                    nc.tensor.transpose(ps[:, s, bt * P:(bt + 1) * P], x_sb[quarter][:, bt, s * P:(s + 1) * P], ident_bf[:])
+            nc.scalar.copy(out=xT[:, 2 * quarter:2 * quarter + 2, :], in_=ps[:])
 
-        def load_base(h):
-            tiles = []
+        sg = {}
+
+        def silu(g):
+            sg[g] = grp.tile([P, B, 4], BF16, name="sg%d" % g, tag="grp", align_bytes=64)
+            nc.scalar.activation(out=sg[g][:], in_=xT[:, 4 * g:4 * g + 4, :].rearrange("p t b -> p b t"), func=AF.Silu)
+
+        def silu_quant(g):
+            nc.vector.quantize_mx(out=a_codes[:, g, :].bitcast(FP8X4), scales=a_scales[:, g, :], in_=sg[g][:].rearrange("p b t -> p (b t)"))
+
+        def base_turn(h, g, half):
+            if half == 0:
+                sg[h, g] = grp.tile([P, OH, 4], BF16, name="bwg%d%d" % (h, g), tag="grp", align_bytes=64)
+            ps = miscp.tile([P, 4, 2 * P], BF16, name="ps_bw", tag="misc")
+            for t in range(4):
+                for o2 in range(2):
+                    nc.tensor.transpose(ps[:, t, o2 * P:(o2 + 1) * P], base_sb[4 * h + 2 * half + o2][:, (4 * g + t) * P:(4 * g + t + 1) * P], ident_bf[:])
+            nc.scalar.copy(out=sg[h, g][:, half * 256:(half + 1) * 256, :], in_=ps[:].rearrange("p t o -> p o t"))
+
+        def base_quant(h, g):
+            nc.vector.quantize_mx(out=bw_codes[:, g, h, :].bitcast(FP8X4), scales=bw_scales[:, g, h, :], in_=sg[h, g][:].rearrange("p o t -> p (o t)"))
+
+        sct = {}
+        banks = {}
+        wgs = {}
+
+        def scaler_tile(it, h):
+            ps = miscp.tile([P, 4, 2 * P], BF16, name="ps_sc", tag="misc")
             for oo in range(4):
-                st = stage.tile([P, IN], BF16, name="bw%d" % oo, tag="in2k")
-                nc.sync.dma_start(out=st[:], in_=base_weight[(4 * h + oo) * P:(4 * h + oo + 1) * P, :])
-                tiles.append(st)
-            return tiles
+                nc.tensor.matmul(out=ps[:, oo, :], lhsT=sc_sb[it // 2][:, 4 * h + oo, (it % 2) * P:(it % 2 + 1) * P], rhs=dup[:].rearrange("p o e -> p (o e)"), start=True, stop=True)
+            sct[it, h] = sctp.tile([P, 2 * OH], BF16, name="sct%d_%d" % (it, h), tag="sct%d" % h)
+            nc.scalar.copy(out=sct[it, h][:], in_=ps[:].rearrange("p a b -> p (a b)"))
 
-        def base_codes(bw_sb, h):
-            for g in range(2):
-                bwg = grp.tile([P, OH, 4], BF16, name="bwg", tag="grp", align_bytes=64)
-                for half in range(2):
-                    ps = trp.tile([P, 4, 2 * P], BF16, name="ps_bw", tag="tr")
-                    for t in range(4):
-                        for o2 in range(2):
-                            nc.tensor.transpose(ps[:, t, o2 * P:(o2 + 1) * P], bw_sb[2 * half + o2][:, (4 * g + t) * P:(4 * g + t + 1) * P], ident_bf[:])
-                    nc.scalar.copy(out=bwg[:, half * 256:(half + 1) * 256, :], in_=ps[:].rearrange("p t o -> p o t"))
-                nc.vector.quantize_mx(out=bw_codes[:, g, h, :].bitcast(FP8X4), scales=bw_scales[:, g, h, :], in_=bwg[:].rearrange("p o t -> p (o t)"))
+        def turn(k):
+            it, h, jh, half = k // 8, (k // 4) % 2, (k // 2) % 2, k % 2
+            words = raws[4 * it + 2 * h + half][:].bitcast(F32).rearrange("p t (i m) -> p t m i", m=4)
+            banks[k] = trp.tile([P, 2, 2 * P], F32, name="ps_w", tag="tr")
+            for m0 in range(2):
+                for o2 in range(2):
+                    nc.tensor.transpose(banks[k][:, m0, o2 * P:(o2 + 1) * P], words[:, o2, 2 * jh + m0, :], ident_f[:])
 
-        sc_view = spline_scaler.rearrange("(t p) i -> p t i", p=P)
+        def scale_bank(k):
+            it, h, half = k // 8, (k // 4) % 2, k % 2
+            g = k // 2
+            if half == 0:
+                wgs[g] = grp.tile([P, OH, 4], BF16, name="wg%d" % g, tag="grp", align_bytes=64)
+            nc.vector.tensor_tensor(
+                out=wgs[g][:, half * 256:(half + 1) * 256, :].rearrange("p o (m e) -> p o m e", e=2),
+                in0=banks[k][:].bitcast(BF16).rearrange("p m (o e) -> p o m e", e=2),
+                in1=sct[it, h][:, half * OH:(half + 1) * OH].rearrange("p (o e) -> p o e", e=2).unsqueeze(2).to_broadcast([P, 256, 2, 2]),
+                op=ALU.mult,
+            )
 
-        def load_scaler(quarter):
-            st = scp.tile([P, 8, 256], BF16, name="sc")
-            nc.sync.dma_start(out=st[:], in_=sc_view[:, :, quarter * 256:(quarter + 1) * 256])
-            return st
+        def weight_quant(g):
+            it, h, jh = g // 4, (g // 2) % 2, g % 2
+            nc.vector.quantize_mx(out=w_codes[it][:, jh, h, :].bitcast(FP8X4), scales=w_scales[it][4 * (2 * h + jh):P, :], in_=wgs[g][:].rearrange("p o t -> p (o t)"))
 
-        def scaler_tile(sc_sb, it, h):
-            ps = trp.tile([P, 4, 2 * P], BF16, name="ps_sc", tag="tr")
-            for oo in range(4):
-                nc.tensor.matmul(out=ps[:, oo, :], lhsT=sc_sb[:, 4 * h + oo, (it % 2) * P:(it % 2 + 1) * P], rhs=dup[:].rearrange("p o e -> p (o e)"), start=True, stop=True)
-            sct = sctp.tile([P, 2 * OH], BF16, name="sct%d" % h)
-            nc.scalar.copy(out=sct[:], in_=ps[:].rearrange("p a b -> p (a b)"))
-            return sct
+        order = []
+        for it in range(NIT):
+            order.append((it, 0))
+            if it % 2 == 1:
+                order.append((it // 2, 1))
+        first_round = len(order)
+        order.extend([(it, 1) for it in range(4, NIT)])
+        cube = {}
+        hi = {}
+        lo = {}
+        planes = {}
+        grouped = {}
+        coded = set()
 
         def fma(o, a, s, b_):
             nc.vector.scalar_tensor_tensor(out=o, in0=a, scalar=s, in1=b_, op0=ALU.mult, op1=ALU.add)
 
-        def cubes(u):
-            it, hb = u
-            v = xT[:, it, hb * HB:(hb + 1) * HB]
-            cube = {}
-            for r in range(4, 8):
-                c = cubep.tile([P, HB], F32, name="cube%d" % r)
-                nc.scalar.activation(out=c[:], in_=v, func=AF.Square, bias=neg_knot[:, it, r:r + 1], scale=1.0)
-                cube[r] = c
-            for r in range(4, 8):
-                nc.vector.scalar_tensor_tensor(out=cube[r][:], in0=v, scalar=knot[:, it, r:r + 1], in1=cube[r][:], op0=ALU.subtract, op1=ALU.mult)
-            return cube
+        def square(n, r):
+            it, hb = order[n]
+            cube[n, r] = cubep.tile([P, HB], F32, name="cube%d_%d" % (n, r), tag="cube%d" % r)
+            nc.scalar.activation(out=cube[n, r][:], in_=xT[:, it, hb * HB:(hb + 1) * HB], func=AF.Square, bias=neg_knot[:, it, r:r + 1], scale=1.0)
 
-        def clip(o, c, s):
-            nc.scalar.activation(out=o, in_=c, func=AF.Relu, scale=s)
+        def make_cube(n, r):
+            it, hb = order[n]
+            nc.vector.scalar_tensor_tensor(out=cube[n, r][:], in0=xT[:, it, hb * HB:(hb + 1) * HB], scalar=knot[:, it, r:r + 1], in1=cube[n, r][:], op0=ALU.subtract, op1=ALU.mult)
 
-        def combine(u, cube):
-            it = u[0]
-            flo = planep.tile([P, 4, HB], F32, name="flo")
-            fhi = planep.tile([P, 4, HB], F32, name="fhi")
-            hi = {4: flo[:, 0, :]}
-            for r in range(5, 8):
-                hq = cubep.tile([P, HB], F32, name="hi%d" % r)
-                hi[r] = hq[:]
-            for r in range(4, 8):
-                clip(hi[r], cube[r][:], neg_mag4[:, it, r - 4:r - 3])
-            lo = {7: fhi[:, 3, :]}
-            clip(lo[7], cube[7][:], mag[0][:, it, 7:8])
-            for r in range(6, 3, -1):
-                clip(cube[r][:], cube[r][:], mag[0][:, it, r:r + 1])
-                lo[r] = cube[r][:]
-            n1, n2, n3 = flo[:, 1, :], flo[:, 2, :], flo[:, 3, :]
-            n6, n5, n4 = fhi[:, 2, :], fhi[:, 1, :], fhi[:, 0, :]
-            fma(n3, hi[4], gamma_q[:, it, 3:4], hi[5])
-            fma(n2, hi[4], alpha_q[:, it, 2:3], hi[5])
-            fma(n1, hi[4], beta_q[:, it, 1:2], hi[5])
-            fma(n3, n3, alpha_q[:, it, 3:4], hi[6])
-            fma(n2, n2, beta_q[:, it, 2:3], hi[6])
-            fma(n4, lo[7], gamma_p[:, it, 4:5], lo[6])
-            fma(n3, n3, beta_q[:, it, 3:4], hi[7])
-            fma(n5, lo[7], alpha_p[:, it, 5:6], lo[6])
-            fma(n6, lo[7], beta_p[:, it, 6:7], lo[6])
-            fma(n4, n4, alpha_p[:, it, 4:5], lo[5])
-            fma(n5, n5, beta_p[:, it, 5:6], lo[5])
-            fma(n4, n4, beta_p[:, it, 4:5], lo[4])
-            return [flo, fhi]
-
-        b0 = {}
-
-        def regroup(u, planes):
-            it, hb = u
-            if hb == 0:
-                bc = bs0p.tile([P, 2, HB], U32, name="bc_now", align_bytes=64)
-                bsc = bs0p.tile([P, 2, HB], U8, name="bsc_now", align_bytes=64)
-                b0[it] = (bc, bsc)
+        def clip_hi(n, r):
+            it = order[n][0]
+            if r == 4:
+                planes[n, 0] = planep.tile([P, 4, HB], F32, name="flo%d" % n, tag="flo")
+                hi[n, r] = planes[n, 0][:, 0, :]
             else:
-                bc, bsc = b1_codes[it], b1_scales[it]
-            for jh in range(2):
-                bg = bgp.tile([P, HB, 4], BF16, name="bg", align_bytes=64)
-                nc.scalar.copy(out=bg[:], in_=planes[jh][:].rearrange("p t b -> p b t"))
-                nc.vector.quantize_mx(out=bc[:, jh, :].bitcast(FP8X4), scales=bsc[:, jh, :], in_=bg[:].rearrange("p b t -> p (b t)"))
+                t = hip.tile([P, HB], F32, name="hi%d_%d" % (n, r), tag="hi%d" % r)
+                hi[n, r] = t[:]
+            nc.scalar.activation(out=hi[n, r], in_=cube[n, r][:], func=AF.Relu, scale=neg_mag4[:, it, r - 4:r - 3])
 
-        sw_view = spline_weight.rearrange("(t p) i j -> p t (i j)", p=P)
+        def clip_lo(n, r):
+            it = order[n][0]
+            if r == 7:
+                planes[n, 1] = planep.tile([P, 4, HB], F32, name="fhi%d" % n, tag="fhi")
+                lo[n, r] = planes[n, 1][:, 3, :]
+            else:
+                lo[n, r] = cube[n, r][:]
+            nc.scalar.activation(out=lo[n, r], in_=cube[n, r][:], func=AF.Relu, scale=mag[:, it, 0, r - 4:r - 3])
 
-        def load_raw(it, h):
-            tiles = []
-            for half in range(2):
-                raw = rawp.tile([P, 2, P * NB], BF16, name="raw")
-                nc.sync.dma_start(out=raw[:], in_=sw_view[:, 4 * h + 2 * half:4 * h + 2 * half + 2, it * P * NB:(it + 1) * P * NB])
-                tiles.append(raw)
-            return tiles
+        def combine(n):
+            it = order[n][0]
+            calls = []
 
-        def weights(it, h, raw, sct):
-            words = [r[:].bitcast(F32).rearrange("p t (i m) -> p t m i", m=4) for r in raw]
-            for jh in range(2):
-                wg = grp.tile([P, OH, 4], BF16, name="wg", tag="grp", align_bytes=64)
-                for half in range(2):
-                    ps = trp.tile([P, 2, 2 * P], F32, name="ps_w", tag="tr")
-                    for m0 in range(2):
-                        for o2 in range(2):
-                            nc.tensor.transpose(ps[:, m0, o2 * P:(o2 + 1) * P], words[half][:, o2, 2 * jh + m0, :], ident_f[:])
-                    nc.vector.tensor_tensor(
-                        out=wg[:, half * 256:(half + 1) * 256, :].rearrange("p o (m e) -> p o m e", e=2),
-                        in0=ps[:].bitcast(BF16).rearrange("p m (o e) -> p o m e", e=2),
-                        in1=sct[:, half * OH:(half + 1) * OH].rearrange("p (o e) -> p o e", e=2).unsqueeze(2).to_broadcast([P, 256, 2, 2]),
-                        op=ALU.mult,
-                    )
-                nc.vector.quantize_mx(out=w_codes[it][:, jh, h, :].bitcast(FP8X4), scales=w_scales[it][:, jh, h, :], in_=wg[:].rearrange("p o t -> p (o t)"))
+            def add(side, j, source, r, other):
+                q = r - j
+                kind = hi if side == 0 else lo
+                factor = (of_hi if side == 0 else of_lo)[q]
+                row = j - 4 * side
+
+                def call():
+                    o = planes[n, side][:, row, :]
+                    fma(o, kind[n, r], factor[:, it, r - 4:r - 3], kind[n, other] if source else o)
+                calls.append(call)
+
+            add(0, 3, True, 6, 7)
+            add(1, 4, True, 5, 4)
+            add(0, 2, True, 5, 6)
+            add(1, 5, True, 6, 5)
+            add(0, 3, False, 5, None)
+            add(1, 4, False, 6, None)
+            add(0, 2, False, 4, None)
+            add(1, 5, False, 7, None)
+            add(0, 1, True, 4, 5)
+            add(1, 6, True, 7, 6)
+            add(0, 3, False, 4, None)
+            add(1, 4, False, 7, None)
+            return calls
+
+        def regroup(n, jh):
+            grouped[n, jh] = bgp.tile([P, HB, 4], BF16, name="bg%d_%d" % (n, jh), tag="bg", align_bytes=64)
+            nc.scalar.copy(out=grouped[n, jh][:].rearrange("p (c i) t -> p c t i", i=4), in_=planes[n, jh][:].rearrange("p t (c i) -> p c t i", i=4))
+
+        def base_function_quant(n, jh):
+            it, hb = order[n]
+            if (it, hb) not in b_codes:
+                b_codes[it, hb] = bs0p.tile([P, 2, HB], U32, name="b0c%d" % it, tag="b0c", align_bytes=64)
+                b_scales[it, hb] = bs0p.tile([P, 2, HB], U8, name="b0s%d" % it, tag="b0s", align_bytes=64)
+            nc.vector.quantize_mx(out=b_codes[it, hb][:, jh, :].bitcast(FP8X4), scales=b_scales[it, hb][:, jh, :], in_=grouped[n, jh][:].rearrange("p b t -> p (b t)"))
+            if jh == 1:
+                coded.add((it, hb))
+
+        def slot(n):
+            vec = []
+            sca = []
+            if n - 1 >= 0:
+                for jh in range(2):
+                    sca.append(lambda jh=jh: regroup(n - 1, jh))
+            if 0 <= n + 1 < len(order):
+                for r in range(4, 8):
+                    sca.append(lambda r=r: clip_hi(n + 1, r))
+                for r in range(7, 3, -1):
+                    sca.append(lambda r=r: clip_lo(n + 1, r))
+            if 0 <= n + 3 < len(order):
+                for r in range(4, 8):
+                    sca.append(lambda r=r: square(n + 3, r))
+            if 0 <= n < len(order):
+                vec = combine(n)
+            if 0 <= n + 2 < len(order):
+                vec = weave(vec, [lambda r=r: make_cube(n + 2, r) for r in range(4, 8)])
+            if n - 1 >= 0:
+                at = (2 * len(vec)) // 3
+                vec = vec[:at] + [lambda: base_function_quant(n - 1, 0)] + vec[at:] + [lambda: base_function_quant(n - 1, 1)]
+            return weave(sca, vec)
 
         acc = {}
 
-        def open_round(hb):
-            for b2 in range(2):
-                for h in range(2):
-                    acc[b2, h] = accp.tile([P, OH], F32, name="acc%d%d" % (b2, h))
-
         def base_pass(hb, start):
-            for g in range(2):
-                for b2 in range(2):
-                    c0 = (2 * hb + b2) * P
-                    for h in range(2):
+            for b2 in range(2):
+                c0 = (2 * hb + b2) * P
+                for h in range(2):
+                    for g in range(2):
                         nc.tensor.matmul_mx(
                             out=acc[b2, h][:],
                             lhsT=a_codes[:, g, c0:c0 + P].bitcast(FP8X4),
@@ -300,80 +357,140 @@ def tile_bsplinekanlayer_kernel(tc, x, base_weight, spline_weight, spline_scaler
                         )
 
         def spline_pass(hb, it, start, stop):
-            bc, bsc = b0[it] if hb == 0 else (b1_codes[it], b1_scales[it])
-            for h in range(2):
-                for jh in range(2):
-                    for b2 in range(2):
+            for b2 in range(2):
+                for h in range(2):
+                    for jh in range(2):
                         nc.tensor.matmul_mx(
                             out=acc[b2, h][:],
-                            lhsT=bc[:, jh, b2 * P:(b2 + 1) * P].bitcast(FP8X4),
-                            lhsT_scale=bsc[:, jh, b2 * P:(b2 + 1) * P],
+                            lhsT=b_codes[it, hb][:, jh, b2 * P:(b2 + 1) * P].bitcast(FP8X4),
+                            lhsT_scale=b_scales[it, hb][:, jh, b2 * P:(b2 + 1) * P],
                             rhs=w_codes[it][:, jh, h, :].bitcast(FP8X4),
-                            rhs_scale=w_scales[it][:, jh, h, :],
+                            rhs_scale=w_scales[it][4 * (2 * h + jh):P, :],
                             start=(start and jh == 0),
                             stop=(stop and jh == 1),
                         )
 
+        def open_round():
+            for b2 in range(2):
+                for h in range(2):
+                    acc[b2, h] = accp.tile([P, OH], F32, name="acc%d%d" % (b2, h))
+
         def close_round(hb):
-            for h in range(2):
-                for b2 in range(2):
+            for b2 in range(2):
+                for h in range(2):
                     bt = 2 * hb + b2
-                    o_sb = outp.tile([P, OH], F32, name="o_sb")
-                    nc.scalar.copy(out=o_sb[:], in_=acc[b2, h][:])
+                    o_sb = stage.tile([P, OH], F32, name="o_sb", tag="in2k")
+                    if hb == 1 and h == 1:
+                        nc.vector.tensor_copy(out=o_sb[:], in_=acc[b2, h][:])
+                    else:
+                        nc.scalar.copy(out=o_sb[:], in_=acc[b2, h][:])
                     nc.sync.dma_start(out=out[bt * P:(bt + 1) * P, h * OH:(h + 1) * OH], in_=o_sb[:])
 
-        order = []
-        for it in range(NIT):
-            order.append((it, 0))
-            if it % 2 == 1:
-                order.append((it // 2, 1))
-        second = [(it, 1) for it in range(4, NIT)]
-        order.extend(second)
-        follower = {order[n]: order[n + 1] for n in range(len(order) - 1)}
+        open_round()
+        passed = [0]
 
-        cube_next = cubes(order[0])
-        sc_sb = {0: load_scaler(0)}
-        raws = {(0, 0): load_raw(0, 0), (0, 1): load_raw(0, 1)}
-        sct = {(0, h): scaler_tile(sc_sb[0], 0, h) for h in range(2)}
-        open_round(0)
-        for it in range(NIT):
-            units = [u for u in order if u == (it, 0) or (it % 2 == 1 and u == (it // 2, 1))]
-            for u in units:
-                planes = combine(u, cube_next)
-                if u in follower:
-                    cube_next = cubes(follower[u])
-                regroup(u, planes)
-            for h in range(2):
-                if it + 1 < NIT:
-                    raws[it + 1, h] = load_raw(it + 1, h)
-                weights(it, h, raws[it, h], sct[it, h])
-            if it + 1 < NIT:
-                q = (it + 1) // 2
-                if q not in sc_sb:
-                    sc_sb[q] = load_scaler(q)
-                for h in range(2):
-                    sct[it + 1, h] = scaler_tile(sc_sb[q], it + 1, h)
-            spline_pass(0, it, it == 0, it == NIT - 1)
-            if it == 2:
-                bw0 = load_base(0)
-            if it == 3:
-                silu_codes(0)
-                silu_codes(1)
-                base_codes(bw0, 0)
-                bw1 = load_base(1)
-            if it == 4:
-                base_codes(bw1, 1)
-                base_pass(0, False)
+        def ready_pass():
+            it = passed[0]
+            if it < NIT - 1 and (it, 0) in coded and 4 * it + 3 in quantised:
+                spline_pass(0, it, it == 0, False)
+                passed[0] = it + 1
+
+        quantised = set()
+        weight_calls = []
+
+        def bank_step(k):
+            it = k // 8
+            if k % 2 == 0 and k + 8 < 64:
+                load_raw((k + 8) // 2)
+            if k % 8 == 0 and it % 2 == 0 and it // 2 + 1 < 4:
+                load_scaler(it // 2 + 1)
+            if k % 4 == 2 and it + 1 < NIT:
+                scaler_tile(it + 1, (k // 4) % 2)
+            if k + AHEAD < 64:
+                turn(k + AHEAD)
+            if k % 4 == 0:
+                ready_pass()
+
+        def weight_step(k):
+            scale_bank(k)
+
+        def quant_step(g):
+            weight_quant(g)
+            quantised.add(g)
+
+        for k in range(64):
+            weight_calls.append(lambda k=k: (bank_step(k), scale_bank(k)))
+            if k % 2 == 0 and k > 0:
+                weight_calls.append(lambda k=k: quant_step(k // 2 - 1))
+        weight_calls.append(lambda: quant_step(31))
+
+        extra = []
+        for n in range(8):
+            extra.append(lambda n=n: load_base(n))
+        extra_turn = []
+        for g in range(2):
+            extra_turn.append(lambda g=g: silu(g))
+        for h in range(2):
+            for g in range(2):
+                for half in range(2):
+                    extra_turn.append(lambda h=h, g=g, half=half: base_turn(h, g, half))
+
+        turn_x(0, trp, "tr")
+        for r in range(4, 8):
+            square(0, r)
+        scaler_tile(0, 0)
+        for k in range(AHEAD):
+            turn(k)
+        scaler_tile(0, 1)
+        for r in range(4, 8):
+            make_cube(0, r)
+        finish_coefficients()
+        bases = []
+        for r in range(4, 8):
+            bases.append(lambda r=r: square(1, r))
+        for n in range(-1, first_round):
+            if n in (-1, 2, 5):
+                bases.append(lambda n=n: turn_x((n + 4) // 3, miscp, "misc"))
+            bases.extend(slot(n))
+
+        def base_operands(step):
+            if step < 2:
+                silu(step)
+            elif step < 4:
+                silu_quant(step - 2)
+
+        side = []
+        for n in range(4):
+            side.append(lambda n=n: load_base(n))
+        side.append(lambda: silu(0))
+        side.append(lambda: silu_quant(0))
+        side.append(lambda: silu(1))
+        side.append(lambda: silu_quant(1))
+        for h in range(2):
+            for g in range(2):
+                for half in range(2):
+                    side.append(lambda h=h, g=g, half=half: base_turn(h, g, half))
+                    if h == 0 and g == 1:
+                        side.append(lambda half=half: (load_base(4 + 2 * half), load_base(5 + 2 * half)))
+                side.append(lambda h=h, g=g: base_quant(h, g))
+        body = weave(weight_calls, bases)
+        middle = len(body) // 2
+        for call in body[:middle] + weave(body[middle:-40], side) + body[-40:]:
+            call()
+        while passed[0] < NIT - 1:
+            ready_pass()
+        base_pass(0, False)
+        for call in slot(first_round):
+            call()
+        spline_pass(0, NIT - 1, False, True)
         close_round(0)
 
-        open_round(1)
+        open_round()
         base_pass(1, True)
-        for it in range(NIT):
-            u = (it, 1)
-            if u in second:
-                planes = combine(u, cube_next)
-                if u in follower:
-                    cube_next = cubes(follower[u])
-                regroup(u, planes)
-            spline_pass(1, it, False, it == NIT - 1)
+        for it in range(4):
+            spline_pass(1, it, False, False)
+        for n in range(first_round + 1, len(order) + 1):
+            for call in slot(n):
+                call()
+            spline_pass(1, order[n - 1][0], False, n == len(order))
         close_round(1)

@@ -57,6 +57,7 @@ def tile_bsplinekanlayer_kernel(tc, x, base_weight, spline_weight, spline_scaler
         bs0p = ctx.enter_context(tc.tile_pool(name="bs0p", bufs=3))
         cubep = ctx.enter_context(tc.tile_pool(name="cubep", bufs=4))
         hip = ctx.enter_context(tc.tile_pool(name="hip", bufs=2))
+        diagp = ctx.enter_context(tc.tile_pool(name="diagp", bufs=2))
         planep = ctx.enter_context(tc.tile_pool(name="planep", bufs=3))
         bgp = ctx.enter_context(tc.tile_pool(name="bgp", bufs=4))
         ctx.enter_context(tc.manual_schedule())
@@ -174,6 +175,7 @@ def tile_bsplinekanlayer_kernel(tc, x, base_weight, spline_weight, spline_scaler
             nc.scalar.copy(out=xT[:, 2 * quarter:2 * quarter + 2, :], in_=ps[:])
 
         sg = {}
+        base_banks = {}
 
         def silu(g):
             sg[g] = grp.tile([P, B, 4], BF16, name="sg%d" % g, tag="grp", align_bytes=64)
@@ -185,25 +187,32 @@ def tile_bsplinekanlayer_kernel(tc, x, base_weight, spline_weight, spline_scaler
         def base_turn(h, g, half):
             if half == 0:
                 sg[h, g] = grp.tile([P, OH, 4], BF16, name="bwg%d%d" % (h, g), tag="grp", align_bytes=64)
-            ps = miscp.tile([P, 4, 2 * P], BF16, name="ps_bw", tag="misc")
+            ps = trp.tile([P, 4, 2 * P], BF16, name="ps_bw", tag="tr")
             for t in range(4):
                 for o2 in range(2):
                     nc.tensor.transpose(ps[:, t, o2 * P:(o2 + 1) * P], base_sb[4 * h + 2 * half + o2][:, (4 * g + t) * P:(4 * g + t + 1) * P], ident_bf[:])
-            nc.scalar.copy(out=sg[h, g][:, half * 256:(half + 1) * 256, :], in_=ps[:].rearrange("p t o -> p o t"))
+            base_banks[h, g, half] = ps
+
+        def base_copy(h, g, half):
+            nc.scalar.copy(out=sg[h, g][:, half * 256:(half + 1) * 256, :], in_=base_banks[h, g, half][:].rearrange("p t o -> p o t"))
 
         def base_quant(h, g):
             nc.vector.quantize_mx(out=bw_codes[:, g, h, :].bitcast(FP8X4), scales=bw_scales[:, g, h, :], in_=sg[h, g][:].rearrange("p o t -> p (o t)"))
 
         sct = {}
+        sc_banks = {}
         banks = {}
         wgs = {}
 
         def scaler_tile(it, h):
-            ps = miscp.tile([P, 4, 2 * P], BF16, name="ps_sc", tag="misc")
+            ps = trp.tile([P, 4, 2 * P], BF16, name="ps_sc", tag="tr")
             for oo in range(4):
                 nc.tensor.matmul(out=ps[:, oo, :], lhsT=sc_sb[it // 2][:, 4 * h + oo, (it % 2) * P:(it % 2 + 1) * P], rhs=dup[:].rearrange("p o e -> p (o e)"), start=True, stop=True)
+            sc_banks[it, h] = ps
+
+        def scaler_copy(it, h):
             sct[it, h] = sctp.tile([P, 2 * OH], BF16, name="sct%d_%d" % (it, h), tag="sct%d" % h)
-            nc.scalar.copy(out=sct[it, h][:], in_=ps[:].rearrange("p a b -> p (a b)"))
+            nc.scalar.copy(out=sct[it, h][:], in_=sc_banks[it, h][:].rearrange("p a b -> p (a b)"))
 
         def turn(k):
             it, h, jh, half = k // 8, (k // 4) % 2, (k // 2) % 2, k % 2
@@ -231,11 +240,13 @@ def tile_bsplinekanlayer_kernel(tc, x, base_weight, spline_weight, spline_scaler
 
         order = []
         for it in range(NIT):
-            order.append((it, 0))
-            if it % 2 == 1:
-                order.append((it // 2, 1))
+            order.append((it, 0, HB))
+            if it % 2 == 0 and it < NIT - 2:
+                order.append((it, HB, HB))
+        order.append((NIT - 2, HB, HB))
         first_round = len(order)
-        order.extend([(it, 1) for it in range(4, NIT)])
+        order.extend([(it, HB, HB) for it in range(1, NIT - 1, 2)])
+        order.extend([(NIT - 1, HB, P), (NIT - 1, HB + P, P)])
         cube = {}
         hi = {}
         lo = {}
@@ -247,32 +258,51 @@ def tile_bsplinekanlayer_kernel(tc, x, base_weight, spline_weight, spline_scaler
             nc.vector.scalar_tensor_tensor(out=o, in0=a, scalar=s, in1=b_, op0=ALU.mult, op1=ALU.add)
 
         def square(n, r):
-            it, hb = order[n]
-            cube[n, r] = cubep.tile([P, HB], F32, name="cube%d_%d" % (n, r), tag="cube%d" % r)
-            nc.scalar.activation(out=cube[n, r][:], in_=xT[:, it, hb * HB:(hb + 1) * HB], func=AF.Square, bias=neg_knot[:, it, r:r + 1], scale=1.0)
+            it, c0, w = order[n]
+            cube[n, r] = cubep.tile([P, w], F32, name="cube%d_%d" % (n, r), tag="cube%d" % r)
+            nc.scalar.activation(out=cube[n, r][:], in_=xT[:, it, c0:c0 + w], func=AF.Square, bias=neg_knot[:, it, r:r + 1], scale=1.0)
 
         def make_cube(n, r):
-            it, hb = order[n]
-            nc.vector.scalar_tensor_tensor(out=cube[n, r][:], in0=xT[:, it, hb * HB:(hb + 1) * HB], scalar=knot[:, it, r:r + 1], in1=cube[n, r][:], op0=ALU.subtract, op1=ALU.mult)
+            it, c0, w = order[n]
+            nc.vector.scalar_tensor_tensor(out=cube[n, r][:], in0=xT[:, it, c0:c0 + w], scalar=knot[:, it, r:r + 1], in1=cube[n, r][:], op0=ALU.subtract, op1=ALU.mult)
 
         def clip_hi(n, r):
-            it = order[n][0]
+            it, c0, w = order[n]
             if r == 4:
-                planes[n, 0] = planep.tile([P, 4, HB], F32, name="flo%d" % n, tag="flo")
+                planes[n, 0] = planep.tile([P, 4, w], F32, name="flo%d" % n, tag="flo")
                 hi[n, r] = planes[n, 0][:, 0, :]
             else:
-                t = hip.tile([P, HB], F32, name="hi%d_%d" % (n, r), tag="hi%d" % r)
+                t = hip.tile([P, w], F32, name="hi%d_%d" % (n, r), tag="hi%d" % r)
                 hi[n, r] = t[:]
             nc.scalar.activation(out=hi[n, r], in_=cube[n, r][:], func=AF.Relu, scale=neg_mag4[:, it, r - 4:r - 3])
 
         def clip_lo(n, r):
-            it = order[n][0]
+            it, c0, w = order[n]
             if r == 7:
-                planes[n, 1] = planep.tile([P, 4, HB], F32, name="fhi%d" % n, tag="fhi")
+                planes[n, 1] = planep.tile([P, 4, w], F32, name="fhi%d" % n, tag="fhi")
                 lo[n, r] = planes[n, 1][:, 3, :]
             else:
                 lo[n, r] = cube[n, r][:]
             nc.scalar.activation(out=lo[n, r], in_=cube[n, r][:], func=AF.Relu, scale=mag[:, it, 0, r - 4:r - 3])
+
+        diag = {}
+        sums = {}
+
+        def make_diag(n, r):
+            it = order[n][0]
+            if n > 0 and order[n - 1][0] == it:
+                diag[n, r] = diag[n - 1, r]
+                return
+            diag[n, r] = diagp.tile([P, P], F32, name="diag%d_%d" % (n, r), tag="diag%d" % r)
+            nc.scalar.activation(out=diag[n, r][:], in_=ident_f[:], func=AF.Copy, scale=of_hi[r - 3][:, it, r - 4:r - 3])
+
+        def sum_n3(n):
+            sums[n] = miscp.tile([P, order[n][2]], F32, name="sum%d" % n, tag="misc")
+            for r in range(4, 7):
+                nc.tensor.matmul(out=sums[n][:], lhsT=diag[n, r][:], rhs=hi[n, r], start=(r == 4), stop=(r == 6))
+
+        def finish_n3(n):
+            nc.vector.tensor_tensor(out=planes[n, 0][:, 3, :], in0=sums[n][:], in1=hi[n, 7], op=ALU.add)
 
         def combine(n):
             it = order[n][0]
@@ -289,114 +319,118 @@ def tile_bsplinekanlayer_kernel(tc, x, base_weight, spline_weight, spline_scaler
                     fma(o, kind[n, r], factor[:, it, r - 4:r - 3], kind[n, other] if source else o)
                 calls.append(call)
 
-            add(0, 3, True, 6, 7)
+            on_tensor = n < first_round
+            if on_tensor:
+                calls.append(lambda: finish_n3(n))
+            else:
+                add(0, 3, True, 6, 7)
             add(1, 4, True, 5, 4)
             add(0, 2, True, 5, 6)
             add(1, 5, True, 6, 5)
-            add(0, 3, False, 5, None)
+            if not on_tensor:
+                add(0, 3, False, 5, None)
             add(1, 4, False, 6, None)
             add(0, 2, False, 4, None)
             add(1, 5, False, 7, None)
             add(0, 1, True, 4, 5)
             add(1, 6, True, 7, 6)
-            add(0, 3, False, 4, None)
+            if not on_tensor:
+                add(0, 3, False, 4, None)
             add(1, 4, False, 7, None)
             return calls
 
         def regroup(n, jh):
-            grouped[n, jh] = bgp.tile([P, HB, 4], BF16, name="bg%d_%d" % (n, jh), tag="bg", align_bytes=64)
+            w = order[n][2]
+            grouped[n, jh] = bgp.tile([P, w, 4], BF16, name="bg%d_%d" % (n, jh), tag="bg", align_bytes=64)
             nc.scalar.copy(out=grouped[n, jh][:].rearrange("p (c i) t -> p c t i", i=4), in_=planes[n, jh][:].rearrange("p t (c i) -> p c t i", i=4))
 
         def base_function_quant(n, jh):
-            it, hb = order[n]
+            it, c0, w = order[n]
+            hb = c0 // HB
             if (it, hb) not in b_codes:
                 b_codes[it, hb] = bs0p.tile([P, 2, HB], U32, name="b0c%d" % it, tag="b0c", align_bytes=64)
                 b_scales[it, hb] = bs0p.tile([P, 2, HB], U8, name="b0s%d" % it, tag="b0s", align_bytes=64)
-            nc.vector.quantize_mx(out=b_codes[it, hb][:, jh, :].bitcast(FP8X4), scales=b_scales[it, hb][:, jh, :], in_=grouped[n, jh][:].rearrange("p b t -> p (b t)"))
+            cols = slice(c0 % HB, c0 % HB + w)
+            nc.vector.quantize_mx(out=b_codes[it, hb][:, jh, cols].bitcast(FP8X4), scales=b_scales[it, hb][:, jh, cols], in_=grouped[n, jh][:].rearrange("p b t -> p (b t)"))
             if jh == 1:
-                coded.add((it, hb))
+                for b2 in range(c0 // P, (c0 + w) // P):
+                    coded.add((it, b2))
 
         def slot(n):
-            vec = []
             sca = []
-            if n - 1 >= 0:
-                for jh in range(2):
-                    sca.append(lambda jh=jh: regroup(n - 1, jh))
             if 0 <= n + 1 < len(order):
-                for r in range(4, 8):
-                    sca.append(lambda r=r: clip_hi(n + 1, r))
-                for r in range(7, 3, -1):
-                    sca.append(lambda r=r: clip_lo(n + 1, r))
+                sca.extend([lambda r=r: clip_hi(n + 1, r) for r in range(4, 8)])
+                if n + 1 < first_round:
+                    sca.append(lambda: sum_n3(n + 1))
+            if n - 1 >= 0:
+                sca.extend([lambda jh=jh: regroup(n - 1, jh) for jh in range(2)])
+            if 0 <= n + 1 < len(order):
+                sca.extend([lambda r=r: clip_lo(n + 1, r) for r in range(7, 3, -1)])
             if 0 <= n + 3 < len(order):
-                for r in range(4, 8):
-                    sca.append(lambda r=r: square(n + 3, r))
-            if 0 <= n < len(order):
-                vec = combine(n)
+                sca.extend([lambda r=r: square(n + 3, r) for r in range(4, 8)])
+            if 0 <= n + 2 < first_round:
+                sca.extend([lambda r=r: make_diag(n + 2, r) for r in range(4, 7)])
+            vec = combine(n) if 0 <= n < len(order) else []
             if 0 <= n + 2 < len(order):
                 vec = weave(vec, [lambda r=r: make_cube(n + 2, r) for r in range(4, 8)])
             if n - 1 >= 0:
-                at = (2 * len(vec)) // 3
+                at = max(len(vec) - 3, 0)
                 vec = vec[:at] + [lambda: base_function_quant(n - 1, 0)] + vec[at:] + [lambda: base_function_quant(n - 1, 1)]
             return weave(sca, vec)
 
         acc = {}
 
-        def base_pass(hb, start):
-            for b2 in range(2):
-                c0 = (2 * hb + b2) * P
-                for h in range(2):
-                    for g in range(2):
-                        nc.tensor.matmul_mx(
-                            out=acc[b2, h][:],
-                            lhsT=a_codes[:, g, c0:c0 + P].bitcast(FP8X4),
-                            lhsT_scale=a_scales[:, g, c0:c0 + P],
-                            rhs=bw_codes[:, g, h, :].bitcast(FP8X4),
-                            rhs_scale=bw_scales[:, g, h, :],
-                            start=(start and g == 0),
-                            stop=False,
-                        )
+        def base_pass(b2, start):
+            for h in range(2):
+                for g in range(2):
+                    nc.tensor.matmul_mx(
+                        out=acc[b2, h][:],
+                        lhsT=a_codes[:, g, b2 * P:(b2 + 1) * P].bitcast(FP8X4),
+                        lhsT_scale=a_scales[:, g, b2 * P:(b2 + 1) * P],
+                        rhs=bw_codes[:, g, h, :].bitcast(FP8X4),
+                        rhs_scale=bw_scales[:, g, h, :],
+                        start=(start and g == 0),
+                        stop=False,
+                    )
 
-        def spline_pass(hb, it, start, stop):
-            for b2 in range(2):
-                for h in range(2):
-                    for jh in range(2):
-                        nc.tensor.matmul_mx(
-                            out=acc[b2, h][:],
-                            lhsT=b_codes[it, hb][:, jh, b2 * P:(b2 + 1) * P].bitcast(FP8X4),
-                            lhsT_scale=b_scales[it, hb][:, jh, b2 * P:(b2 + 1) * P],
-                            rhs=w_codes[it][:, jh, h, :].bitcast(FP8X4),
-                            rhs_scale=w_scales[it][4 * (2 * h + jh):P, :],
-                            start=(start and jh == 0),
-                            stop=(stop and jh == 1),
-                        )
+        def spline_pass(b2, it, start, stop):
+            cols = slice((b2 % 2) * P, (b2 % 2 + 1) * P)
+            for h in range(2):
+                for jh in range(2):
+                    nc.tensor.matmul_mx(
+                        out=acc[b2, h][:],
+                        lhsT=b_codes[it, b2 // 2][:, jh, cols].bitcast(FP8X4),
+                        lhsT_scale=b_scales[it, b2 // 2][:, jh, cols],
+                        rhs=w_codes[it][:, jh, h, :].bitcast(FP8X4),
+                        rhs_scale=w_scales[it][4 * (2 * h + jh):P, :],
+                        start=(start and jh == 0),
+                        stop=(stop and jh == 1),
+                    )
 
-        def open_round():
-            for b2 in range(2):
-                for h in range(2):
-                    acc[b2, h] = accp.tile([P, OH], F32, name="acc%d%d" % (b2, h))
+        def open_rows(b2):
+            for h in range(2):
+                acc[b2, h] = accp.tile([P, OH], F32, name="acc%d_%d" % (b2, h), tag="acc%d%d" % (b2 % 2, h))
 
-        def close_round(hb):
-            for b2 in range(2):
-                for h in range(2):
-                    bt = 2 * hb + b2
-                    o_sb = stage.tile([P, OH], F32, name="o_sb", tag="in2k")
-                    if hb == 1 and h == 1:
-                        nc.vector.tensor_copy(out=o_sb[:], in_=acc[b2, h][:])
-                    else:
-                        nc.scalar.copy(out=o_sb[:], in_=acc[b2, h][:])
-                    nc.sync.dma_start(out=out[bt * P:(bt + 1) * P, h * OH:(h + 1) * OH], in_=o_sb[:])
-
-        open_round()
-        passed = [0]
-
-        def ready_pass():
-            it = passed[0]
-            if it < NIT - 1 and (it, 0) in coded and 4 * it + 3 in quantised:
-                spline_pass(0, it, it == 0, False)
-                passed[0] = it + 1
+        def close_rows(b2):
+            for h in range(2):
+                o_sb = stage.tile([P, OH], F32, name="o_sb", tag="in2k")
+                if b2 == 3 and h == 1:
+                    nc.vector.tensor_copy(out=o_sb[:], in_=acc[b2, h][:])
+                else:
+                    nc.scalar.copy(out=o_sb[:], in_=acc[b2, h][:])
+                nc.sync.dma_start(out=out[b2 * P:(b2 + 1) * P, h * OH:(h + 1) * OH], in_=o_sb[:])
 
         quantised = set()
-        weight_calls = []
+        base_ready = set()
+        rows = {0: [], 1: []}
+        todo = [(it, b2) for it in range(NIT) for b2 in range(2)]
+
+        def next_pass():
+            if todo:
+                it, b2 = todo[0]
+                if (it, b2) in coded and 4 * it + 3 in quantised:
+                    todo.pop(0)
+                    spline_pass(b2, it, it == 0, False)
 
         def bank_step(k):
             it = k // 8
@@ -406,91 +440,92 @@ def tile_bsplinekanlayer_kernel(tc, x, base_weight, spline_weight, spline_scaler
                 load_scaler(it // 2 + 1)
             if k % 4 == 2 and it + 1 < NIT:
                 scaler_tile(it + 1, (k // 4) % 2)
+            if k % 4 == 3 and it + 1 < NIT:
+                scaler_copy(it + 1, (k // 4) % 2)
             if k + AHEAD < 64:
                 turn(k + AHEAD)
-            if k % 4 == 0:
-                ready_pass()
-
-        def weight_step(k):
+            if k % 2 == 1:
+                next_pass()
             scale_bank(k)
 
         def quant_step(g):
             weight_quant(g)
             quantised.add(g)
 
+        weight_calls = []
         for k in range(64):
-            weight_calls.append(lambda k=k: (bank_step(k), scale_bank(k)))
+            weight_calls.append(lambda k=k: bank_step(k))
             if k % 2 == 0 and k > 0:
                 weight_calls.append(lambda k=k: quant_step(k // 2 - 1))
         weight_calls.append(lambda: quant_step(31))
-
-        extra = []
-        for n in range(8):
-            extra.append(lambda n=n: load_base(n))
-        extra_turn = []
-        for g in range(2):
-            extra_turn.append(lambda g=g: silu(g))
-        for h in range(2):
-            for g in range(2):
-                for half in range(2):
-                    extra_turn.append(lambda h=h, g=g, half=half: base_turn(h, g, half))
 
         turn_x(0, trp, "tr")
         for r in range(4, 8):
             square(0, r)
         scaler_tile(0, 0)
+        scaler_copy(0, 0)
         for k in range(AHEAD):
             turn(k)
         scaler_tile(0, 1)
+        scaler_copy(0, 1)
         for r in range(4, 8):
             make_cube(0, r)
         finish_coefficients()
+
         bases = []
         for r in range(4, 8):
             bases.append(lambda r=r: square(1, r))
+        for n in range(2):
+            for r in range(4, 7):
+                bases.append(lambda n=n, r=r: make_diag(n, r))
         for n in range(-1, first_round):
             if n in (-1, 2, 5):
-                bases.append(lambda n=n: turn_x((n + 4) // 3, miscp, "misc"))
+                bases.append(lambda n=n: turn_x((n + 4) // 3, trp, "tr"))
             bases.extend(slot(n))
-
-        def base_operands(step):
-            if step < 2:
-                silu(step)
-            elif step < 4:
-                silu_quant(step - 2)
 
         side = []
         for n in range(4):
             side.append(lambda n=n: load_base(n))
-        side.append(lambda: silu(0))
-        side.append(lambda: silu_quant(0))
-        side.append(lambda: silu(1))
-        side.append(lambda: silu_quant(1))
+        for g in range(2):
+            side.append(lambda g=g: silu(g))
+            side.append(lambda g=g: silu_quant(g))
         for h in range(2):
             for g in range(2):
                 for half in range(2):
                     side.append(lambda h=h, g=g, half=half: base_turn(h, g, half))
+                    side.append(lambda h=h, g=g, half=half: base_copy(h, g, half))
                     if h == 0 and g == 1:
                         side.append(lambda half=half: (load_base(4 + 2 * half), load_base(5 + 2 * half)))
                 side.append(lambda h=h, g=g: base_quant(h, g))
+        for b2 in range(2):
+            open_rows(b2)
         body = weave(weight_calls, bases)
         middle = len(body) // 2
-        for call in body[:middle] + weave(body[middle:-40], side) + body[-40:]:
+        for call in body[:middle] + weave(body[middle:-20], side) + body[-20:]:
             call()
-        while passed[0] < NIT - 1:
-            ready_pass()
-        base_pass(0, False)
-        for call in slot(first_round):
+        tail = [lambda b2=b2: base_pass(b2, False) for b2 in range(2)]
+        tail.extend([lambda it=it, b2=b2: spline_pass(b2, it, False, it == NIT - 1) for it, b2 in todo])
+        for call in weave(slot(first_round), tail):
             call()
-        spline_pass(0, NIT - 1, False, True)
-        close_round(0)
+        for b2 in range(2):
+            close_rows(b2)
 
-        open_round()
-        base_pass(1, True)
-        for it in range(4):
-            spline_pass(1, it, False, False)
+        for b2 in range(2, 4):
+            open_rows(b2)
+        ready = []
+        for b2 in range(2, 4):
+            ready.append(lambda b2=b2: base_pass(b2, True))
+            ready.extend([lambda it=it, b2=b2: spline_pass(b2, it, False, False) for it in range(0, NIT, 2)])
+        done = set(range(0, NIT, 2))
         for n in range(first_round + 1, len(order) + 1):
-            for call in slot(n):
+            calls = slot(n)
+            for call in weave(calls, ready):
                 call()
-            spline_pass(1, order[n - 1][0], False, n == len(order))
-        close_round(1)
+            ready = []
+            it, c0, w = order[n - 1]
+            for b2 in range(c0 // P, (c0 + w) // P):
+                ready.append(lambda it=it, b2=b2: spline_pass(b2, it, False, it == NIT - 1))
+                if it == NIT - 1:
+                    ready.append(lambda b2=b2: close_rows(b2))
+        for call in ready:
+            call()

@@ -21,6 +21,7 @@ NIT = IN // P
 OH = 512
 HB = 256
 AHEAD = 2
+EARLY = (0, 2, 4)
 FLOPS = 2 * B * OUT * (IN + IN * NB)
 
 
@@ -241,11 +242,11 @@ def tile_bsplinekanlayer_kernel(tc, x, base_weight, spline_weight, spline_scaler
         order = []
         for it in range(NIT):
             order.append((it, 0, HB))
-            if it % 2 == 0 and it < NIT - 2:
+            if it in (0, 2):
                 order.append((it, HB, HB))
-        order.append((NIT - 2, HB, HB))
+        order.append((4, HB, HB))
         first_round = len(order)
-        order.extend([(it, HB, HB) for it in range(1, NIT - 1, 2)])
+        order.extend([(it, HB, HB) for it in (1, 3, 5, 6)])
         order.extend([(NIT - 1, HB, P), (NIT - 1, HB + P, P)])
         cube = {}
         hi = {}
@@ -479,8 +480,8 @@ def tile_bsplinekanlayer_kernel(tc, x, base_weight, spline_weight, spline_scaler
             for r in range(4, 7):
                 bases.append(lambda n=n, r=r: make_diag(n, r))
         for n in range(-1, first_round):
-            if n in (-1, 2, 5):
-                bases.append(lambda n=n: turn_x((n + 4) // 3, trp, "tr"))
+            if n in (-1, 0, 1):
+                bases.append(lambda n=n: turn_x(n + 2, trp, "tr"))
             bases.extend(slot(n))
 
         side = []
@@ -500,8 +501,8 @@ def tile_bsplinekanlayer_kernel(tc, x, base_weight, spline_weight, spline_scaler
         for b2 in range(2):
             open_rows(b2)
         body = weave(weight_calls, bases)
-        middle = len(body) // 2
-        for call in body[:middle] + weave(body[middle:-20], side) + body[-20:]:
+        begin, end = len(body) // 5, len(body) - 20
+        for call in body[:begin] + weave(body[begin:end], side) + body[end:]:
             call()
         tail = [lambda b2=b2: base_pass(b2, False) for b2 in range(2)]
         tail.extend([lambda it=it, b2=b2: spline_pass(b2, it, False, it == NIT - 1) for it, b2 in todo])
@@ -515,8 +516,8 @@ def tile_bsplinekanlayer_kernel(tc, x, base_weight, spline_weight, spline_scaler
         ready = []
         for b2 in range(2, 4):
             ready.append(lambda b2=b2: base_pass(b2, True))
-            ready.extend([lambda it=it, b2=b2: spline_pass(b2, it, False, False) for it in range(0, NIT, 2)])
-        done = set(range(0, NIT, 2))
+            ready.extend([lambda it=it, b2=b2: spline_pass(b2, it, False, False) for it in EARLY])
+        done = set(EARLY)
         for n in range(first_round + 1, len(order) + 1):
             calls = slot(n)
             for call in weave(calls, ready):

@@ -21,7 +21,10 @@ NIT = IN // P
 OH = 512
 HB = 256
 AHEAD = 2
-EARLY = (0, 2, 4)
+SHARE = 6
+EARLY = (0, 6)
+UNIT_ORDER = (0, 1, 2, 3, 4, 5, 7, 6)
+DUPLICATE_ON_TENSOR = range(6)
 FLOPS = 2 * B * OUT * (IN + IN * NB)
 
 
@@ -47,20 +50,21 @@ def tile_bsplinekanlayer_kernel(tc, x, base_weight, spline_weight, spline_scaler
     with ExitStack() as ctx:
         const = ctx.enter_context(tc.tile_pool(name="const", bufs=1))
         stage = ctx.enter_context(tc.tile_pool(name="stage", bufs=4))
-        accp = ctx.enter_context(tc.psum_pool(name="accp", bufs=1))
-        trp = ctx.enter_context(tc.psum_pool(name="trp", bufs=3))
-        miscp = ctx.enter_context(tc.psum_pool(name="miscp", bufs=1))
+        accp = ctx.enter_context(tc.psum_pool(name="accp", bufs=2))
+        trp = ctx.enter_context(tc.psum_pool(name="trp", bufs=4))
+        sump = ctx.enter_context(tc.psum_pool(name="sump", bufs=2))
         keep = ctx.enter_context(tc.tile_pool(name="keep", bufs=1))
-        scp = ctx.enter_context(tc.tile_pool(name="scp", bufs=2))
-        rawp = ctx.enter_context(tc.tile_pool(name="rawp", bufs=5))
-        sctp = ctx.enter_context(tc.tile_pool(name="sctp", bufs=2))
-        grp = ctx.enter_context(tc.tile_pool(name="grp", bufs=3))
-        bs0p = ctx.enter_context(tc.tile_pool(name="bs0p", bufs=3))
+        scp = ctx.enter_context(tc.tile_pool(name="scp", bufs=1))
+        rawp = ctx.enter_context(tc.tile_pool(name="rawp", bufs=4))
+        sctp = ctx.enter_context(tc.tile_pool(name="sctp", bufs=3))
+        grp = ctx.enter_context(tc.tile_pool(name="grp", bufs=2))
+        basep = ctx.enter_context(tc.tile_pool(name="basep", bufs=1))
+        bs0p = ctx.enter_context(tc.tile_pool(name="bs0p", bufs=2))
         cubep = ctx.enter_context(tc.tile_pool(name="cubep", bufs=4))
         hip = ctx.enter_context(tc.tile_pool(name="hip", bufs=2))
         diagp = ctx.enter_context(tc.tile_pool(name="diagp", bufs=2))
         planep = ctx.enter_context(tc.tile_pool(name="planep", bufs=3))
-        bgp = ctx.enter_context(tc.tile_pool(name="bgp", bufs=4))
+        bgp = ctx.enter_context(tc.tile_pool(name="bgp", bufs=2))
         ctx.enter_context(tc.manual_schedule())
 
         x_view = x.rearrange("(t p) i -> p t i", p=P)
@@ -107,11 +111,12 @@ def tile_bsplinekanlayer_kernel(tc, x, base_weight, spline_weight, spline_scaler
         make_identity(nc, ident_bf[:])
         ident_f = const.tile([P, P], F32)
         make_identity(nc, ident_f[:])
+
         dup = const.tile([P, P, 2], BF16)
         nc.vector.tensor_copy(out=dup[:], in_=ident_bf[:].unsqueeze(2).to_broadcast([P, P, 2]))
 
         def tt(o, a, b_, op):
-            nc.vector.tensor_tensor(out=o, in0=a, in1=b_, op=op)
+            nc.gpsimd.tensor_tensor(out=o, in0=a, in1=b_, op=op)
 
         knot = const.tile([P, NIT, NK], F32)
         nc.vector.tensor_copy(out=knot[:], in_=grid_sb[:])
@@ -142,8 +147,10 @@ def tile_bsplinekanlayer_kernel(tc, x, base_weight, spline_weight, spline_scaler
             of_hi[q] = const.tile([P, NIT, 4], F32, name="ofhi%d" % q)
             of_lo[q] = const.tile([P, NIT, 4], F32, name="oflo%d" % q)
 
-        def finish_coefficients():
+        def invert_differences():
             nc.vector.reciprocal(out=mag[:], in_=mag[:])
+
+        def finish_coefficients():
             for q in (4, 0, 3, 1, 2):
                 tt(mag[:, :, q, :], mag[:, :, q, :], dif[4][:, :, 4 - q:8 - q], ALU.mult)
             nc.vector.tensor_scalar_mul(out=neg_mag4[:], in0=mag[:, :, 4, :], scalar1=-1.0)
@@ -160,26 +167,27 @@ def tile_bsplinekanlayer_kernel(tc, x, base_weight, spline_weight, spline_scaler
         bw_scales = keep.tile([P, 2, 2, OH], U8, align_bytes=64)
         w_codes = []
         w_scales = []
-        b_codes = {}
-        b_scales = {}
         for it in range(NIT):
             w_codes.append(keep.tile([P, 2, 2, OH], U32, name="wc%d" % it, align_bytes=64))
             w_scales.append(keep.tile([P, OH], U8, name="ws%d" % it, align_bytes=64))
-            b_codes[it, 1] = keep.tile([P, 2, HB], U32, name="bc%d" % it, align_bytes=64)
-            b_scales[it, 1] = keep.tile([P, 2, HB], U8, name="bsc%d" % it, align_bytes=64)
+
+        x_banks = {}
 
         def turn_x(quarter, pool, tag):
             ps = pool.tile([P, 2, B], BF16, name="ps_x%d" % quarter, tag=tag)
             for s in range(2):
                 for bt in range(4):
                     nc.tensor.transpose(ps[:, s, bt * P:(bt + 1) * P], x_sb[quarter][:, bt, s * P:(s + 1) * P], ident_bf[:])
-            nc.scalar.copy(out=xT[:, 2 * quarter:2 * quarter + 2, :], in_=ps[:])
+            x_banks[quarter] = ps
+
+        def keep_x(quarter):
+            nc.scalar.copy(out=xT[:, 2 * quarter:2 * quarter + 2, :], in_=x_banks[quarter][:])
 
         sg = {}
         base_banks = {}
 
         def silu(g):
-            sg[g] = grp.tile([P, B, 4], BF16, name="sg%d" % g, tag="grp", align_bytes=64)
+            sg[g] = basep.tile([P, B, 4], BF16, name="sg%d" % g, tag="base", align_bytes=64)
             nc.scalar.activation(out=sg[g][:], in_=xT[:, 4 * g:4 * g + 4, :].rearrange("p t b -> p b t"), func=AF.Silu)
 
         def silu_quant(g):
@@ -187,7 +195,7 @@ def tile_bsplinekanlayer_kernel(tc, x, base_weight, spline_weight, spline_scaler
 
         def base_turn(h, g, half):
             if half == 0:
-                sg[h, g] = grp.tile([P, OH, 4], BF16, name="bwg%d%d" % (h, g), tag="grp", align_bytes=64)
+                sg[h, g] = basep.tile([P, OH, 4], BF16, name="bwg%d%d" % (h, g), tag="base", align_bytes=64)
             ps = trp.tile([P, 4, 2 * P], BF16, name="ps_bw", tag="tr")
             for t in range(4):
                 for o2 in range(2):
@@ -206,14 +214,24 @@ def tile_bsplinekanlayer_kernel(tc, x, base_weight, spline_weight, spline_scaler
         wgs = {}
 
         def scaler_tile(it, h):
-            ps = trp.tile([P, 4, 2 * P], BF16, name="ps_sc", tag="tr")
-            for oo in range(4):
-                nc.tensor.matmul(out=ps[:, oo, :], lhsT=sc_sb[it // 2][:, 4 * h + oo, (it % 2) * P:(it % 2 + 1) * P], rhs=dup[:].rearrange("p o e -> p (o e)"), start=True, stop=True)
+            cols = slice((it % 2) * P, (it % 2 + 1) * P)
+            if it in DUPLICATE_ON_TENSOR:
+                ps = trp.tile([P, 4, 2 * P], BF16, name="ps_sc", tag="tr")
+                for oo in range(4):
+                    nc.tensor.matmul(out=ps[:, oo, :], lhsT=sc_sb[it // 2][:, 4 * h + oo, cols], rhs=dup[:].rearrange("p o e -> p (o e)"), start=True, stop=True)
+            else:
+                ps = trp.tile([P, 4, P], BF16, name="ps_sc", tag="tr")
+                for oo in range(4):
+                    nc.tensor.transpose(ps[:, oo, :], sc_sb[it // 2][:, 4 * h + oo, cols], ident_bf[:])
             sc_banks[it, h] = ps
 
         def scaler_copy(it, h):
-            sct[it, h] = sctp.tile([P, 2 * OH], BF16, name="sct%d_%d" % (it, h), tag="sct%d" % h)
-            nc.scalar.copy(out=sct[it, h][:], in_=sc_banks[it, h][:].rearrange("p a b -> p (a b)"))
+            sct[it, h] = sctp.tile([P, OH, 2], BF16, name="sct%d_%d" % (it, h), tag="sct")
+            ps = sc_banks[it, h][:].rearrange("p a b -> p (a b)")
+            if it in DUPLICATE_ON_TENSOR:
+                nc.scalar.copy(out=sct[it, h][:].rearrange("p o e -> p (o e)"), in_=ps)
+            else:
+                nc.scalar.copy(out=sct[it, h][:], in_=ps.unsqueeze(2).to_broadcast([P, OH, 2]))
 
         def turn(k):
             it, h, jh, half = k // 8, (k // 4) % 2, (k // 2) % 2, k % 2
@@ -231,7 +249,7 @@ def tile_bsplinekanlayer_kernel(tc, x, base_weight, spline_weight, spline_scaler
             nc.vector.tensor_tensor(
                 out=wgs[g][:, half * 256:(half + 1) * 256, :].rearrange("p o (m e) -> p o m e", e=2),
                 in0=banks[k][:].bitcast(BF16).rearrange("p m (o e) -> p o m e", e=2),
-                in1=sct[it, h][:, half * OH:(half + 1) * OH].rearrange("p (o e) -> p o e", e=2).unsqueeze(2).to_broadcast([P, 256, 2, 2]),
+                in1=sct[it, h][:, half * 256:(half + 1) * 256, :].unsqueeze(2).to_broadcast([P, 256, 2, 2]),
                 op=ALU.mult,
             )
 
@@ -240,20 +258,22 @@ def tile_bsplinekanlayer_kernel(tc, x, base_weight, spline_weight, spline_scaler
             nc.vector.quantize_mx(out=w_codes[it][:, jh, h, :].bitcast(FP8X4), scales=w_scales[it][4 * (2 * h + jh):P, :], in_=wgs[g][:].rearrange("p o t -> p (o t)"))
 
         order = []
-        for it in range(NIT):
+        for it in UNIT_ORDER:
             order.append((it, 0, HB))
-            if it in (0, 2):
+            if it in EARLY:
                 order.append((it, HB, HB))
-        order.append((4, HB, HB))
         first_round = len(order)
-        order.extend([(it, HB, HB) for it in (1, 3, 5, 6)])
+        on_tensor_n3 = set(range(first_round))
+        on_tensor_n4 = set(range(first_round))
+        order.extend([(it, HB, HB) for it in range(NIT - 1) if it not in EARLY])
         order.extend([(NIT - 1, HB, P), (NIT - 1, HB + P, P)])
         cube = {}
         hi = {}
         lo = {}
         planes = {}
+        ends = {}
         grouped = {}
-        coded = set()
+        coded = {}
 
         def fma(o, a, s, b_):
             nc.vector.scalar_tensor_tensor(out=o, in0=a, scalar=s, in1=b_, op0=ALU.mult, op1=ALU.add)
@@ -270,8 +290,11 @@ def tile_bsplinekanlayer_kernel(tc, x, base_weight, spline_weight, spline_scaler
         def clip_hi(n, r):
             it, c0, w = order[n]
             if r == 4:
-                planes[n, 0] = planep.tile([P, 4, w], F32, name="flo%d" % n, tag="flo")
-                hi[n, r] = planes[n, 0][:, 0, :]
+                planes[n] = planep.tile([P, NB, w], F32, name="planes%d" % n, tag="planes")
+                ends[n] = hip.tile([P, 2, w], F32, name="ends%d" % n, tag="ends")
+                hi[n, r] = planes[n][:, 0, :]
+            elif r == 7:
+                hi[n, r] = ends[n][:, 0, :]
             else:
                 t = hip.tile([P, w], F32, name="hi%d_%d" % (n, r), tag="hi%d" % r)
                 hi[n, r] = t[:]
@@ -280,8 +303,9 @@ def tile_bsplinekanlayer_kernel(tc, x, base_weight, spline_weight, spline_scaler
         def clip_lo(n, r):
             it, c0, w = order[n]
             if r == 7:
-                planes[n, 1] = planep.tile([P, 4, w], F32, name="fhi%d" % n, tag="fhi")
-                lo[n, r] = planes[n, 1][:, 3, :]
+                lo[n, r] = planes[n][:, 7, :]
+            elif r == 4:
+                lo[n, r] = ends[n][:, 1, :]
             else:
                 lo[n, r] = cube[n, r][:]
             nc.scalar.activation(out=lo[n, r], in_=cube[n, r][:], func=AF.Relu, scale=mag[:, it, 0, r - 4:r - 3])
@@ -289,21 +313,27 @@ def tile_bsplinekanlayer_kernel(tc, x, base_weight, spline_weight, spline_scaler
         diag = {}
         sums = {}
 
-        def make_diag(n, r):
+        def make_diag(n, side, r):
             it = order[n][0]
-            if n > 0 and order[n - 1][0] == it:
-                diag[n, r] = diag[n - 1, r]
+            if n > 0 and (n - 1, side, r) in diag and order[n - 1][0] == it:
+                diag[n, side, r] = diag[n - 1, side, r]
                 return
-            diag[n, r] = diagp.tile([P, P], F32, name="diag%d_%d" % (n, r), tag="diag%d" % r)
-            nc.scalar.activation(out=diag[n, r][:], in_=ident_f[:], func=AF.Copy, scale=of_hi[r - 3][:, it, r - 4:r - 3])
+            diag[n, side, r] = diagp.tile([P, P], F32, name="diag%d_%d_%d" % (n, side, r), tag="diag%d_%d" % (side, r))
+            factor = of_hi[r - 3] if side == 0 else of_lo[r - 4]
+            nc.scalar.activation(out=diag[n, side, r][:], in_=ident_f[:], func=AF.Copy, scale=factor[:, it, r - 4:r - 3])
 
         def sum_n3(n):
-            sums[n] = miscp.tile([P, order[n][2]], F32, name="sum%d" % n, tag="misc")
+            sums[n] = sump.tile([P, 2, order[n][2]], F32, name="sum%d" % n, tag="sum")
             for r in range(4, 7):
-                nc.tensor.matmul(out=sums[n][:], lhsT=diag[n, r][:], rhs=hi[n, r], start=(r == 4), stop=(r == 6))
+                nc.tensor.matmul(out=sums[n][:, 0, :], lhsT=diag[n, 0, r][:], rhs=hi[n, r], start=(r == 4), stop=(r == 6))
 
-        def finish_n3(n):
-            nc.vector.tensor_tensor(out=planes[n, 0][:, 3, :], in0=sums[n][:], in1=hi[n, 7], op=ALU.add)
+        def sum_n4(n):
+            for r in range(7, 4, -1):
+                nc.tensor.matmul(out=sums[n][:, 1, :], lhsT=diag[n, 1, r][:], rhs=lo[n, r], start=(r == 7), stop=(r == 5))
+
+        def finish_sums(n):
+            last = 2 if n in on_tensor_n4 else 1
+            nc.vector.tensor_tensor(out=planes[n][:, 3:3 + last, :], in0=sums[n][:, 0:last, :], in1=ends[n][:, 0:last, :], op=ALU.add)
 
         def combine(n):
             it = order[n][0]
@@ -313,71 +343,75 @@ def tile_bsplinekanlayer_kernel(tc, x, base_weight, spline_weight, spline_scaler
                 q = r - j
                 kind = hi if side == 0 else lo
                 factor = (of_hi if side == 0 else of_lo)[q]
-                row = j - 4 * side
-
                 def call():
-                    o = planes[n, side][:, row, :]
+                    o = planes[n][:, j, :]
                     fma(o, kind[n, r], factor[:, it, r - 4:r - 3], kind[n, other] if source else o)
                 calls.append(call)
 
-            on_tensor = n < first_round
-            if on_tensor:
-                calls.append(lambda: finish_n3(n))
-            else:
+            on_tensor = n in on_tensor_n3
+            n4_on_tensor = n in on_tensor_n4
+            if not on_tensor:
                 add(0, 3, True, 6, 7)
-            add(1, 4, True, 5, 4)
+            if not n4_on_tensor:
+                add(1, 4, True, 5, 4)
             add(0, 2, True, 5, 6)
             add(1, 5, True, 6, 5)
             if not on_tensor:
                 add(0, 3, False, 5, None)
-            add(1, 4, False, 6, None)
+            if not n4_on_tensor:
+                add(1, 4, False, 6, None)
             add(0, 2, False, 4, None)
             add(1, 5, False, 7, None)
             add(0, 1, True, 4, 5)
             add(1, 6, True, 7, 6)
             if not on_tensor:
                 add(0, 3, False, 4, None)
-            add(1, 4, False, 7, None)
+            if not n4_on_tensor:
+                add(1, 4, False, 7, None)
+            if on_tensor:
+                calls.insert(2, lambda: finish_sums(n))
             return calls
 
         def regroup(n, jh):
             w = order[n][2]
-            grouped[n, jh] = bgp.tile([P, w, 4], BF16, name="bg%d_%d" % (n, jh), tag="bg", align_bytes=64)
-            nc.scalar.copy(out=grouped[n, jh][:].rearrange("p (c i) t -> p c t i", i=4), in_=planes[n, jh][:].rearrange("p t (c i) -> p c t i", i=4))
+            if jh == 0:
+                grouped[n] = bgp.tile([P, 2, w, 4], BF16, name="bg%d" % n, tag="bg", align_bytes=64)
+            nc.scalar.copy(out=grouped[n][:, jh, :, :].rearrange("p (c i) t -> p c t i", i=4), in_=planes[n][:, 4 * jh:4 * jh + 4, :].rearrange("p t (c i) -> p c t i", i=4))
 
-        def base_function_quant(n, jh):
+        def base_function_quant(n):
             it, c0, w = order[n]
-            hb = c0 // HB
-            if (it, hb) not in b_codes:
-                b_codes[it, hb] = bs0p.tile([P, 2, HB], U32, name="b0c%d" % it, tag="b0c", align_bytes=64)
-                b_scales[it, hb] = bs0p.tile([P, 2, HB], U8, name="b0s%d" % it, tag="b0s", align_bytes=64)
-            cols = slice(c0 % HB, c0 % HB + w)
-            nc.vector.quantize_mx(out=b_codes[it, hb][:, jh, cols].bitcast(FP8X4), scales=b_scales[it, hb][:, jh, cols], in_=grouped[n, jh][:].rearrange("p b t -> p (b t)"))
-            if jh == 1:
-                for b2 in range(c0 // P, (c0 + w) // P):
-                    coded.add((it, b2))
+            pool, tag = (keep, "bc%d" % n) if n < first_round else (bs0p, "late")
+            codes = pool.tile([P, 2, w], U32, name="bc%d" % n, tag=tag, align_bytes=64)
+            scales = pool.tile([P, 2, w], U8, name="bs%d" % n, tag=tag + "s", align_bytes=64)
+            nc.vector.quantize_mx(out=codes[:].rearrange("p j b -> p (j b)").bitcast(FP8X4), scales=scales[:].rearrange("p j b -> p (j b)"), in_=grouped[n][:].rearrange("p j b t -> p (j b t)"))
+            for b2 in range(c0 // P, (c0 + w) // P):
+                coded[it, b2] = (codes, scales, b2 * P - c0)
 
         def slot(n):
             sca = []
             if 0 <= n + 1 < len(order):
                 sca.extend([lambda r=r: clip_hi(n + 1, r) for r in range(4, 8)])
-                if n + 1 < first_round:
-                    sca.append(lambda: sum_n3(n + 1))
             if n - 1 >= 0:
                 sca.extend([lambda jh=jh: regroup(n - 1, jh) for jh in range(2)])
             if 0 <= n + 1 < len(order):
                 sca.extend([lambda r=r: clip_lo(n + 1, r) for r in range(7, 3, -1)])
             if 0 <= n + 3 < len(order):
                 sca.extend([lambda r=r: square(n + 3, r) for r in range(4, 8)])
-            if 0 <= n + 2 < first_round:
-                sca.extend([lambda r=r: make_diag(n + 2, r) for r in range(4, 7)])
+            if n + 2 in on_tensor_n3:
+                sca.extend([lambda r=r: make_diag(n + 2, 0, r) for r in range(4, 7)])
+                if n + 2 in on_tensor_n4:
+                    sca.extend([lambda r=r: make_diag(n + 2, 1, r) for r in range(5, 8)])
+            if n + 1 in on_tensor_n4:
+                sca.insert(min(13, len(sca)), lambda: sum_n4(n + 1))
+            if n + 1 in on_tensor_n3:
+                sca.insert(min(6, len(sca)), lambda: sum_n3(n + 1))
             vec = combine(n) if 0 <= n < len(order) else []
             if 0 <= n + 2 < len(order):
                 vec = weave(vec, [lambda r=r: make_cube(n + 2, r) for r in range(4, 8)])
+            merged = weave(sca, vec)
             if n - 1 >= 0:
-                at = max(len(vec) - 3, 0)
-                vec = vec[:at] + [lambda: base_function_quant(n - 1, 0)] + vec[at:] + [lambda: base_function_quant(n - 1, 1)]
-            return weave(sca, vec)
+                merged.append(lambda: base_function_quant(n - 1))
+            return merged
 
         acc = {}
 
@@ -395,13 +429,13 @@ def tile_bsplinekanlayer_kernel(tc, x, base_weight, spline_weight, spline_scaler
                     )
 
         def spline_pass(b2, it, start, stop):
-            cols = slice((b2 % 2) * P, (b2 % 2 + 1) * P)
+            codes, scales, c0 = coded[it, b2]
             for h in range(2):
                 for jh in range(2):
                     nc.tensor.matmul_mx(
                         out=acc[b2, h][:],
-                        lhsT=b_codes[it, b2 // 2][:, jh, cols].bitcast(FP8X4),
-                        lhsT_scale=b_scales[it, b2 // 2][:, jh, cols],
+                        lhsT=codes[:, jh, c0:c0 + P].bitcast(FP8X4),
+                        lhsT_scale=scales[:, jh, c0:c0 + P],
                         rhs=w_codes[it][:, jh, h, :].bitcast(FP8X4),
                         rhs_scale=w_scales[it][4 * (2 * h + jh):P, :],
                         start=(start and jh == 0),
@@ -409,8 +443,9 @@ def tile_bsplinekanlayer_kernel(tc, x, base_weight, spline_weight, spline_scaler
                     )
 
         def open_rows(b2):
+            pool, tag = (accp, "acc") if b2 < 2 else (trp, "tr")
             for h in range(2):
-                acc[b2, h] = accp.tile([P, OH], F32, name="acc%d_%d" % (b2, h), tag="acc%d%d" % (b2 % 2, h))
+                acc[b2, h] = pool.tile([P, OH], F32, name="acc%d_%d" % (b2, h), tag=tag)
 
         def close_rows(b2):
             for h in range(2):
@@ -424,7 +459,7 @@ def tile_bsplinekanlayer_kernel(tc, x, base_weight, spline_weight, spline_scaler
         quantised = set()
         base_ready = set()
         rows = {0: [], 1: []}
-        todo = [(it, b2) for it in range(NIT) for b2 in range(2)]
+        todo = [(it, 0) for it in range(NIT)]
 
         def next_pass():
             if todo:
@@ -435,9 +470,9 @@ def tile_bsplinekanlayer_kernel(tc, x, base_weight, spline_weight, spline_scaler
 
         def bank_step(k):
             it = k // 8
-            if k % 2 == 0 and k + 8 < 64:
-                load_raw((k + 8) // 2)
-            if k % 8 == 0 and it % 2 == 0 and it // 2 + 1 < 4:
+            if k % 2 == 1 and k + 7 < 64:
+                load_raw((k + 7) // 2)
+            if k % 16 == 7 and it // 2 + 1 < 4:
                 load_scaler(it // 2 + 1)
             if k % 4 == 2 and it + 1 < NIT:
                 scaler_tile(it + 1, (k // 4) % 2)
@@ -460,7 +495,9 @@ def tile_bsplinekanlayer_kernel(tc, x, base_weight, spline_weight, spline_scaler
                 weight_calls.append(lambda k=k: quant_step(k // 2 - 1))
         weight_calls.append(lambda: quant_step(31))
 
+        open_rows(0)
         turn_x(0, trp, "tr")
+        keep_x(0)
         for r in range(4, 8):
             square(0, r)
         scaler_tile(0, 0)
@@ -471,18 +508,27 @@ def tile_bsplinekanlayer_kernel(tc, x, base_weight, spline_weight, spline_scaler
         scaler_copy(0, 1)
         for r in range(4, 8):
             make_cube(0, r)
+        for r in range(4, 8):
+            square(1, r)
+        for call in weight_calls[:1]:
+            call()
+        invert_differences()
+        for call in weight_calls[1:4]:
+            call()
         finish_coefficients()
 
         bases = []
-        for r in range(4, 8):
-            bases.append(lambda r=r: square(1, r))
         for n in range(2):
             for r in range(4, 7):
-                bases.append(lambda n=n, r=r: make_diag(n, r))
+                bases.append(lambda n=n, r=r: make_diag(n, 0, r))
+            for r in range(5, 8):
+                bases.append(lambda n=n, r=r: make_diag(n, 1, r))
         for n in range(-1, first_round):
+            calls = slot(n)
             if n in (-1, 0, 1):
-                bases.append(lambda n=n: turn_x(n + 2, trp, "tr"))
-            bases.extend(slot(n))
+                calls.insert(len(calls) // 2, lambda n=n: turn_x(n + 2, trp, "tr"))
+                calls.append(lambda n=n: keep_x(n + 2))
+            bases.extend(calls)
 
         side = []
         for n in range(4):
@@ -498,35 +544,32 @@ def tile_bsplinekanlayer_kernel(tc, x, base_weight, spline_weight, spline_scaler
                     if h == 0 and g == 1:
                         side.append(lambda half=half: (load_base(4 + 2 * half), load_base(5 + 2 * half)))
                 side.append(lambda h=h, g=g: base_quant(h, g))
-        for b2 in range(2):
-            open_rows(b2)
-        body = weave(weight_calls, bases)
+        body = weave(weight_calls[4:], bases)
         begin, end = len(body) // 5, len(body) - 20
         for call in body[:begin] + weave(body[begin:end], side) + body[end:]:
             call()
-        tail = [lambda b2=b2: base_pass(b2, False) for b2 in range(2)]
-        tail.extend([lambda it=it, b2=b2: spline_pass(b2, it, False, it == NIT - 1) for it, b2 in todo])
-        for call in weave(slot(first_round), tail):
-            call()
-        for b2 in range(2):
-            close_rows(b2)
 
-        for b2 in range(2, 4):
-            open_rows(b2)
-        ready = []
-        for b2 in range(2, 4):
-            ready.append(lambda b2=b2: base_pass(b2, True))
-            ready.extend([lambda it=it, b2=b2: spline_pass(b2, it, False, False) for it in EARLY])
-        done = set(EARLY)
-        for n in range(first_round + 1, len(order) + 1):
+        ready = [lambda: base_pass(0, False)]
+        ready.extend([lambda it=it, b2=b2: spline_pass(b2, it, False, it == NIT - 1) for it, b2 in todo])
+        ready.append(lambda: close_rows(0))
+        ready.append(lambda: (open_rows(1), base_pass(1, True)))
+        ready.extend([lambda it=it: spline_pass(1, it, False, it == NIT - 1) for it in range(NIT)])
+        ready.append(lambda: close_rows(1))
+        ready.extend([lambda b2=b2: (open_rows(b2), base_pass(b2, True)) for b2 in range(2, 4)])
+        ready.extend([lambda it=it, b2=b2: spline_pass(b2, it, False, False) for it in EARLY for b2 in range(2, 4)])
+        behind = len(ready)
+        share = SHARE
+        for n in range(first_round, len(order) + 1):
             calls = slot(n)
-            for call in weave(calls, ready):
+            now = ready[:share]
+            ready = ready[share:]
+            for call in weave(calls, now):
                 call()
-            ready = []
-            it, c0, w = order[n - 1]
-            for b2 in range(c0 // P, (c0 + w) // P):
-                ready.append(lambda it=it, b2=b2: spline_pass(b2, it, False, it == NIT - 1))
-                if it == NIT - 1:
-                    ready.append(lambda b2=b2: close_rows(b2))
+            if n > first_round:
+                it, c0, w = order[n - 1]
+                for b2 in range(c0 // P, (c0 + w) // P):
+                    ready.append(lambda it=it, b2=b2: spline_pass(b2, it, False, it == NIT - 1))
+                    if it == NIT - 1:
+                        ready.append(lambda b2=b2: close_rows(b2))
         for call in ready:
             call()

@@ -21,10 +21,10 @@ NIT = IN // P
 OH = 512
 HB = 256
 AHEAD = 2
-SHARE = 6
-EARLY = (0, 6)
+SHARE = 20
+EARLY = (0,)
 UNIT_ORDER = (0, 1, 2, 3, 4, 5, 7, 6)
-DUPLICATE_ON_TENSOR = range(6)
+DUPLICATE_ON_TENSOR = range(5)
 FLOPS = 2 * B * OUT * (IN + IN * NB)
 
 
@@ -141,6 +141,7 @@ def tile_bsplinekanlayer_kernel(tc, x, base_weight, spline_weight, spline_scaler
         tt(mag[:, :, 3, :], part[:, :, 2, :], right[1], ALU.mult)
         neg_mag4 = const.tile([P, NIT, 4], F32)
         inv = const.tile([P, NIT, 2, 4], F32)
+        neg_inv = const.tile([P, NIT, 2, 4], F32)
         of_hi = {}
         of_lo = {}
         for q in (3, 1, 2):
@@ -153,12 +154,13 @@ def tile_bsplinekanlayer_kernel(tc, x, base_weight, spline_weight, spline_scaler
         def finish_coefficients():
             for q in (4, 0, 3, 1, 2):
                 tt(mag[:, :, q, :], mag[:, :, q, :], dif[4][:, :, 4 - q:8 - q], ALU.mult)
-            nc.vector.tensor_scalar_mul(out=neg_mag4[:], in0=mag[:, :, 4, :], scalar1=-1.0)
+            nc.gpsimd.tensor_scalar(out=neg_mag4[:], in0=mag[:, :, 4, :], scalar1=-1.0, scalar2=0.0, op0=ALU.mult, op1=ALU.add)
             nc.vector.reciprocal(out=inv[:, :, 0, :], in_=mag[:, :, 4, :])
             nc.vector.reciprocal(out=inv[:, :, 1, :], in_=mag[:, :, 0, :])
+            nc.gpsimd.tensor_scalar(out=neg_inv[:], in0=inv[:], scalar1=-1.0, scalar2=0.0, op0=ALU.mult, op1=ALU.add)
             for q in (3, 1, 2):
                 for side, factor in ((0, of_hi[q]), (1, of_lo[q])):
-                    nc.vector.scalar_tensor_tensor(out=factor[:], in0=mag[:, :, q, :], scalar=(1.0 if q == 2 else -1.0), in1=inv[:, :, side, :], op0=ALU.mult, op1=ALU.mult)
+                    tt(factor[:], mag[:, :, q, :], (inv if q == 2 else neg_inv)[:, :, side, :], ALU.mult)
 
         xT = keep.tile([P, NIT, B], BF16)
         a_codes = keep.tile([P, 2, B], U32, align_bytes=64)
@@ -263,8 +265,8 @@ def tile_bsplinekanlayer_kernel(tc, x, base_weight, spline_weight, spline_scaler
             if it in EARLY:
                 order.append((it, HB, HB))
         first_round = len(order)
-        on_tensor_n3 = set(range(first_round))
-        on_tensor_n4 = set(range(first_round))
+        on_tensor_n3 = set(range(first_round + 2))
+        on_tensor_n4 = set(range(first_round + 1))
         order.extend([(it, HB, HB) for it in range(NIT - 1) if it not in EARLY])
         order.extend([(NIT - 1, HB, P), (NIT - 1, HB + P, P)])
         cube = {}
@@ -378,14 +380,20 @@ def tile_bsplinekanlayer_kernel(tc, x, base_weight, spline_weight, spline_scaler
                 grouped[n] = bgp.tile([P, 2, w, 4], BF16, name="bg%d" % n, tag="bg", align_bytes=64)
             nc.scalar.copy(out=grouped[n][:, jh, :, :].rearrange("p (c i) t -> p c t i", i=4), in_=planes[n][:, 4 * jh:4 * jh + 4, :].rearrange("p t (c i) -> p c t i", i=4))
 
-        def base_function_quant(n):
+        def base_function_quant(n, sides):
             it, c0, w = order[n]
-            pool, tag = (keep, "bc%d" % n) if n < first_round else (bs0p, "late")
-            codes = pool.tile([P, 2, w], U32, name="bc%d" % n, tag=tag, align_bytes=64)
-            scales = pool.tile([P, 2, w], U8, name="bs%d" % n, tag=tag + "s", align_bytes=64)
-            nc.vector.quantize_mx(out=codes[:].rearrange("p j b -> p (j b)").bitcast(FP8X4), scales=scales[:].rearrange("p j b -> p (j b)"), in_=grouped[n][:].rearrange("p j b t -> p (j b t)"))
-            for b2 in range(c0 // P, (c0 + w) // P):
-                coded[it, b2] = (codes, scales, b2 * P - c0)
+            if 0 in sides:
+                pool, tag = (keep, "bc%d" % n) if n < first_round else (bs0p, "late")
+                codes = pool.tile([P, 2, w], U32, name="bc%d" % n, tag=tag, align_bytes=64)
+                scales = pool.tile([P, 2, w], U8, name="bs%d" % n, tag=tag + "s", align_bytes=64)
+                for b2 in range(c0 // P, (c0 + w) // P):
+                    coded[it, b2] = (codes, scales, b2 * P - c0)
+            codes, scales, start = coded[it, c0 // P]
+            nc.vector.quantize_mx(
+                out=codes[:, sides[0]:sides[-1] + 1, :].rearrange("p j b -> p (j b)").bitcast(FP8X4),
+                scales=scales[:, sides[0]:sides[-1] + 1, :].rearrange("p j b -> p (j b)"),
+                in_=grouped[n][:, sides[0]:sides[-1] + 1, :, :].rearrange("p j b t -> p (j b t)"),
+            )
 
         def slot(n):
             sca = []
@@ -408,39 +416,41 @@ def tile_bsplinekanlayer_kernel(tc, x, base_weight, spline_weight, spline_scaler
             vec = combine(n) if 0 <= n < len(order) else []
             if 0 <= n + 2 < len(order):
                 vec = weave(vec, [lambda r=r: make_cube(n + 2, r) for r in range(4, 8)])
+            if n == len(order):
+                return [sca[0], lambda: base_function_quant(n - 1, (0,)), sca[1], lambda: base_function_quant(n - 1, (1,))]
             merged = weave(sca, vec)
             if n - 1 >= 0:
-                merged.append(lambda: base_function_quant(n - 1))
+                merged.append(lambda: base_function_quant(n - 1, (0, 1)))
             return merged
 
         acc = {}
 
         def base_pass(b2, start):
-            for h in range(2):
-                for g in range(2):
-                    nc.tensor.matmul_mx(
-                        out=acc[b2, h][:],
-                        lhsT=a_codes[:, g, b2 * P:(b2 + 1) * P].bitcast(FP8X4),
-                        lhsT_scale=a_scales[:, g, b2 * P:(b2 + 1) * P],
-                        rhs=bw_codes[:, g, h, :].bitcast(FP8X4),
-                        rhs_scale=bw_scales[:, g, h, :],
-                        start=(start and g == 0),
-                        stop=False,
-                    )
+            def call(h, g):
+                nc.tensor.matmul_mx(
+                    out=acc[b2, h][:],
+                    lhsT=a_codes[:, g, b2 * P:(b2 + 1) * P].bitcast(FP8X4),
+                    lhsT_scale=a_scales[:, g, b2 * P:(b2 + 1) * P],
+                    rhs=bw_codes[:, g, h, :].bitcast(FP8X4),
+                    rhs_scale=bw_scales[:, g, h, :],
+                    start=(start and g == 0),
+                    stop=False,
+                )
+            return [lambda h=h, g=g: call(h, g) for h in range(2) for g in range(2)]
 
         def spline_pass(b2, it, start, stop):
-            codes, scales, c0 = coded[it, b2]
-            for h in range(2):
-                for jh in range(2):
-                    nc.tensor.matmul_mx(
-                        out=acc[b2, h][:],
-                        lhsT=codes[:, jh, c0:c0 + P].bitcast(FP8X4),
-                        lhsT_scale=scales[:, jh, c0:c0 + P],
-                        rhs=w_codes[it][:, jh, h, :].bitcast(FP8X4),
-                        rhs_scale=w_scales[it][4 * (2 * h + jh):P, :],
-                        start=(start and jh == 0),
-                        stop=(stop and jh == 1),
-                    )
+            def call(h, jh):
+                codes, scales, c0 = coded[it, b2]
+                nc.tensor.matmul_mx(
+                    out=acc[b2, h][:],
+                    lhsT=codes[:, jh, c0:c0 + P].bitcast(FP8X4),
+                    lhsT_scale=scales[:, jh, c0:c0 + P],
+                    rhs=w_codes[it][:, jh, h, :].bitcast(FP8X4),
+                    rhs_scale=w_scales[it][4 * (2 * h + jh):P, :],
+                    start=(start and jh == 0),
+                    stop=(stop and jh == 1),
+                )
+            return [lambda h=h, jh=jh: call(h, jh) for jh in range(2) for h in range(2)]
 
         def open_rows(b2):
             pool, tag = (accp, "acc") if b2 < 2 else (trp, "tr")
@@ -449,12 +459,15 @@ def tile_bsplinekanlayer_kernel(tc, x, base_weight, spline_weight, spline_scaler
 
         def close_rows(b2):
             for h in range(2):
-                o_sb = stage.tile([P, OH], F32, name="o_sb", tag="in2k")
-                if b2 == 3 and h == 1:
-                    nc.vector.tensor_copy(out=o_sb[:], in_=acc[b2, h][:])
-                else:
-                    nc.scalar.copy(out=o_sb[:], in_=acc[b2, h][:])
-                nc.sync.dma_start(out=out[b2 * P:(b2 + 1) * P, h * OH:(h + 1) * OH], in_=o_sb[:])
+                for c in range(0, OH, OH if b2 < 3 else OH // 2):
+                    w = OH if b2 < 3 else OH // 2
+                    pool, tag = (stage, "in2k") if b2 < 3 else (rawp, "raw")
+                    o_sb = pool.tile([P, w], F32, name="o_sb", tag=tag)
+                    if b2 == 3 and h == 1:
+                        nc.vector.tensor_copy(out=o_sb[:], in_=acc[b2, h][:, c:c + w])
+                    else:
+                        nc.scalar.copy(out=o_sb[:], in_=acc[b2, h][:, c:c + w])
+                    nc.sync.dma_start(out=out[b2 * P:(b2 + 1) * P, h * OH + c:h * OH + c + w], in_=o_sb[:])
 
         quantised = set()
         base_ready = set()
@@ -466,7 +479,8 @@ def tile_bsplinekanlayer_kernel(tc, x, base_weight, spline_weight, spline_scaler
                 it, b2 = todo[0]
                 if (it, b2) in coded and 4 * it + 3 in quantised:
                     todo.pop(0)
-                    spline_pass(b2, it, it == 0, False)
+                    for call in spline_pass(b2, it, it == 0, False):
+                        call()
 
         def bank_step(k):
             it = k // 8
@@ -549,26 +563,33 @@ def tile_bsplinekanlayer_kernel(tc, x, base_weight, spline_weight, spline_scaler
         for call in body[:begin] + weave(body[begin:end], side) + body[end:]:
             call()
 
-        ready = [lambda: base_pass(0, False)]
-        ready.extend([lambda it=it, b2=b2: spline_pass(b2, it, False, it == NIT - 1) for it, b2 in todo])
+        ready = base_pass(0, False)
+        for b2 in range(2, 4):
+            ready.append(lambda b2=b2: open_rows(b2))
+            ready.extend(base_pass(b2, True))
+            for it in EARLY:
+                if it != UNIT_ORDER[-1]:
+                    ready.extend(spline_pass(b2, it, False, False))
+        for it, b2 in todo:
+            ready.extend(spline_pass(b2, it, False, it == NIT - 1))
         ready.append(lambda: close_rows(0))
-        ready.append(lambda: (open_rows(1), base_pass(1, True)))
-        ready.extend([lambda it=it: spline_pass(1, it, False, it == NIT - 1) for it in range(NIT)])
+        ready.append(lambda: open_rows(1))
+        ready.extend(base_pass(1, True))
+        for it in range(NIT):
+            ready.extend(spline_pass(1, it, False, it == NIT - 1))
         ready.append(lambda: close_rows(1))
-        ready.extend([lambda b2=b2: (open_rows(b2), base_pass(b2, True)) for b2 in range(2, 4)])
-        ready.extend([lambda it=it, b2=b2: spline_pass(b2, it, False, False) for it in EARLY for b2 in range(2, 4)])
-        behind = len(ready)
-        share = SHARE
+        if UNIT_ORDER[-1] in EARLY:
+            for b2 in range(2, 4):
+                ready.extend(spline_pass(b2, UNIT_ORDER[-1], False, False))
         for n in range(first_round, len(order) + 1):
-            calls = slot(n)
-            now = ready[:share]
-            ready = ready[share:]
-            for call in weave(calls, now):
+            now = ready[:SHARE]
+            ready = ready[SHARE:]
+            for call in weave(slot(n), now):
                 call()
             if n > first_round:
                 it, c0, w = order[n - 1]
                 for b2 in range(c0 // P, (c0 + w) // P):
-                    ready.append(lambda it=it, b2=b2: spline_pass(b2, it, False, it == NIT - 1))
+                    ready.extend(spline_pass(b2, it, False, it == NIT - 1))
                     if it == NIT - 1:
                         ready.append(lambda b2=b2: close_rows(b2))
         for call in ready:

@@ -63,6 +63,7 @@ def tile_bsplinekanlayer_kernel(tc, x, base_weight, spline_weight, spline_scaler
         cubep = ctx.enter_context(tc.tile_pool(name="cubep", bufs=4))
         hip = ctx.enter_context(tc.tile_pool(name="hip", bufs=2))
         diagp = ctx.enter_context(tc.tile_pool(name="diagp", bufs=2))
+        gpp = ctx.enter_context(tc.tile_pool(name="gpp", bufs=2))
         planep = ctx.enter_context(tc.tile_pool(name="planep", bufs=3))
         bgp = ctx.enter_context(tc.tile_pool(name="bgp", bufs=2))
         ctx.enter_context(tc.manual_schedule())
@@ -337,6 +338,15 @@ def tile_bsplinekanlayer_kernel(tc, x, base_weight, spline_weight, spline_scaler
             last = 2 if n in on_tensor_n4 else 1
             nc.vector.tensor_tensor(out=planes[n][:, 3:3 + last, :], in0=sums[n][:, 0:last, :], in1=ends[n][:, 0:last, :], op=ALU.add)
 
+        on_gpsimd = set(range(first_round))
+
+        def gpsimd_add(n, side):
+            it, c0, w = order[n]
+            kind, factor, j, r, lead = (hi, of_hi[3], 1, 4, 5) if side == 0 else (lo, of_lo[1], 6, 7, 6)
+            t = gpp.tile([P, w], F32, name="gp%d_%d" % (n, side), tag="gp")
+            nc.gpsimd.tensor_scalar(out=t[:], in0=kind[n, r], scalar1=factor[:, it, r - 4:r - 3], scalar2=0.0, op0=ALU.mult, op1=ALU.add)
+            nc.gpsimd.tensor_tensor(out=planes[n][:, j, :], in0=t[:], in1=kind[n, lead], op=ALU.add)
+
         def combine(n):
             it = order[n][0]
             calls = []
@@ -364,8 +374,9 @@ def tile_bsplinekanlayer_kernel(tc, x, base_weight, spline_weight, spline_scaler
                 add(1, 4, False, 6, None)
             add(0, 2, False, 4, None)
             add(1, 5, False, 7, None)
-            add(0, 1, True, 4, 5)
-            add(1, 6, True, 7, 6)
+            if n not in on_gpsimd:
+                add(0, 1, True, 4, 5)
+                add(1, 6, True, 7, 6)
             if not on_tensor:
                 add(0, 3, False, 4, None)
             if not n4_on_tensor:
@@ -414,6 +425,8 @@ def tile_bsplinekanlayer_kernel(tc, x, base_weight, spline_weight, spline_scaler
             if n + 1 in on_tensor_n3:
                 sca.insert(min(6, len(sca)), lambda: sum_n3(n + 1))
             vec = combine(n) if 0 <= n < len(order) else []
+            if n in on_gpsimd:
+                vec = [lambda: (gpsimd_add(n, 0), gpsimd_add(n, 1))] + vec
             if 0 <= n + 2 < len(order):
                 vec = weave(vec, [lambda r=r: make_cube(n + 2, r) for r in range(4, 8)])
             if n == len(order):

@@ -21,6 +21,8 @@ NIT = IN // P
 OH = 512
 HB = 256
 AHEAD = 2
+FIN = 2
+ROOTED = 4
 SHARE = 20
 EARLY = (0,)
 UNIT_ORDER = (0, 1, 2, 3, 4, 5, 7, 6)
@@ -107,7 +109,7 @@ def tile_bsplinekanlayer_kernel(tc, x, base_weight, spline_weight, spline_scaler
 
         warm = const.tile([P, 2], F32)
         nc.vector.memset(warm[:, 0:1], 0.0)
-        nc.scalar.activation(out=warm[:, 1:2], in_=warm[:, 0:1], func=AF.Silu)
+        nc.scalar.activation(out=warm[:, 1:2], in_=warm[:, 0:1], func=AF.Sqrt)
         ident_bf = const.tile([P, P], BF16)
         make_identity(nc, ident_bf[:])
         ident_f = const.tile([P, P], F32)
@@ -148,6 +150,26 @@ def tile_bsplinekanlayer_kernel(tc, x, base_weight, spline_weight, spline_scaler
         for q in (3, 1, 2):
             of_hi[q] = const.tile([P, NIT, 4], F32, name="ofhi%d" % q)
             of_lo[q] = const.tile([P, NIT, 4], F32, name="oflo%d" % q)
+
+        root = const.tile([P, NIT, 2], F32)
+        root_bias = const.tile([P, NIT, 2], F32)
+        root_scale = const.tile([P, NIT, 2], F32)
+        newton = const.tile([P, NIT, 2], F32)
+
+        def start_roots():
+            nc.scalar.activation(out=root[:, :, 0:1], in_=mag[:, :, 0, 0:1], func=AF.Sqrt)
+            nc.scalar.activation(out=root[:, :, 1:2], in_=mag[:, :, 4, 3:4], func=AF.Sqrt)
+            tt(root_scale[:, :, 0:1], neg_mag4[:, :, 0:1], inv[:, :, 1, 0:1], ALU.mult)
+            tt(root_scale[:, :, 1:2], mag[:, :, 0, 3:4], inv[:, :, 0, 3:4], ALU.mult)
+
+        def finish_roots():
+            nc.vector.reciprocal(out=newton[:], in_=root[:])
+            tt(newton[:, :, 0:1], newton[:, :, 0:1], mag[:, :, 0, 0:1], ALU.mult)
+            tt(newton[:, :, 1:2], newton[:, :, 1:2], mag[:, :, 4, 3:4], ALU.mult)
+            tt(root[:], root[:], newton[:], ALU.add)
+            nc.gpsimd.tensor_scalar(out=root[:], in0=root[:], scalar1=0.5, scalar2=0.0, op0=ALU.mult, op1=ALU.add)
+            tt(root_bias[:, :, 0:1], root[:, :, 0:1], neg_knot[:, :, 4:5], ALU.mult)
+            tt(root_bias[:, :, 1:2], root[:, :, 1:2], neg_knot[:, :, 7:8], ALU.mult)
 
         def invert_differences():
             nc.vector.reciprocal(out=mag[:], in_=mag[:])
@@ -274,17 +296,17 @@ def tile_bsplinekanlayer_kernel(tc, x, base_weight, spline_weight, spline_scaler
         hi = {}
         lo = {}
         planes = {}
-        ends = {}
         grouped = {}
         coded = {}
-
-        def fma(o, a, s, b_):
-            nc.vector.scalar_tensor_tensor(out=o, in0=a, scalar=s, in1=b_, op0=ALU.mult, op1=ALU.add)
 
         def square(n, r):
             it, c0, w = order[n]
             cube[n, r] = cubep.tile([P, w], F32, name="cube%d_%d" % (n, r), tag="cube%d" % r)
-            nc.scalar.activation(out=cube[n, r][:], in_=xT[:, it, c0:c0 + w], func=AF.Square, bias=neg_knot[:, it, r:r + 1], scale=1.0)
+            if n >= ROOTED and r in (4, 7):
+                e = (r - 4) // 3
+                nc.scalar.activation(out=cube[n, r][:], in_=xT[:, it, c0:c0 + w], func=AF.Square, bias=root_bias[:, it, e:e + 1], scale=root[:, it, e:e + 1])
+            else:
+                nc.scalar.activation(out=cube[n, r][:], in_=xT[:, it, c0:c0 + w], func=AF.Square, bias=neg_knot[:, it, r:r + 1], scale=1.0)
 
         def make_cube(n, r):
             it, c0, w = order[n]
@@ -292,26 +314,32 @@ def tile_bsplinekanlayer_kernel(tc, x, base_weight, spline_weight, spline_scaler
 
         def clip_hi(n, r):
             it, c0, w = order[n]
+            scale = neg_mag4[:, it, r - 4:r - 3]
             if r == 4:
                 planes[n] = planep.tile([P, NB, w], F32, name="planes%d" % n, tag="planes")
-                ends[n] = hip.tile([P, 2, w], F32, name="ends%d" % n, tag="ends")
                 hi[n, r] = planes[n][:, 0, :]
-            elif r == 7:
-                hi[n, r] = ends[n][:, 0, :]
+                if n >= ROOTED:
+                    scale = root_scale[:, it, 0:1]
             else:
                 t = hip.tile([P, w], F32, name="hi%d_%d" % (n, r), tag="hi%d" % r)
                 hi[n, r] = t[:]
-            nc.scalar.activation(out=hi[n, r], in_=cube[n, r][:], func=AF.Relu, scale=neg_mag4[:, it, r - 4:r - 3])
+            nc.scalar.activation(out=hi[n, r], in_=cube[n, r][:], func=AF.Relu, scale=scale)
 
         def clip_lo(n, r):
             it, c0, w = order[n]
+            scale = mag[:, it, 0, r - 4:r - 3]
             if r == 7:
                 lo[n, r] = planes[n][:, 7, :]
-            elif r == 4:
-                lo[n, r] = ends[n][:, 1, :]
+                if n >= ROOTED:
+                    scale = root_scale[:, it, 1:2]
             else:
                 lo[n, r] = cube[n, r][:]
-            nc.scalar.activation(out=lo[n, r], in_=cube[n, r][:], func=AF.Relu, scale=mag[:, it, 0, r - 4:r - 3])
+            nc.scalar.activation(out=lo[n, r], in_=cube[n, r][:], func=AF.Relu, scale=scale)
+
+        def lead(n, side):
+            if n < ROOTED:
+                return (hi[n, 7] if side == 0 else lo[n, 4]), ALU.add
+            return cube[n, 7 - 3 * side][:], (ALU.subtract if side == 0 else ALU.add)
 
         diag = {}
         sums = {}
@@ -334,18 +362,33 @@ def tile_bsplinekanlayer_kernel(tc, x, base_weight, spline_weight, spline_scaler
             for r in range(7, 4, -1):
                 nc.tensor.matmul(out=sums[n][:, 1, :], lhsT=diag[n, 1, r][:], rhs=lo[n, r], start=(r == 7), stop=(r == 5))
 
-        def finish_sums(n):
-            last = 2 if n in on_tensor_n4 else 1
-            nc.vector.tensor_tensor(out=planes[n][:, 3:3 + last, :], in0=sums[n][:, 0:last, :], in1=ends[n][:, 0:last, :], op=ALU.add)
+        def finish_sum(n, side):
+            plane, op = lead(n, side)
+            nc.vector.tensor_tensor(out=planes[n][:, 3 + side, :], in0=sums[n][:, side, :], in1=plane, op=op)
 
         on_gpsimd = set(range(first_round))
 
-        def gpsimd_add(n, side):
+        n5_on_gpsimd = set(range(2, first_round))
+        n2_on_gpsimd = set(())
+
+        def gpsimd_term(n, side, j, r, other):
             it, c0, w = order[n]
-            kind, factor, j, r, lead = (hi, of_hi[3], 1, 4, 5) if side == 0 else (lo, of_lo[1], 6, 7, 6)
-            t = gpp.tile([P, w], F32, name="gp%d_%d" % (n, side), tag="gp")
-            nc.gpsimd.tensor_scalar(out=t[:], in0=kind[n, r], scalar1=factor[:, it, r - 4:r - 3], scalar2=0.0, op0=ALU.mult, op1=ALU.add)
-            nc.gpsimd.tensor_tensor(out=planes[n][:, j, :], in0=t[:], in1=kind[n, lead], op=ALU.add)
+            kind, factor = (hi, of_hi) if side == 0 else (lo, of_lo)
+            t = gpp.tile([P, w], F32, name="gp%d_%d_%d" % (n, j, r), tag="gp")
+            nc.gpsimd.tensor_scalar(out=t[:], in0=kind[n, r], scalar1=factor[r - j][:, it, r - 4:r - 3], scalar2=0.0, op0=ALU.mult, op1=ALU.add)
+            o = planes[n][:, j, :]
+            nc.gpsimd.tensor_tensor(out=o, in0=t[:], in1=kind[n, other] if other else o, op=ALU.add)
+
+        def gpsimd_terms(n):
+            if n in on_gpsimd:
+                gpsimd_term(n, 0, 1, 4, 5)
+                gpsimd_term(n, 1, 6, 7, 6)
+            if n in n5_on_gpsimd:
+                gpsimd_term(n, 1, 5, 6, 5)
+                gpsimd_term(n, 1, 5, 7, None)
+            if n in n2_on_gpsimd:
+                gpsimd_term(n, 0, 2, 5, 6)
+                gpsimd_term(n, 0, 2, 4, None)
 
         def combine(n):
             it = order[n][0]
@@ -357,7 +400,10 @@ def tile_bsplinekanlayer_kernel(tc, x, base_weight, spline_weight, spline_scaler
                 factor = (of_hi if side == 0 else of_lo)[q]
                 def call():
                     o = planes[n][:, j, :]
-                    fma(o, kind[n, r], factor[:, it, r - 4:r - 3], kind[n, other] if source else o)
+                    third, op = o, ALU.add
+                    if source:
+                        third, op = lead(n, side) if (j, other) in ((3, 7), (4, 4)) else (kind[n, other], ALU.add)
+                    nc.vector.scalar_tensor_tensor(out=o, in0=kind[n, r], scalar=factor[:, it, r - 4:r - 3], in1=third, op0=ALU.mult, op1=op)
                 calls.append(call)
 
             on_tensor = n in on_tensor_n3
@@ -366,14 +412,18 @@ def tile_bsplinekanlayer_kernel(tc, x, base_weight, spline_weight, spline_scaler
                 add(0, 3, True, 6, 7)
             if not n4_on_tensor:
                 add(1, 4, True, 5, 4)
-            add(0, 2, True, 5, 6)
-            add(1, 5, True, 6, 5)
+            if n not in n2_on_gpsimd:
+                add(0, 2, True, 5, 6)
+            if n not in n5_on_gpsimd:
+                add(1, 5, True, 6, 5)
             if not on_tensor:
                 add(0, 3, False, 5, None)
             if not n4_on_tensor:
                 add(1, 4, False, 6, None)
-            add(0, 2, False, 4, None)
-            add(1, 5, False, 7, None)
+            if n not in n2_on_gpsimd:
+                add(0, 2, False, 4, None)
+            if n not in n5_on_gpsimd:
+                add(1, 5, False, 7, None)
             if n not in on_gpsimd:
                 add(0, 1, True, 4, 5)
                 add(1, 6, True, 7, 6)
@@ -382,14 +432,16 @@ def tile_bsplinekanlayer_kernel(tc, x, base_weight, spline_weight, spline_scaler
             if not n4_on_tensor:
                 add(1, 4, False, 7, None)
             if on_tensor:
-                calls.insert(2, lambda: finish_sums(n))
+                calls.insert(FIN, lambda: finish_sum(n, 0))
+            if n4_on_tensor:
+                calls.insert(FIN + 1, lambda: finish_sum(n, 1))
             return calls
 
         def regroup(n, jh):
             w = order[n][2]
             if jh == 0:
                 grouped[n] = bgp.tile([P, 2, w, 4], BF16, name="bg%d" % n, tag="bg", align_bytes=64)
-            nc.scalar.copy(out=grouped[n][:, jh, :, :].rearrange("p (c i) t -> p c t i", i=4), in_=planes[n][:, 4 * jh:4 * jh + 4, :].rearrange("p t (c i) -> p c t i", i=4))
+            nc.scalar.activation(out=grouped[n][:, jh, :, :].rearrange("p (c i) t -> p c t i", i=4), in_=planes[n][:, 4 * jh:4 * jh + 4, :].rearrange("p t (c i) -> p c t i", i=4), func=AF.Relu)
 
         def base_function_quant(n, sides):
             it, c0, w = order[n]
@@ -409,11 +461,11 @@ def tile_bsplinekanlayer_kernel(tc, x, base_weight, spline_weight, spline_scaler
         def slot(n):
             sca = []
             if 0 <= n + 1 < len(order):
-                sca.extend([lambda r=r: clip_hi(n + 1, r) for r in range(4, 8)])
+                sca.extend([lambda r=r: clip_hi(n + 1, r) for r in range(4, 7 if n + 1 >= ROOTED else 8)])
             if n - 1 >= 0:
                 sca.extend([lambda jh=jh: regroup(n - 1, jh) for jh in range(2)])
             if 0 <= n + 1 < len(order):
-                sca.extend([lambda r=r: clip_lo(n + 1, r) for r in range(7, 3, -1)])
+                sca.extend([lambda r=r: clip_lo(n + 1, r) for r in range(7, 4 if n + 1 >= ROOTED else 3, -1)])
             if 0 <= n + 3 < len(order):
                 sca.extend([lambda r=r: square(n + 3, r) for r in range(4, 8)])
             if n + 2 in on_tensor_n3:
@@ -425,8 +477,8 @@ def tile_bsplinekanlayer_kernel(tc, x, base_weight, spline_weight, spline_scaler
             if n + 1 in on_tensor_n3:
                 sca.insert(min(6, len(sca)), lambda: sum_n3(n + 1))
             vec = combine(n) if 0 <= n < len(order) else []
-            if n in on_gpsimd:
-                vec = [lambda: (gpsimd_add(n, 0), gpsimd_add(n, 1))] + vec
+            if 0 <= n < len(order):
+                vec = [lambda: gpsimd_terms(n)] + vec
             if 0 <= n + 2 < len(order):
                 vec = weave(vec, [lambda r=r: make_cube(n + 2, r) for r in range(4, 8)])
             if n == len(order):
@@ -552,6 +604,9 @@ def tile_bsplinekanlayer_kernel(tc, x, base_weight, spline_weight, spline_scaler
                 bases.append(lambda n=n, r=r: make_diag(n, 1, r))
         for n in range(-1, first_round):
             calls = slot(n)
+            if n == ROOTED - 4:
+                calls.insert(0, start_roots)
+                calls.insert(len(calls) // 2, finish_roots)
             if n in (-1, 0, 1):
                 calls.insert(len(calls) // 2, lambda n=n: turn_x(n + 2, trp, "tr"))
                 calls.append(lambda n=n: keep_x(n + 2))

from contextlib import ExitStack

import concourse.mybir as mybir
from concourse.masks import make_identity

F32 = mybir.dt.float32
BF16 = mybir.dt.bfloat16
U32 = mybir.dt.uint32
U8 = mybir.dt.uint8
FP8X4 = mybir.dt.float8_e4m3fn_x4
ALU = mybir.AluOpType
AF = mybir.ActivationFunctionType

P = 128
B = 512
IN = 1024
OUT = 1024
NB = 8
NK = 12
NIT = IN // P
OH = 512
HB = 256
AHEAD = 2
FIN = 2
ROOTED = 4
SHARE = 20
EARLY = (0,)
UNIT_ORDER = (0, 1, 2, 3, 4, 5, 7, 6)
DUPLICATE_ON_TENSOR = range(5)
FLOPS = 2 * B * OUT * (IN + IN * NB)


def weave(*streams):
    total = [len(s) for s in streams]
    done = [0] * len(streams)
    merged = []
    for step in range(sum(total)):
        best = None
        for n in range(len(streams)):
            if done[n] < total[n]:
                due = (done[n] + 0.5) / total[n]
                if best is None or due < best[0]:
                    best = (due, n)
        n = best[1]
        merged.append(streams[n][done[n]])
        done[n] += 1
    return merged


def tile_bsplinekanlayer_kernel(tc, x, base_weight, spline_weight, spline_scaler, grid, out):
    nc = tc.nc
    with ExitStack() as ctx:
        const = ctx.enter_context(tc.tile_pool(name="const", bufs=1))
        stage = ctx.enter_context(tc.tile_pool(name="stage", bufs=4))
        accp = ctx.enter_context(tc.psum_pool(name="accp", bufs=2))
        trp = ctx.enter_context(tc.psum_pool(name="trp", bufs=4))
        sump = ctx.enter_context(tc.psum_pool(name="sump", bufs=2))
        keep = ctx.enter_context(tc.tile_pool(name="keep", bufs=1))
        scp = ctx.enter_context(tc.tile_pool(name="scp", bufs=1))
        rawp = ctx.enter_context(tc.tile_pool(name="rawp", bufs=4))
        sctp = ctx.enter_context(tc.tile_pool(name="sctp", bufs=3))
        grp = ctx.enter_context(tc.tile_pool(name="grp", bufs=2))
        basep = ctx.enter_context(tc.tile_pool(name="basep", bufs=1))
        bs0p = ctx.enter_context(tc.tile_pool(name="bs0p", bufs=2))
        cubep = ctx.enter_context(tc.tile_pool(name="cubep", bufs=4))
        hip = ctx.enter_context(tc.tile_pool(name="hip", bufs=2))
        diagp = ctx.enter_context(tc.tile_pool(name="diagp", bufs=2))
        gpp = ctx.enter_context(tc.tile_pool(name="gpp", bufs=2))
        planep = ctx.enter_context(tc.tile_pool(name="planep", bufs=3))
        bgp = ctx.enter_context(tc.tile_pool(name="bgp", bufs=2))
        ctx.enter_context(tc.manual_schedule())

        x_view = x.rearrange("(t p) i -> p t i", p=P)
        sc_view = spline_scaler.rearrange("(t p) i -> p t i", p=P)
        sw_view = spline_weight.rearrange("(t p) i j -> p t (i j)", p=P)

        x_sb = {}
        sc_sb = {}
        raws = {}
        base_sb = {}

        def load_x(quarter):
            x_sb[quarter] = stage.tile([P, 4, 256], BF16, name="x%d" % quarter, tag="in2k")
            nc.sync.dma_start(out=x_sb[quarter][:], in_=x_view[:, :, quarter * 256:(quarter + 1) * 256])

        def load_scaler(quarter):
            sc_sb[quarter] = scp.tile([P, 8, 256], BF16, name="sc%d" % quarter, tag="sc")
            nc.sync.dma_start(out=sc_sb[quarter][:], in_=sc_view[:, :, quarter * 256:(quarter + 1) * 256])

        def load_raw(n):
            it, t0 = n // 4, 2 * (n % 4)
            raws[n] = rawp.tile([P, 2, P * NB], BF16, name="raw%d" % n, tag="raw")
            nc.sync.dma_start(out=raws[n][:], in_=sw_view[:, t0:t0 + 2, it * P * NB:(it + 1) * P * NB])

        def load_base(n):
            base_sb[n] = stage.tile([P, IN], BF16, name="bw%d" % n, tag="in2k")
            nc.sync.dma_start(out=base_sb[n][:], in_=base_weight[n * P:(n + 1) * P, :])

        grid_sb = const.tile([P, NIT, NK], BF16)
        nc.sync.dma_start(out=grid_sb[:], in_=grid.rearrange("(t p) r -> p t r", p=P))
        load_x(0)
        load_scaler(0)
        load_raw(0)
        load_x(1)
        for n in range(1, 4):
            load_raw(n)
        for quarter in range(2, 4):
            load_x(quarter)

        warm = const.tile([P, 2], F32)
        nc.vector.memset(warm[:, 0:1], 0.0)
        nc.scalar.activation(out=warm[:, 1:2], in_=warm[:, 0:1], func=AF.Sqrt)
        ident_bf = const.tile([P, P], BF16)
        make_identity(nc, ident_bf[:])
        ident_f = const.tile([P, P], F32)
        make_identity(nc, ident_f[:])

        dup = const.tile([P, P, 2], BF16)
        nc.vector.tensor_copy(out=dup[:], in_=ident_bf[:].unsqueeze(2).to_broadcast([P, P, 2]))

        def tt(o, a, b_, op):
            nc.gpsimd.tensor_tensor(out=o, in0=a, in1=b_, op=op)

        knot = const.tile([P, NIT, NK], F32)
        nc.vector.tensor_copy(out=knot[:], in_=grid_sb[:])
        neg_knot = const.tile([P, NIT, NK], F32)
        nc.vector.tensor_scalar_mul(out=neg_knot[:], in0=knot[:], scalar1=-1.0)
        dif = {}
        for d in range(1, 5):
            dif[d] = const.tile([P, NIT, NK], F32, name="dif%d" % d)
            tt(dif[d][:, :, 0:NK - d], knot[:, :, d:NK], knot[:, :, 0:NK - d], ALU.subtract)
        left = {d: dif[d][:, :, 4 - d:8 - d] for d in range(1, 5)}
        right = {d: dif[d][:, :, 4:8] for d in range(1, 5)}
        mag = const.tile([P, NIT, 5, 4], F32)
        part = const.tile([P, NIT, 4, 4], F32)
        tt(part[:, :, 0, :], left[1], left[2], ALU.mult)
        tt(part[:, :, 1, :], right[1], right[2], ALU.mult)
        tt(part[:, :, 2, :], part[:, :, 0, :], left[3], ALU.mult)
        tt(part[:, :, 3, :], part[:, :, 1, :], right[3], ALU.mult)
        tt(mag[:, :, 2, :], part[:, :, 0, :], part[:, :, 1, :], ALU.mult)
        tt(mag[:, :, 4, :], part[:, :, 2, :], left[4], ALU.mult)
        tt(mag[:, :, 0, :], part[:, :, 3, :], right[4], ALU.mult)
        tt(mag[:, :, 1, :], left[1], part[:, :, 3, :], ALU.mult)
        tt(mag[:, :, 3, :], part[:, :, 2, :], right[1], ALU.mult)
        neg_mag4 = const.tile([P, NIT, 4], F32)
        inv = const.tile([P, NIT, 2, 4], F32)
        neg_inv = const.tile([P, NIT, 2, 4], F32)
        of_hi = {}
        of_lo = {}
        for q in (3, 1, 2):
            of_hi[q] = const.tile([P, NIT, 4], F32, name="ofhi%d" % q)
            of_lo[q] = const.tile([P, NIT, 4], F32, name="oflo%d" % q)

        root = const.tile([P, NIT, 2], F32)
        root_bias = const.tile([P, NIT, 2], F32)
        root_scale = const.tile([P, NIT, 2], F32)
        newton = const.tile([P, NIT, 2], F32)

        def start_roots():
            nc.scalar.activation(out=root[:, :, 0:1], in_=mag[:, :, 0, 0:1], func=AF.Sqrt)
            nc.scalar.activation(out=root[:, :, 1:2], in_=mag[:, :, 4, 3:4], func=AF.Sqrt)
            tt(root_scale[:, :, 0:1], neg_mag4[:, :, 0:1], inv[:, :, 1, 0:1], ALU.mult)
            tt(root_scale[:, :, 1:2], mag[:, :, 0, 3:4], inv[:, :, 0, 3:4], ALU.mult)

        def finish_roots():
            nc.vector.reciprocal(out=newton[:], in_=root[:])
            tt(newton[:, :, 0:1], newton[:, :, 0:1], mag[:, :, 0, 0:1], ALU.mult)
            tt(newton[:, :, 1:2], newton[:, :, 1:2], mag[:, :, 4, 3:4], ALU.mult)
            tt(root[:], root[:], newton[:], ALU.add)
            nc.gpsimd.tensor_scalar(out=root[:], in0=root[:], scalar1=0.5, scalar2=0.0, op0=ALU.mult, op1=ALU.add)
            tt(root_bias[:, :, 0:1], root[:, :, 0:1], neg_knot[:, :, 4:5], ALU.mult)
            tt(root_bias[:, :, 1:2], root[:, :, 1:2], neg_knot[:, :, 7:8], ALU.mult)

        def invert_differences():
            nc.vector.reciprocal(out=mag[:], in_=mag[:])

        def finish_coefficients():
            for q in (4, 0, 3, 1, 2):
                tt(mag[:, :, q, :], mag[:, :, q, :], dif[4][:, :, 4 - q:8 - q], ALU.mult)
            nc.gpsimd.tensor_scalar(out=neg_mag4[:], in0=mag[:, :, 4, :], scalar1=-1.0, scalar2=0.0, op0=ALU.mult, op1=ALU.add)
            nc.vector.reciprocal(out=inv[:, :, 0, :], in_=mag[:, :, 4, :])
            nc.vector.reciprocal(out=inv[:, :, 1, :], in_=mag[:, :, 0, :])
            nc.gpsimd.tensor_scalar(out=neg_inv[:], in0=inv[:], scalar1=-1.0, scalar2=0.0, op0=ALU.mult, op1=ALU.add)
            for q in (3, 1, 2):
                for side, factor in ((0, of_hi[q]), (1, of_lo[q])):
                    tt(factor[:], mag[:, :, q, :], (inv if q == 2 else neg_inv)[:, :, side, :], ALU.mult)

        xT = keep.tile([P, NIT, B], BF16)
        a_codes = keep.tile([P, 2, B], U32, align_bytes=64)
        a_scales = keep.tile([P, 2, B], U8, align_bytes=64)
        bw_codes = keep.tile([P, 2, 2, OH], U32, align_bytes=64)
        bw_scales = keep.tile([P, 2, 2, OH], U8, align_bytes=64)
        w_codes = []
        w_scales = []
        for it in range(NIT):
            w_codes.append(keep.tile([P, 2, 2, OH], U32, name="wc%d" % it, align_bytes=64))
            w_scales.append(keep.tile([P, OH], U8, name="ws%d" % it, align_bytes=64))

        x_banks = {}

        def turn_x(quarter, pool, tag):
            ps = pool.tile([P, 2, B], BF16, name="ps_x%d" % quarter, tag=tag)
            for s in range(2):
                for bt in range(4):
                    nc.tensor.transpose(ps[:, s, bt * P:(bt + 1) * P], x_sb[quarter][:, bt, s * P:(s + 1) * P], ident_bf[:])
            x_banks[quarter] = ps

        def keep_x(quarter):
            nc.scalar.copy(out=xT[:, 2 * quarter:2 * quarter + 2, :], in_=x_banks[quarter][:])

        sg = {}
        base_banks = {}

        def silu(g):
            sg[g] = basep.tile([P, B, 4], BF16, name="sg%d" % g, tag="base", align_bytes=64)
            nc.scalar.activation(out=sg[g][:], in_=xT[:, 4 * g:4 * g + 4, :].rearrange("p t b -> p b t"), func=AF.Silu)

        def silu_quant(g):
            nc.vector.quantize_mx(out=a_codes[:, g, :].bitcast(FP8X4), scales=a_scales[:, g, :], in_=sg[g][:].rearrange("p b t -> p (b t)"))

        def base_turn(h, g, half):
            if half == 0:
                sg[h, g] = basep.tile([P, OH, 4], BF16, name="bwg%d%d" % (h, g), tag="base", align_bytes=64)
            ps = trp.tile([P, 4, 2 * P], BF16, name="ps_bw", tag="tr")
            for t in range(4):
                for o2 in range(2):
                    nc.tensor.transpose(ps[:, t, o2 * P:(o2 + 1) * P], base_sb[4 * h + 2 * half + o2][:, (4 * g + t) * P:(4 * g + t + 1) * P], ident_bf[:])
            base_banks[h, g, half] = ps

        def base_copy(h, g, half):
            nc.scalar.copy(out=sg[h, g][:, half * 256:(half + 1) * 256, :], in_=base_banks[h, g, half][:].rearrange("p t o -> p o t"))

        def base_quant(h, g):
            nc.vector.quantize_mx(out=bw_codes[:, g, h, :].bitcast(FP8X4), scales=bw_scales[:, g, h, :], in_=sg[h, g][:].rearrange("p o t -> p (o t)"))

        sct = {}
        sc_banks = {}
        banks = {}
        wgs = {}

        def scaler_tile(it, h):
            cols = slice((it % 2) * P, (it % 2 + 1) * P)
            if it in DUPLICATE_ON_TENSOR:
                ps = trp.tile([P, 4, 2 * P], BF16, name="ps_sc", tag="tr")
                for oo in range(4):
                    nc.tensor.matmul(out=ps[:, oo, :], lhsT=sc_sb[it // 2][:, 4 * h + oo, cols], rhs=dup[:].rearrange("p o e -> p (o e)"), start=True, stop=True)
            else:
                ps = trp.tile([P, 4, P], BF16, name="ps_sc", tag="tr")
                for oo in range(4):
                    nc.tensor.transpose(ps[:, oo, :], sc_sb[it // 2][:, 4 * h + oo, cols], ident_bf[:])
            sc_banks[it, h] = ps

        def scaler_copy(it, h):
            sct[it, h] = sctp.tile([P, OH, 2], BF16, name="sct%d_%d" % (it, h), tag="sct")
            ps = sc_banks[it, h][:].rearrange("p a b -> p (a b)")
            if it in DUPLICATE_ON_TENSOR:
                nc.scalar.copy(out=sct[it, h][:].rearrange("p o e -> p (o e)"), in_=ps)
            else:
                nc.scalar.copy(out=sct[it, h][:], in_=ps.unsqueeze(2).to_broadcast([P, OH, 2]))

        def turn(k):
            it, h, jh, half = k // 8, (k // 4) % 2, (k // 2) % 2, k % 2
            words = raws[4 * it + 2 * h + half][:].bitcast(F32).rearrange("p t (i m) -> p t m i", m=4)
            banks[k] = trp.tile([P, 2, 2 * P], F32, name="ps_w", tag="tr")
            for m0 in range(2):
                for o2 in range(2):
                    nc.tensor.transpose(banks[k][:, m0, o2 * P:(o2 + 1) * P], words[:, o2, 2 * jh + m0, :], ident_f[:])

        def scale_bank(k):
            it, h, half = k // 8, (k // 4) % 2, k % 2
            g = k // 2
            if half == 0:
                wgs[g] = grp.tile([P, OH, 4], BF16, name="wg%d" % g, tag="grp", align_bytes=64)
            nc.vector.tensor_tensor(
                out=wgs[g][:, half * 256:(half + 1) * 256, :].rearrange("p o (m e) -> p o m e", e=2),
                in0=banks[k][:].bitcast(BF16).rearrange("p m (o e) -> p o m e", e=2),
                in1=sct[it, h][:, half * 256:(half + 1) * 256, :].unsqueeze(2).to_broadcast([P, 256, 2, 2]),
                op=ALU.mult,
            )

        def weight_quant(g):
            it, h, jh = g // 4, (g // 2) % 2, g % 2
            nc.vector.quantize_mx(out=w_codes[it][:, jh, h, :].bitcast(FP8X4), scales=w_scales[it][4 * (2 * h + jh):P, :], in_=wgs[g][:].rearrange("p o t -> p (o t)"))

        order = []
        for it in UNIT_ORDER:
            order.append((it, 0, HB))
            if it in EARLY:
                order.append((it, HB, HB))
        first_round = len(order)
        on_tensor_n3 = set(range(first_round + 2))
        on_tensor_n4 = set(range(first_round + 1))
        order.extend([(it, HB, HB) for it in range(NIT - 1) if it not in EARLY])
        order.extend([(NIT - 1, HB, P), (NIT - 1, HB + P, P)])
        cube = {}
        hi = {}
        lo = {}
        planes = {}
        grouped = {}
        coded = {}

        def square(n, r):
            it, c0, w = order[n]
            cube[n, r] = cubep.tile([P, w], F32, name="cube%d_%d" % (n, r), tag="cube%d" % r)
            if n >= ROOTED and r in (4, 7):
                e = (r - 4) // 3
                nc.scalar.activation(out=cube[n, r][:], in_=xT[:, it, c0:c0 + w], func=AF.Square, bias=root_bias[:, it, e:e + 1], scale=root[:, it, e:e + 1])
            else:
                nc.scalar.activation(out=cube[n, r][:], in_=xT[:, it, c0:c0 + w], func=AF.Square, bias=neg_knot[:, it, r:r + 1], scale=1.0)

        def make_cube(n, r):
            it, c0, w = order[n]
            nc.vector.scalar_tensor_tensor(out=cube[n, r][:], in0=xT[:, it, c0:c0 + w], scalar=knot[:, it, r:r + 1], in1=cube[n, r][:], op0=ALU.subtract, op1=ALU.mult)

        def clip_hi(n, r):
            it, c0, w = order[n]
            scale = neg_mag4[:, it, r - 4:r - 3]
            if r == 4:
                planes[n] = planep.tile([P, NB, w], F32, name="planes%d" % n, tag="planes")
                hi[n, r] = planes[n][:, 0, :]
                if n >= ROOTED:
                    scale = root_scale[:, it, 0:1]
            else:
                t = hip.tile([P, w], F32, name="hi%d_%d" % (n, r), tag="hi%d" % r)
                hi[n, r] = t[:]
            nc.scalar.activation(out=hi[n, r], in_=cube[n, r][:], func=AF.Relu, scale=scale)

        def clip_lo(n, r):
            it, c0, w = order[n]
            scale = mag[:, it, 0, r - 4:r - 3]
            if r == 7:
                lo[n, r] = planes[n][:, 7, :]
                if n >= ROOTED:
                    scale = root_scale[:, it, 1:2]
            else:
                lo[n, r] = cube[n, r][:]
            nc.scalar.activation(out=lo[n, r], in_=cube[n, r][:], func=AF.Relu, scale=scale)

        def lead(n, side):
            if n < ROOTED:
                return (hi[n, 7] if side == 0 else lo[n, 4]), ALU.add
            return cube[n, 7 - 3 * side][:], (ALU.subtract if side == 0 else ALU.add)

        diag = {}
        sums = {}

        def make_diag(n, side, r):
            it = order[n][0]
            if n > 0 and (n - 1, side, r) in diag and order[n - 1][0] == it:
                diag[n, side, r] = diag[n - 1, side, r]
                return
            diag[n, side, r] = diagp.tile([P, P], F32, name="diag%d_%d_%d" % (n, side, r), tag="diag%d_%d" % (side, r))
            factor = of_hi[r - 3] if side == 0 else of_lo[r - 4]
            nc.scalar.activation(out=diag[n, side, r][:], in_=ident_f[:], func=AF.Copy, scale=factor[:, it, r - 4:r - 3])

        def sum_n3(n):
            sums[n] = sump.tile([P, 2, order[n][2]], F32, name="sum%d" % n, tag="sum")
            for r in range(4, 7):
                nc.tensor.matmul(out=sums[n][:, 0, :], lhsT=diag[n, 0, r][:], rhs=hi[n, r], start=(r == 4), stop=(r == 6))

        def sum_n4(n):
            for r in range(7, 4, -1):
                nc.tensor.matmul(out=sums[n][:, 1, :], lhsT=diag[n, 1, r][:], rhs=lo[n, r], start=(r == 7), stop=(r == 5))

        def finish_sum(n, side):
            plane, op = lead(n, side)
            nc.vector.tensor_tensor(out=planes[n][:, 3 + side, :], in0=sums[n][:, side, :], in1=plane, op=op)

        on_gpsimd = set(range(first_round))

        n5_on_gpsimd = set(range(2, first_round))
        n2_on_gpsimd = set(())

        def gpsimd_term(n, side, j, r, other):
            it, c0, w = order[n]
            kind, factor = (hi, of_hi) if side == 0 else (lo, of_lo)
            t = gpp.tile([P, w], F32, name="gp%d_%d_%d" % (n, j, r), tag="gp")
            nc.gpsimd.tensor_scalar(out=t[:], in0=kind[n, r], scalar1=factor[r - j][:, it, r - 4:r - 3], scalar2=0.0, op0=ALU.mult, op1=ALU.add)
            o = planes[n][:, j, :]
            nc.gpsimd.tensor_tensor(out=o, in0=t[:], in1=kind[n, other] if other else o, op=ALU.add)

        def gpsimd_terms(n):
            if n in on_gpsimd:
                gpsimd_term(n, 0, 1, 4, 5)
                gpsimd_term(n, 1, 6, 7, 6)
            if n in n5_on_gpsimd:
                gpsimd_term(n, 1, 5, 6, 5)
                gpsimd_term(n, 1, 5, 7, None)
            if n in n2_on_gpsimd:
                gpsimd_term(n, 0, 2, 5, 6)
                gpsimd_term(n, 0, 2, 4, None)

        def combine(n):
            it = order[n][0]
            calls = []

            def add(side, j, source, r, other):
                q = r - j
                kind = hi if side == 0 else lo
                factor = (of_hi if side == 0 else of_lo)[q]
                def call():
                    o = planes[n][:, j, :]
                    third, op = o, ALU.add
                    if source:
                        third, op = lead(n, side) if (j, other) in ((3, 7), (4, 4)) else (kind[n, other], ALU.add)
                    nc.vector.scalar_tensor_tensor(out=o, in0=kind[n, r], scalar=factor[:, it, r - 4:r - 3], in1=third, op0=ALU.mult, op1=op)
                calls.append(call)

            on_tensor = n in on_tensor_n3
            n4_on_tensor = n in on_tensor_n4
            if not on_tensor:
                add(0, 3, True, 6, 7)
            if not n4_on_tensor:
                add(1, 4, True, 5, 4)
            if n not in n2_on_gpsimd:
                add(0, 2, True, 5, 6)
            if n not in n5_on_gpsimd:
                add(1, 5, True, 6, 5)
            if not on_tensor:
                add(0, 3, False, 5, None)
            if not n4_on_tensor:
                add(1, 4, False, 6, None)
            if n not in n2_on_gpsimd:
                add(0, 2, False, 4, None)
            if n not in n5_on_gpsimd:
                add(1, 5, False, 7, None)
            if n not in on_gpsimd:
                add(0, 1, True, 4, 5)
                add(1, 6, True, 7, 6)
            if not on_tensor:
                add(0, 3, False, 4, None)
            if not n4_on_tensor:
                add(1, 4, False, 7, None)
            if on_tensor:
                calls.insert(FIN, lambda: finish_sum(n, 0))
            if n4_on_tensor:
                calls.insert(FIN + 1, lambda: finish_sum(n, 1))
            return calls

        def regroup(n, jh):
            w = order[n][2]
            if jh == 0:
                grouped[n] = bgp.tile([P, 2, w, 4], BF16, name="bg%d" % n, tag="bg", align_bytes=64)
            nc.scalar.activation(out=grouped[n][:, jh, :, :].rearrange("p (c i) t -> p c t i", i=4), in_=planes[n][:, 4 * jh:4 * jh + 4, :].rearrange("p t (c i) -> p c t i", i=4), func=AF.Relu)

        def base_function_quant(n, sides):
            it, c0, w = order[n]
            if 0 in sides:
                pool, tag = (keep, "bc%d" % n) if n < first_round else (bs0p, "late")
                codes = pool.tile([P, 2, w], U32, name="bc%d" % n, tag=tag, align_bytes=64)
                scales = pool.tile([P, 2, w], U8, name="bs%d" % n, tag=tag + "s", align_bytes=64)
                for b2 in range(c0 // P, (c0 + w) // P):
                    coded[it, b2] = (codes, scales, b2 * P - c0)
            codes, scales, start = coded[it, c0 // P]
            nc.vector.quantize_mx(
                out=codes[:, sides[0]:sides[-1] + 1, :].rearrange("p j b -> p (j b)").bitcast(FP8X4),
                scales=scales[:, sides[0]:sides[-1] + 1, :].rearrange("p j b -> p (j b)"),
                in_=grouped[n][:, sides[0]:sides[-1] + 1, :, :].rearrange("p j b t -> p (j b t)"),
            )

        def slot(n):
            sca = []
            if 0 <= n + 1 < len(order):
                sca.extend([lambda r=r: clip_hi(n + 1, r) for r in range(4, 7 if n + 1 >= ROOTED else 8)])
            if n - 1 >= 0:
                sca.extend([lambda jh=jh: regroup(n - 1, jh) for jh in range(2)])
            if 0 <= n + 1 < len(order):
                sca.extend([lambda r=r: clip_lo(n + 1, r) for r in range(7, 4 if n + 1 >= ROOTED else 3, -1)])
            if 0 <= n + 3 < len(order):
                sca.extend([lambda r=r: square(n + 3, r) for r in range(4, 8)])
            if n + 2 in on_tensor_n3:
                sca.extend([lambda r=r: make_diag(n + 2, 0, r) for r in range(4, 7)])
                if n + 2 in on_tensor_n4:
                    sca.extend([lambda r=r: make_diag(n + 2, 1, r) for r in range(5, 8)])
            if n + 1 in on_tensor_n4:
                sca.insert(min(13, len(sca)), lambda: sum_n4(n + 1))
            if n + 1 in on_tensor_n3:
                sca.insert(min(6, len(sca)), lambda: sum_n3(n + 1))
            vec = combine(n) if 0 <= n < len(order) else []
            if 0 <= n < len(order):
                vec = [lambda: gpsimd_terms(n)] + vec
            if 0 <= n + 2 < len(order):
                vec = weave(vec, [lambda r=r: make_cube(n + 2, r) for r in range(4, 8)])
            if n == len(order):
                return [sca[0], lambda: base_function_quant(n - 1, (0,)), sca[1], lambda: base_function_quant(n - 1, (1,))]
            merged = weave(sca, vec)
            if n - 1 >= 0:
                merged.append(lambda: base_function_quant(n - 1, (0, 1)))
            return merged

        acc = {}

        def base_pass(b2, start):
            def call(h, g):
                nc.tensor.matmul_mx(
                    out=acc[b2, h][:],
                    lhsT=a_codes[:, g, b2 * P:(b2 + 1) * P].bitcast(FP8X4),
                    lhsT_scale=a_scales[:, g, b2 * P:(b2 + 1) * P],
                    rhs=bw_codes[:, g, h, :].bitcast(FP8X4),
                    rhs_scale=bw_scales[:, g, h, :],
                    start=(start and g == 0),
                    stop=False,
                )
            return [lambda h=h, g=g: call(h, g) for h in range(2) for g in range(2)]

        def spline_pass(b2, it, start, stop):
            def call(h, jh):
                codes, scales, c0 = coded[it, b2]
                nc.tensor.matmul_mx(
                    out=acc[b2, h][:],
                    lhsT=codes[:, jh, c0:c0 + P].bitcast(FP8X4),
                    lhsT_scale=scales[:, jh, c0:c0 + P],
                    rhs=w_codes[it][:, jh, h, :].bitcast(FP8X4),
                    rhs_scale=w_scales[it][4 * (2 * h + jh):P, :],
                    start=(start and jh == 0),
                    stop=(stop and jh == 1),
                )
            return [lambda h=h, jh=jh: call(h, jh) for jh in range(2) for h in range(2)]

        def open_rows(b2):
            pool, tag = (accp, "acc") if b2 < 2 else (trp, "tr")
            for h in range(2):
                acc[b2, h] = pool.tile([P, OH], F32, name="acc%d_%d" % (b2, h), tag=tag)

        def close_rows(b2):
            for h in range(2):
                for c in range(0, OH, OH if b2 < 3 else OH // 2):
                    w = OH if b2 < 3 else OH // 2
                    pool, tag = (stage, "in2k") if b2 < 3 else (rawp, "raw")
                    o_sb = pool.tile([P, w], F32, name="o_sb", tag=tag)
                    if b2 == 3 and h == 1:
                        nc.vector.tensor_copy(out=o_sb[:], in_=acc[b2, h][:, c:c + w])
                    else:
                        nc.scalar.copy(out=o_sb[:], in_=acc[b2, h][:, c:c + w])
                    nc.sync.dma_start(out=out[b2 * P:(b2 + 1) * P, h * OH + c:h * OH + c + w], in_=o_sb[:])

        quantised = set()
        base_ready = set()
        rows = {0: [], 1: []}
        todo = [(it, 0) for it in range(NIT)]

        def next_pass():
            if todo:
                it, b2 = todo[0]
                if (it, b2) in coded and 4 * it + 3 in quantised:
                    todo.pop(0)
                    for call in spline_pass(b2, it, it == 0, False):
                        call()

        def bank_step(k):
            it = k // 8
            if k % 2 == 1 and k + 7 < 64:
                load_raw((k + 7) // 2)
            if k % 16 == 7 and it // 2 + 1 < 4:
                load_scaler(it // 2 + 1)
            if k % 4 == 2 and it + 1 < NIT:
                scaler_tile(it + 1, (k // 4) % 2)
            if k % 4 == 3 and it + 1 < NIT:
                scaler_copy(it + 1, (k // 4) % 2)
            if k + AHEAD < 64:
                turn(k + AHEAD)
            if k % 2 == 1:
                next_pass()
            scale_bank(k)

        def quant_step(g):
            weight_quant(g)
            quantised.add(g)

        weight_calls = []
        for k in range(64):
            weight_calls.append(lambda k=k: bank_step(k))
            if k % 2 == 0 and k > 0:
                weight_calls.append(lambda k=k: quant_step(k // 2 - 1))
        weight_calls.append(lambda: quant_step(31))

        open_rows(0)
        turn_x(0, trp, "tr")
        keep_x(0)
        for r in range(4, 8):
            square(0, r)
        scaler_tile(0, 0)
        scaler_copy(0, 0)
        for k in range(AHEAD):
            turn(k)
        scaler_tile(0, 1)
        scaler_copy(0, 1)
        for r in range(4, 8):
            make_cube(0, r)
        for r in range(4, 8):
            square(1, r)
        for call in weight_calls[:1]:
            call()
        invert_differences()
        for call in weight_calls[1:4]:
            call()
        finish_coefficients()

        bases = []
        for n in range(2):
            for r in range(4, 7):
                bases.append(lambda n=n, r=r: make_diag(n, 0, r))
            for r in range(5, 8):
                bases.append(lambda n=n, r=r: make_diag(n, 1, r))
        for n in range(-1, first_round):
            calls = slot(n)
            if n == ROOTED - 4:
                calls.insert(0, start_roots)
                calls.insert(len(calls) // 2, finish_roots)
            if n in (-1, 0, 1):
                calls.insert(len(calls) // 2, lambda n=n: turn_x(n + 2, trp, "tr"))
                calls.append(lambda n=n: keep_x(n + 2))
            bases.extend(calls)

        side = []
        for n in range(4):
            side.append(lambda n=n: load_base(n))
        for g in range(2):
            side.append(lambda g=g: silu(g))
            side.append(lambda g=g: silu_quant(g))
        for h in range(2):
            for g in range(2):
                for half in range(2):
                    side.append(lambda h=h, g=g, half=half: base_turn(h, g, half))
                    side.append(lambda h=h, g=g, half=half: base_copy(h, g, half))
                    if h == 0 and g == 1:
                        side.append(lambda half=half: (load_base(4 + 2 * half), load_base(5 + 2 * half)))
                side.append(lambda h=h, g=g: base_quant(h, g))
        body = weave(weight_calls[4:], bases)
        begin, end = len(body) // 5, len(body) - 20
        for call in body[:begin] + weave(body[begin:end], side) + body[end:]:
            call()

        ready = base_pass(0, False)
        for b2 in range(2, 4):
            ready.append(lambda b2=b2: open_rows(b2))
            ready.extend(base_pass(b2, True))
            for it in EARLY:
                if it != UNIT_ORDER[-1]:
                    ready.extend(spline_pass(b2, it, False, False))
        for it, b2 in todo:
            ready.extend(spline_pass(b2, it, False, it == NIT - 1))
        ready.append(lambda: close_rows(0))
        ready.append(lambda: open_rows(1))
        ready.extend(base_pass(1, True))
        for it in range(NIT):
            ready.extend(spline_pass(1, it, False, it == NIT - 1))
        ready.append(lambda: close_rows(1))
        if UNIT_ORDER[-1] in EARLY:
            for b2 in range(2, 4):
                ready.extend(spline_pass(b2, UNIT_ORDER[-1], False, False))
        for n in range(first_round, len(order) + 1):
            now = ready[:SHARE]
            ready = ready[SHARE:]
            for call in weave(slot(n), now):
                call()
            if n > first_round:
                it, c0, w = order[n - 1]
                for b2 in range(c0 // P, (c0 + w) // P):
                    ready.extend(spline_pass(b2, it, False, it == NIT - 1))
                    if it == NIT - 1:
                        ready.append(lambda b2=b2: close_rows(b2))
        for call in ready:
            call()
